import numpy as np
import ml_dtypes


def mxq(x, axis, fmt="e4m3"):
    dtype, down = {"e4m3": (ml_dtypes.float8_e4m3fn, 7), "e5m2": (ml_dtypes.float8_e5m2, 14)}[fmt]
    v = np.moveaxis(np.asarray(x, np.float32).astype(ml_dtypes.bfloat16).astype(np.float64), axis, -1)
    blocks = v.reshape(v.shape[:-1] + (-1, 32))
    amax = np.abs(blocks).max(-1, keepdims=True)
    byte = np.maximum(np.where(amax > 0, np.frexp(amax)[1] - 1 + 127, 0) - down, 1)
    scale = np.exp2(byte - 127.0)
    codes = (blocks / scale).astype(np.float32).astype(dtype).astype(np.float64)
    return np.moveaxis((codes * scale).reshape(v.shape), -1, axis)


WIDE = False


def mx_kscale(k):
    if not WIDE:
        return np.ones(k)
    levels = np.array([10, -10, 5, -5, 0])
    a = np.random.permutation(np.resize(levels, k // 512 * 4)).reshape(k // 512, 4)
    idx = np.arange(k)
    return np.exp2(a[idx // 512, idx % 128 // 32])


BF16 = ml_dtypes.bfloat16


def bf(x):
    return np.asarray(x, np.float32).astype(BF16)


def f64(x):
    return np.asarray(x).astype(np.float64)


B, IN, H = 2048, 512, 512
G = 4 * H
EPS = 1e-5


def _layernorm(v, gamma, beta):
    mean = np.mean(v, axis=-1, keepdims=True)
    var = np.mean(np.square(v - mean), axis=-1, keepdims=True)
    return (v - mean) / np.sqrt(var + EPS) * gamma + beta


def sigmoid(v):
    return 1.0 / (1.0 + np.exp(-v))


def setup_inputs():
    s, t = mx_kscale(IN), mx_kscale(H)
    return {
        "x": bf(np.random.standard_normal((B, IN)) * s),
        "h_prev": bf(np.random.standard_normal((B, H)) * t),
        "c_prev": bf(np.random.standard_normal((B, H))),
        "W_ih": bf(np.random.standard_normal((IN, G)) / np.sqrt(IN) / s[:, None]),
        "W_hh": bf(np.random.standard_normal((H, G)) / np.sqrt(H) / t[:, None]),
        "gamma_ih": bf(1.0 + 0.2 * np.random.standard_normal(G)),
        "beta_ih": bf(0.3 * np.random.standard_normal(G)),
        "gamma_hh": bf(1.0 + 0.2 * np.random.standard_normal(G)),
        "beta_hh": bf(0.3 * np.random.standard_normal(G)),
        "gamma_c": bf(1.0 + 0.2 * np.random.standard_normal(H)),
        "beta_c": bf(0.3 * np.random.standard_normal(H)),
    }


def reference(x, h_prev, c_prev, W_ih, W_hh, gamma_ih, beta_ih, gamma_hh, beta_hh, gamma_c, beta_c):
    a_ih = mxq(f64(x), 1, "e4m3") @ mxq(f64(W_ih), 0, "e4m3")
    a_hh = mxq(f64(h_prev), 1, "e4m3") @ mxq(f64(W_hh), 0, "e4m3")
    gates_ih = _layernorm(a_ih, f64(gamma_ih), f64(beta_ih))
    gates_hh = _layernorm(a_hh, f64(gamma_hh), f64(beta_hh))
    gates = gates_ih + gates_hh
    i_g, f_g, g_g, o_g = np.split(gates, 4, axis=1)
    i_t = sigmoid(i_g)
    f_t = sigmoid(f_g)
    g_t = np.tanh(g_g)
    o_t = sigmoid(o_g)
    c_t = f_t * f64(c_prev) + i_t * g_t
    h_t = o_t * np.tanh(_layernorm(c_t, f64(gamma_c), f64(beta_c)))
    return (h_t, c_t)

@@ -1,0 +1,234 @@
+from contextlib import ExitStack
+
+import concourse.mybir as mybir
+from concourse.masks import make_identity
+
+F32 = mybir.dt.float32
+BF16 = mybir.dt.bfloat16
+U32 = mybir.dt.uint32
+U8 = mybir.dt.uint8
+FP8X4 = mybir.dt.float8_e4m3fn_x4
+ALU = mybir.AluOpType
+ACT = mybir.ActivationFunctionType
+AX = mybir.AxisListType
+
+P = 128
+B = 2048
+K = 512
+H = 512
+G = 2048
+NT = B // P
+GRP = 4
+EPS = 1e-5
+FLOPS = 2 * 2 * B * K * G
+
+
+def tile_layernormlstmcell_kernel(
+    tc, x, h_prev, c_prev, W_ih, W_hh, gamma_ih, beta_ih, gamma_hh, beta_hh, gamma_c, beta_c, out_0, out_1
+):
+    nc = tc.nc
+    x_v = x.rearrange("(p t) k -> p t k", t=NT)
+    h_v = h_prev.rearrange("(p t) k -> p t k", t=NT)
+    c_v = c_prev.rearrange("(p t) k -> p t k", t=NT)
+    ho_v = out_0.rearrange("(p t) k -> p t k", t=NT)
+    co_v = out_1.rearrange("(p t) k -> p t k", t=NT)
+
+    with ExitStack() as ctx:
+        const = ctx.enter_context(tc.tile_pool(name="const", bufs=1))
+        io = ctx.enter_context(tc.tile_pool(name="io", bufs=2))
+        xp = ctx.enter_context(tc.tile_pool(name="xp", bufs=3))
+        ps_xt = ctx.enter_context(tc.psum_pool(name="ps_xt", bufs=1))
+        ps_mean = ctx.enter_context(tc.psum_pool(name="ps_mean", bufs=2))
+        ps_acc = ctx.enter_context(tc.psum_pool(name="ps_acc", bufs=5))
+
+        ident = const.tile([P, P], F32, name="ident")
+        make_identity(nc, ident[:])
+        neghalf = const.tile([P, 2], F32, name="neghalf")
+        nc.gpsimd.memset(neghalf[:], -0.5)
+
+        wc = [const.tile([P, G], U32, name="wc%d" % m, align_bytes=64) for m in range(2)]
+        ws = [const.tile([P, G], U8, name="ws%d" % m, align_bytes=64) for m in range(2)]
+        gam = [const.tile([P, G], BF16, name="gam%d" % m) for m in range(2)]
+        bsum = const.tile([P, G], F32, name="bsum")
+        gamc = const.tile([P, H], BF16, name="gamc")
+        betc = const.tile([P, H], BF16, name="betc")
+
+        groups = {}
+        quant = {}
+
+        def xprep(t):
+            g = t // GRP
+            if t % GRP == 0:
+                xin = io.tile([P, GRP, K], BF16, name="xin")
+                hin = io.tile([P, GRP, K], BF16, name="hin")
+                cin = io.tile([P, GRP, H], BF16, name="cin")
+                nc.sync.dma_start(out=xin[:], in_=x_v[:, g * GRP:(g + 1) * GRP, :])
+                nc.sync.dma_start(out=hin[:], in_=h_v[:, g * GRP:(g + 1) * GRP, :])
+                nc.sync.dma_start(out=cin[:], in_=c_v[:, g * GRP:(g + 1) * GRP, :])
+                groups[g] = (xin, hin, cin)
+            xin, hin, cin = groups[g]
+            xt = ps_xt.tile([P, 4, P], F32, name="xt")
+            for o, src in enumerate((xin, hin)):
+                words = src[:, t % GRP, :].bitcast(F32).rearrange("p (w u) -> p u w", u=2)
+                for u in range(2):
+                    nc.tensor.transpose(xt[:, 2 * o + u, :], words[:, u, :], ident[:])
+            gx = xp.tile([P, 2, P, 2], F32, name="gx", align_bytes=64)
+            nc.scalar.copy(out=gx[:], in_=xt[:].rearrange("p (o u) r -> p o r u", u=2))
+            xc = xp.tile([P, 2 * P], U32, name="xc", align_bytes=64)
+            xs = xp.tile([P, 2 * P], U8, name="xs", align_bytes=64)
+            nc.vector.quantize_mx(
+                out=xc[:].bitcast(FP8X4),
+                scales=xs[:],
+                in_=gx[:].rearrange("p o r u -> p (o r u)").bitcast(BF16),
+            )
+            quant[t] = (xc, xs)
+
+        with tc.tile_pool(name="prep", bufs=1) as prep:
+            raws = []
+            for m, W in enumerate((W_ih, W_hh)):
+                for hf in range(2):
+                    raw = prep.tile([P, 4, 1024], BF16, name="raw", bufs=4)
+                    nc.sync.dma_start(
+                        out=raw[:],
+                        in_=W[:, hf * 1024:(hf + 1) * 1024].rearrange("(p j) c -> p j c", j=4),
+                    )
+                    raws.append((m, hf, raw))
+                if m == 0:
+                    xprep(0)
+            nc.scalar.dma_start(out=gam[0][:], in_=gamma_ih.partition_broadcast(P))
+            nc.scalar.dma_start(out=gam[1][:], in_=gamma_hh.partition_broadcast(P))
+            b1 = prep.tile([P, G], BF16, name="b1")
+            b2 = prep.tile([P, G], BF16, name="b2")
+            nc.scalar.dma_start(out=b1[:], in_=beta_ih.partition_broadcast(P))
+            nc.scalar.dma_start(out=b2[:], in_=beta_hh.partition_broadcast(P))
+            nc.scalar.dma_start(out=gamc[:], in_=gamma_c.partition_broadcast(P))
+            nc.scalar.dma_start(out=betc[:], in_=beta_c.partition_broadcast(P))
+            unit = 0
+            for m, hf, raw in raws:
+                for q in range(2):
+                    grp = prep.tile([P, 512, 4], BF16, name="grp", bufs=3, align_bytes=64)
+                    dst = grp[:].rearrange("p (c i) t -> p c t i", i=4)
+                    src = raw[:, :, q * 512:(q + 1) * 512].rearrange("p t (c i) -> p c t i", i=4)
+                    if unit % 2 == 0:
+                        nc.vector.tensor_copy(out=dst, in_=src)
+                    else:
+                        nc.scalar.copy(out=dst, in_=src)
+                    c0 = hf * 1024 + q * 512
+                    nc.vector.quantize_mx(
+                        out=wc[m][:, c0:c0 + 512].bitcast(FP8X4),
+                        scales=ws[m][:, c0:c0 + 512],
+                        in_=grp[:].rearrange("p c t -> p (c t)"),
+                    )
+                    unit += 1
+            nc.gpsimd.tensor_tensor(out=bsum[:], in0=b1[:], in1=b2[:], op=ALU.add)
+            xprep(1)
+
+        work = ctx.enter_context(tc.tile_pool(name="work", bufs=2))
+        small = ctx.enter_context(tc.tile_pool(name="small", bufs=3))
+
+        for t in range(NT):
+            if t + 2 < NT:
+                xprep(t + 2)
+            xc, xs = quant[t]
+            cin = groups[t // GRP][2]
+
+            mean_ps = ps_mean.tile([P, 2, P], F32, name="mean_ps")
+            for m in range(2):
+                for j in range(G // P):
+                    nc.tensor.matmul_mx(
+                        out=mean_ps[:, m, :],
+                        lhsT=xc[:, m * P:(m + 1) * P].bitcast(FP8X4),
+                        lhsT_scale=xs[:, m * P:(m + 1) * P],
+                        rhs=wc[m][:, j * P:(j + 1) * P].bitcast(FP8X4),
+                        rhs_scale=ws[m][:, j * P:(j + 1) * P],
+                        start=(j == 0),
+                        stop=(j == G // P - 1),
+                    )
+            nm = small.tile([P, 2], F32, name="nm")
+            junk = small.tile([P, P], F32, name="junk")
+            for m in range(2):
+                nc.scalar.activation(
+                    out=junk[:], in_=mean_ps[:, m, :], func=ACT.Identity, scale=-1.0 / G,
+                    accum_out=nm[:, m:m + 1],
+                )
+            ssq = small.tile([P, 8], F32, name="ssq")
+            s = [work.tile([P, G], F32, name="s%d" % m, bufs=3) for m in range(2)]
+            for m in range(2):
+                for j in range(4):
+                    cols = slice(j * 512, (j + 1) * 512)
+                    acc = ps_acc.tile([P, 512], F32, name="acc")
+                    nc.tensor.matmul_mx(
+                        out=acc[:],
+                        lhsT=xc[:, m * P:(m + 1) * P].bitcast(FP8X4),
+                        lhsT_scale=xs[:, m * P:(m + 1) * P],
+                        rhs=wc[m][:, cols].bitcast(FP8X4),
+                        rhs_scale=ws[m][:, cols],
+                        start=True,
+                        stop=True,
+                    )
+                    nc.scalar.activation(
+                        out=s[m][:, cols], in_=acc[:], func=ACT.Square, bias=nm[:, m:m + 1], scale=1.0,
+                        accum_out=ssq[:, 4 * m + j:4 * m + j + 1],
+                    )
+                    nc.vector.scalar_tensor_tensor(
+                        out=s[m][:, cols], in0=acc[:], scalar=nm[:, m:m + 1], in1=gam[m][:, cols],
+                        op0=ALU.add, op1=ALU.mult,
+                    )
+            ssum = small.tile([P, 2], F32, name="ssum")
+            nc.vector.tensor_reduce(
+                out=ssum[:], in_=ssq[:].rearrange("p (m j) -> p m j", m=2), axis=AX.X, op=ALU.add
+            )
+            var = small.tile([P, 2], F32, name="var")
+            nc.gpsimd.tensor_scalar(
+                out=var[:], in0=ssum[:], scalar1=1.0 / G, scalar2=EPS, op0=ALU.mult, op1=ALU.add
+            )
+            r = small.tile([P, 2], F32, name="r")
+            nc.gpsimd.tensor_tensor(out=r[:], in0=var[:], in1=neghalf[:], op=ALU.pow)
+
+            nc.vector.scalar_tensor_tensor(
+                out=s[0][:], in0=s[0][:], scalar=r[:, 0:1], in1=bsum[:], op0=ALU.mult, op1=ALU.add
+            )
+            nc.vector.scalar_tensor_tensor(
+                out=s[1][:], in0=s[1][:], scalar=r[:, 1:2], in1=s[0][:], op0=ALU.mult, op1=ALU.add
+            )
+            ga = work.tile([P, G], F32, name="ga")
+            nc.scalar.activation(out=ga[:, 0:1024], in_=s[1][:, 0:1024], func=ACT.Sigmoid)
+            nc.scalar.activation(out=ga[:, 1024:1536], in_=s[1][:, 1024:1536], func=ACT.Tanh)
+            nc.scalar.activation(out=ga[:, 1536:2048], in_=s[1][:, 1536:2048], func=ACT.Sigmoid)
+
+            fa = work.tile([P, H], F32, name="fa")
+            nc.gpsimd.tensor_tensor(out=fa[:], in0=ga[:, 512:1024], in1=cin[:, t % GRP, :], op=ALU.mult)
+            ig = work.tile([P, H], F32, name="ig")
+            nc.gpsimd.tensor_tensor(out=ig[:], in0=ga[:, 0:512], in1=ga[:, 1024:1536], op=ALU.mult)
+            ct = work.tile([P, H], F32, name="ct")
+            csum = small.tile([P, 1], F32, name="csum")
+            nc.vector.scalar_tensor_tensor(
+                out=ct[:], in0=fa[:], scalar=1.0, in1=ig[:], op0=ALU.mult, op1=ALU.add, accum_out=csum[:]
+            )
+            nc.sync.dma_start(out=co_v[:, t, :], in_=ct[:])
+            nmc = small.tile([P, 1], F32, name="nmc")
+            nc.gpsimd.tensor_scalar(
+                out=nmc[:], in0=csum[:], scalar1=-1.0 / H, scalar2=0.0, op0=ALU.mult, op1=ALU.add
+            )
+            sc = work.tile([P, H], F32, name="sc")
+            ssqc = small.tile([P, 1], F32, name="ssqc")
+            nc.scalar.activation(
+                out=sc[:], in_=ct[:], func=ACT.Square, bias=nmc[:], scale=1.0, accum_out=ssqc[:]
+            )
+            varc = small.tile([P, 1], F32, name="varc")
+            nc.gpsimd.tensor_scalar(
+                out=varc[:], in0=ssqc[:], scalar1=1.0 / H, scalar2=EPS, op0=ALU.mult, op1=ALU.add
+            )
+            rc = small.tile([P, 1], F32, name="rc")
+            nc.gpsimd.tensor_tensor(out=rc[:], in0=varc[:], in1=neghalf[:, 0:1], op=ALU.pow)
+            nc.vector.scalar_tensor_tensor(
+                out=sc[:], in0=ct[:], scalar=nmc[:], in1=gamc[:], op0=ALU.add, op1=ALU.mult
+            )
+            nc.vector.scalar_tensor_tensor(
+                out=sc[:], in0=sc[:], scalar=rc[:], in1=betc[:], op0=ALU.mult, op1=ALU.add
+            )
+            th = work.tile([P, H], F32, name="th")
+            nc.scalar.activation(out=th[:], in_=sc[:], func=ACT.Tanh)
+            ht = work.tile([P, H], F32, name="ht")
+            nc.gpsimd.tensor_tensor(out=ht[:], in0=ga[:, 1536:2048], in1=th[:], op=ALU.mult)
+            nc.sync.dma_start(out=ho_v[:, t, :], in_=ht[:])

@@ -21,6 +21,7 @@ NT = B // P
 GRP = 4
 EPS = 1e-5
 FLOPS = 2 * 2 * B * K * G
+LEAD = 3
 
 
 def tile_layernormlstmcell_kernel(
@@ -36,15 +37,21 @@ def tile_layernormlstmcell_kernel(
     with ExitStack() as ctx:
         const = ctx.enter_context(tc.tile_pool(name="const", bufs=1))
         io = ctx.enter_context(tc.tile_pool(name="io", bufs=2))
-        xp = ctx.enter_context(tc.tile_pool(name="xp", bufs=3))
+        xp = ctx.enter_context(tc.tile_pool(name="xp", bufs=4))
+        prep = ctx.enter_context(tc.tile_pool(name="prep", bufs=1))
+        work = ctx.enter_context(tc.tile_pool(name="work", bufs=2))
+        small = ctx.enter_context(tc.tile_pool(name="small", bufs=4))
         ps_xt = ctx.enter_context(tc.psum_pool(name="ps_xt", bufs=1))
         ps_mean = ctx.enter_context(tc.psum_pool(name="ps_mean", bufs=2))
         ps_acc = ctx.enter_context(tc.psum_pool(name="ps_acc", bufs=5))
+        ctx.enter_context(tc.manual_schedule())
 
         ident = const.tile([P, P], F32, name="ident")
         make_identity(nc, ident[:])
         neghalf = const.tile([P, 2], F32, name="neghalf")
         nc.gpsimd.memset(neghalf[:], -0.5)
+        junkm = const.tile([P, P], F32, name="junkm")
+        junkc = const.tile([P, H], F32, name="junkc")
 
         wc = [const.tile([P, G], U32, name="wc%d" % m, align_bytes=64) for m in range(2)]
         ws = [const.tile([P, G], U8, name="ws%d" % m, align_bytes=64) for m in range(2)]
@@ -53,182 +60,315 @@ def tile_layernormlstmcell_kernel(
         gamc = const.tile([P, H], BF16, name="gamc")
         betc = const.tile([P, H], BF16, name="betc")
 
-        groups = {}
-        quant = {}
+        T = {}
 
-        def xprep(t):
-            g = t // GRP
-            if t % GRP == 0:
-                xin = io.tile([P, GRP, K], BF16, name="xin")
-                hin = io.tile([P, GRP, K], BF16, name="hin")
-                cin = io.tile([P, GRP, H], BF16, name="cin")
-                nc.sync.dma_start(out=xin[:], in_=x_v[:, g * GRP:(g + 1) * GRP, :])
-                nc.sync.dma_start(out=hin[:], in_=h_v[:, g * GRP:(g + 1) * GRP, :])
-                nc.sync.dma_start(out=cin[:], in_=c_v[:, g * GRP:(g + 1) * GRP, :])
-                groups[g] = (xin, hin, cin)
-            xin, hin, cin = groups[g]
+        def ok(t):
+            return 0 <= t < NT
+
+        def load_group(g, which):
+            names = ("xin", "hin", "cin")
+            views = (x_v, h_v, c_v)
+            til = io.tile([P, GRP, K], BF16, name=names[which])
+            nc.sync.dma_start(out=til[:], in_=views[which][:, g * GRP:(g + 1) * GRP, :])
+            T[(names[which], g)] = til
+
+        def pe_xT(t):
             xt = ps_xt.tile([P, 4, P], F32, name="xt")
-            for o, src in enumerate((xin, hin)):
+            for o, nm_ in enumerate(("xin", "hin")):
+                src = T[(nm_, t // GRP)]
                 words = src[:, t % GRP, :].bitcast(F32).rearrange("p (w u) -> p u w", u=2)
                 for u in range(2):
                     nc.tensor.transpose(xt[:, 2 * o + u, :], words[:, u, :], ident[:])
-            gx = xp.tile([P, 2, P, 2], F32, name="gx", align_bytes=64)
-            nc.scalar.copy(out=gx[:], in_=xt[:].rearrange("p (o u) r -> p o r u", u=2))
+            T[("xt", t)] = xt
+
+        def s_xcopy(t):
+            gx = xp.tile([P, 2, P, 2], F32, name="gx", bufs=2, align_bytes=64)
+            nc.scalar.copy(out=gx[:], in_=T[("xt", t)][:].rearrange("p (o u) r -> p o r u", u=2))
+            T[("gx", t)] = gx
+
+        def v_q(t):
             xc = xp.tile([P, 2 * P], U32, name="xc", align_bytes=64)
             xs = xp.tile([P, 2 * P], U8, name="xs", align_bytes=64)
             nc.vector.quantize_mx(
                 out=xc[:].bitcast(FP8X4),
                 scales=xs[:],
-                in_=gx[:].rearrange("p o r u -> p (o r u)").bitcast(BF16),
+                in_=T[("gx", t)][:].rearrange("p o r u -> p (o r u)").bitcast(BF16),
             )
-            quant[t] = (xc, xs)
+            T[("xc", t)] = xc
+            T[("xs", t)] = xs
 
-        with tc.tile_pool(name="prep", bufs=1) as prep:
-            raws = []
-            for m, W in enumerate((W_ih, W_hh)):
-                for hf in range(2):
-                    raw = prep.tile([P, 4, 1024], BF16, name="raw", bufs=4)
-                    nc.sync.dma_start(
-                        out=raw[:],
-                        in_=W[:, hf * 1024:(hf + 1) * 1024].rearrange("(p j) c -> p j c", j=4),
-                    )
-                    raws.append((m, hf, raw))
-                if m == 0:
-                    xprep(0)
-            nc.scalar.dma_start(out=gam[0][:], in_=gamma_ih.partition_broadcast(P))
-            nc.scalar.dma_start(out=gam[1][:], in_=gamma_hh.partition_broadcast(P))
-            b1 = prep.tile([P, G], BF16, name="b1")
-            b2 = prep.tile([P, G], BF16, name="b2")
-            nc.scalar.dma_start(out=b1[:], in_=beta_ih.partition_broadcast(P))
-            nc.scalar.dma_start(out=b2[:], in_=beta_hh.partition_broadcast(P))
-            nc.scalar.dma_start(out=gamc[:], in_=gamma_c.partition_broadcast(P))
-            nc.scalar.dma_start(out=betc[:], in_=beta_c.partition_broadcast(P))
-            unit = 0
-            for m, hf, raw in raws:
-                for q in range(2):
-                    grp = prep.tile([P, 512, 4], BF16, name="grp", bufs=3, align_bytes=64)
-                    dst = grp[:].rearrange("p (c i) t -> p c t i", i=4)
-                    src = raw[:, :, q * 512:(q + 1) * 512].rearrange("p t (c i) -> p c t i", i=4)
-                    if unit % 2 == 0:
-                        nc.vector.tensor_copy(out=dst, in_=src)
-                    else:
-                        nc.scalar.copy(out=dst, in_=src)
-                    c0 = hf * 1024 + q * 512
-                    nc.vector.quantize_mx(
-                        out=wc[m][:, c0:c0 + 512].bitcast(FP8X4),
-                        scales=ws[m][:, c0:c0 + 512],
-                        in_=grp[:].rearrange("p c t -> p (c t)"),
-                    )
-                    unit += 1
-            nc.gpsimd.tensor_tensor(out=bsum[:], in0=b1[:], in1=b2[:], op=ALU.add)
-            xprep(1)
+        def mx(out, t, m, cols, start, stop):
+            nc.tensor.matmul_mx(
+                out=out,
+                lhsT=T[("xc", t)][:, m * P:(m + 1) * P].bitcast(FP8X4),
+                lhsT_scale=T[("xs", t)][:, m * P:(m + 1) * P],
+                rhs=wc[m][:, cols].bitcast(FP8X4),
+                rhs_scale=ws[m][:, cols],
+                start=start,
+                stop=stop,
+            )
 
-        work = ctx.enter_context(tc.tile_pool(name="work", bufs=2))
-        small = ctx.enter_context(tc.tile_pool(name="small", bufs=3))
+        def pe_mean(t, m):
+            if m == 0:
+                T[("mean", t)] = ps_mean.tile([P, 2, P], F32, name="mean_ps")
+            for j in range(G // P):
+                mx(T[("mean", t)][:, m, :], t, m, slice(j * P, (j + 1) * P), j == 0, j == G // P - 1)
 
-        for t in range(NT):
-            if t + 2 < NT:
-                xprep(t + 2)
-            xc, xs = quant[t]
-            cin = groups[t // GRP][2]
+        def s_nm(t, m):
+            if m == 0:
+                T[("nm", t)] = small.tile([P, 2], F32, name="nm")
+            nc.scalar.activation(
+                out=junkm[:], in_=T[("mean", t)][:, m, :], func=ACT.Identity, scale=-1.0 / G,
+                accum_out=T[("nm", t)][:, m:m + 1],
+            )
 
-            mean_ps = ps_mean.tile([P, 2, P], F32, name="mean_ps")
-            for m in range(2):
-                for j in range(G // P):
-                    nc.tensor.matmul_mx(
-                        out=mean_ps[:, m, :],
-                        lhsT=xc[:, m * P:(m + 1) * P].bitcast(FP8X4),
-                        lhsT_scale=xs[:, m * P:(m + 1) * P],
-                        rhs=wc[m][:, j * P:(j + 1) * P].bitcast(FP8X4),
-                        rhs_scale=ws[m][:, j * P:(j + 1) * P],
-                        start=(j == 0),
-                        stop=(j == G // P - 1),
-                    )
-            nm = small.tile([P, 2], F32, name="nm")
-            junk = small.tile([P, P], F32, name="junk")
-            for m in range(2):
-                nc.scalar.activation(
-                    out=junk[:], in_=mean_ps[:, m, :], func=ACT.Identity, scale=-1.0 / G,
-                    accum_out=nm[:, m:m + 1],
-                )
-            ssq = small.tile([P, 8], F32, name="ssq")
-            s = [work.tile([P, G], F32, name="s%d" % m, bufs=3) for m in range(2)]
-            for m in range(2):
-                for j in range(4):
-                    cols = slice(j * 512, (j + 1) * 512)
-                    acc = ps_acc.tile([P, 512], F32, name="acc")
-                    nc.tensor.matmul_mx(
-                        out=acc[:],
-                        lhsT=xc[:, m * P:(m + 1) * P].bitcast(FP8X4),
-                        lhsT_scale=xs[:, m * P:(m + 1) * P],
-                        rhs=wc[m][:, cols].bitcast(FP8X4),
-                        rhs_scale=ws[m][:, cols],
-                        start=True,
-                        stop=True,
-                    )
-                    nc.scalar.activation(
-                        out=s[m][:, cols], in_=acc[:], func=ACT.Square, bias=nm[:, m:m + 1], scale=1.0,
-                        accum_out=ssq[:, 4 * m + j:4 * m + j + 1],
-                    )
-                    nc.vector.scalar_tensor_tensor(
-                        out=s[m][:, cols], in0=acc[:], scalar=nm[:, m:m + 1], in1=gam[m][:, cols],
-                        op0=ALU.add, op1=ALU.mult,
-                    )
+        def pe_main(t, k):
+            acc = ps_acc.tile([P, 512], F32, name="acc")
+            mx(acc[:], t, k // 4, slice((k % 4) * 512, (k % 4 + 1) * 512), True, True)
+            T[("acc", t, k)] = acc
+
+        def s_sq(t, k):
+            m = k // 4
+            cols = slice((k % 4) * 512, (k % 4 + 1) * 512)
+            if k == 0:
+                T[("ssq", t)] = small.tile([P, 8], F32, name="ssq")
+            if k % 4 == 0:
+                T[("s", t, m)] = work.tile([P, G], F32, name="s%d" % m, bufs=3)
+            nc.scalar.activation(
+                out=T[("s", t, m)][:, cols], in_=T[("acc", t, k)][:], func=ACT.Square,
+                bias=T[("nm", t)][:, m:m + 1], scale=1.0, accum_out=T[("ssq", t)][:, k:k + 1],
+            )
+
+        def v_s(t, k):
+            m = k // 4
+            cols = slice((k % 4) * 512, (k % 4 + 1) * 512)
+            nc.vector.scalar_tensor_tensor(
+                out=T[("s", t, m)][:, cols], in0=T[("acc", t, k)][:], scalar=T[("nm", t)][:, m:m + 1],
+                in1=gam[m][:, cols], op0=ALU.add, op1=ALU.mult,
+            )
+
+        def v_red(t):
             ssum = small.tile([P, 2], F32, name="ssum")
             nc.vector.tensor_reduce(
-                out=ssum[:], in_=ssq[:].rearrange("p (m j) -> p m j", m=2), axis=AX.X, op=ALU.add
+                out=ssum[:], in_=T[("ssq", t)][:].rearrange("p (m j) -> p m j", m=2), axis=AX.X, op=ALU.add
             )
+            T[("ssum", t)] = ssum
+
+        def g_r(t):
             var = small.tile([P, 2], F32, name="var")
             nc.gpsimd.tensor_scalar(
-                out=var[:], in0=ssum[:], scalar1=1.0 / G, scalar2=EPS, op0=ALU.mult, op1=ALU.add
+                out=var[:], in0=T[("ssum", t)][:], scalar1=1.0 / G, scalar2=EPS, op0=ALU.mult, op1=ALU.add
             )
             r = small.tile([P, 2], F32, name="r")
             nc.gpsimd.tensor_tensor(out=r[:], in0=var[:], in1=neghalf[:], op=ALU.pow)
+            T[("r", t)] = r
 
+        def v_uw(t, blk):
+            cols = slice(blk * 512, (blk + 1) * 512)
+            s0 = T[("s", t, 0)]
+            s1 = T[("s", t, 1)]
+            r = T[("r", t)]
             nc.vector.scalar_tensor_tensor(
-                out=s[0][:], in0=s[0][:], scalar=r[:, 0:1], in1=bsum[:], op0=ALU.mult, op1=ALU.add
+                out=s0[:, cols], in0=s0[:, cols], scalar=r[:, 0:1], in1=bsum[:, cols], op0=ALU.mult, op1=ALU.add
             )
             nc.vector.scalar_tensor_tensor(
-                out=s[1][:], in0=s[1][:], scalar=r[:, 1:2], in1=s[0][:], op0=ALU.mult, op1=ALU.add
+                out=s1[:, cols], in0=s1[:, cols], scalar=r[:, 1:2], in1=s0[:, cols], op0=ALU.mult, op1=ALU.add
             )
-            ga = work.tile([P, G], F32, name="ga")
-            nc.scalar.activation(out=ga[:, 0:1024], in_=s[1][:, 0:1024], func=ACT.Sigmoid)
-            nc.scalar.activation(out=ga[:, 1024:1536], in_=s[1][:, 1024:1536], func=ACT.Tanh)
-            nc.scalar.activation(out=ga[:, 1536:2048], in_=s[1][:, 1536:2048], func=ACT.Sigmoid)
 
+        def s_act(t, blk):
+            cols = slice(blk * 512, (blk + 1) * 512)
+            gt = work.tile([P, H], F32, name="gate%d" % blk, bufs=(5 if blk == 3 else 2))
+            nc.scalar.activation(
+                out=gt[:], in_=T[("s", t, 1)][:, cols], func=(ACT.Tanh if blk == 2 else ACT.Sigmoid)
+            )
+            T[("gate", t, blk)] = gt
+
+        def g_fa(t):
             fa = work.tile([P, H], F32, name="fa")
-            nc.gpsimd.tensor_tensor(out=fa[:], in0=ga[:, 512:1024], in1=cin[:, t % GRP, :], op=ALU.mult)
+            nc.gpsimd.tensor_tensor(
+                out=fa[:], in0=T[("gate", t, 1)][:], in1=T[("cin", t // GRP)][:, t % GRP, :], op=ALU.mult
+            )
+            T[("fa", t)] = fa
+
+        def g_ig(t):
             ig = work.tile([P, H], F32, name="ig")
-            nc.gpsimd.tensor_tensor(out=ig[:], in0=ga[:, 0:512], in1=ga[:, 1024:1536], op=ALU.mult)
-            ct = work.tile([P, H], F32, name="ct")
+            nc.gpsimd.tensor_tensor(out=ig[:], in0=T[("gate", t, 0)][:], in1=T[("gate", t, 2)][:], op=ALU.mult)
+            T[("ig", t)] = ig
+
+        def v_c(t):
+            ct = work.tile([P, H], F32, name="ct", bufs=3)
             csum = small.tile([P, 1], F32, name="csum")
             nc.vector.scalar_tensor_tensor(
-                out=ct[:], in0=fa[:], scalar=1.0, in1=ig[:], op0=ALU.mult, op1=ALU.add, accum_out=csum[:]
+                out=ct[:], in0=T[("fa", t)][:], scalar=1.0, in1=T[("ig", t)][:], op0=ALU.mult, op1=ALU.add,
+                accum_out=csum[:],
             )
             nc.sync.dma_start(out=co_v[:, t, :], in_=ct[:])
+            T[("ct", t)] = ct
+            T[("csum", t)] = csum
+
+        def s_cstat(t):
             nmc = small.tile([P, 1], F32, name="nmc")
-            nc.gpsimd.tensor_scalar(
-                out=nmc[:], in0=csum[:], scalar1=-1.0 / H, scalar2=0.0, op0=ALU.mult, op1=ALU.add
-            )
-            sc = work.tile([P, H], F32, name="sc")
+            nc.scalar.mul(out=nmc[:], in_=T[("csum", t)][:], mul=-1.0 / H)
             ssqc = small.tile([P, 1], F32, name="ssqc")
             nc.scalar.activation(
-                out=sc[:], in_=ct[:], func=ACT.Square, bias=nmc[:], scale=1.0, accum_out=ssqc[:]
+                out=junkc[:], in_=T[("ct", t)][:], func=ACT.Square, bias=nmc[:], scale=1.0, accum_out=ssqc[:]
             )
+            T[("nmc", t)] = nmc
+            T[("ssqc", t)] = ssqc
+
+        def g_rc(t):
             varc = small.tile([P, 1], F32, name="varc")
             nc.gpsimd.tensor_scalar(
-                out=varc[:], in0=ssqc[:], scalar1=1.0 / H, scalar2=EPS, op0=ALU.mult, op1=ALU.add
+                out=varc[:], in0=T[("ssqc", t)][:], scalar1=1.0 / H, scalar2=EPS, op0=ALU.mult, op1=ALU.add
             )
             rc = small.tile([P, 1], F32, name="rc")
             nc.gpsimd.tensor_tensor(out=rc[:], in0=varc[:], in1=neghalf[:, 0:1], op=ALU.pow)
+            T[("rc", t)] = rc
+
+        def v_lnc(t):
+            sc = work.tile([P, H], F32, name="sc")
             nc.vector.scalar_tensor_tensor(
-                out=sc[:], in0=ct[:], scalar=nmc[:], in1=gamc[:], op0=ALU.add, op1=ALU.mult
+                out=sc[:], in0=T[("ct", t)][:], scalar=T[("nmc", t)][:], in1=gamc[:], op0=ALU.add, op1=ALU.mult
             )
             nc.vector.scalar_tensor_tensor(
-                out=sc[:], in0=sc[:], scalar=rc[:], in1=betc[:], op0=ALU.mult, op1=ALU.add
+                out=sc[:], in0=sc[:], scalar=T[("rc", t)][:], in1=betc[:], op0=ALU.mult, op1=ALU.add
             )
+            T[("sc", t)] = sc
+
+        def s_tanh(t):
             th = work.tile([P, H], F32, name="th")
-            nc.scalar.activation(out=th[:], in_=sc[:], func=ACT.Tanh)
+            nc.scalar.activation(out=th[:], in_=T[("sc", t)][:], func=ACT.Tanh)
+            T[("th", t)] = th
+
+        def g_ht(t):
             ht = work.tile([P, H], F32, name="ht")
-            nc.gpsimd.tensor_tensor(out=ht[:], in0=ga[:, 1536:2048], in1=th[:], op=ALU.mult)
+            nc.gpsimd.tensor_tensor(out=ht[:], in0=T[("gate", t, 3)][:], in1=T[("th", t)][:], op=ALU.mult)
             nc.sync.dma_start(out=ho_v[:, t, :], in_=ht[:])
+
+        raws = []
+        for m, W in enumerate((W_ih, W_hh)):
+            for hf in range(2):
+                raw = prep.tile([P, 4, 1024], BF16, name="raw", bufs=4)
+                nc.sync.dma_start(
+                    out=raw[:], in_=W[:, hf * 1024:(hf + 1) * 1024].rearrange("(p j) c -> p j c", j=4)
+                )
+                raws.append(raw)
+            if m == 0:
+                load_group(0, 0)
+                load_group(0, 1)
+        load_group(0, 2)
+        nc.scalar.dma_start(out=gam[0][:], in_=gamma_ih.partition_broadcast(P))
+        nc.scalar.dma_start(out=gam[1][:], in_=gamma_hh.partition_broadcast(P))
+        b1 = prep.tile([P, G], BF16, name="b1")
+        b2 = prep.tile([P, G], BF16, name="b2")
+        nc.scalar.dma_start(out=b1[:], in_=beta_ih.partition_broadcast(P))
+        nc.scalar.dma_start(out=b2[:], in_=beta_hh.partition_broadcast(P))
+        nc.scalar.dma_start(out=gamc[:], in_=gamma_c.partition_broadcast(P))
+        nc.scalar.dma_start(out=betc[:], in_=beta_c.partition_broadcast(P))
+
+        grps = {}
+
+        def w_copy(u, eng):
+            grp = prep.tile([P, 512, 4], BF16, name="grp", bufs=4, align_bytes=64)
+            dst = grp[:].rearrange("p (c i) t -> p c t i", i=4)
+            src = raws[u // 2][:, :, (u % 2) * 512:(u % 2 + 1) * 512].rearrange("p t (c i) -> p c t i", i=4)
+            if eng == 0:
+                nc.vector.tensor_copy(out=dst, in_=src)
+            else:
+                nc.scalar.copy(out=dst, in_=src)
+            grps[u] = grp
+
+        def w_quant(u):
+            m = u // 4
+            c0 = (u % 4) * 512
+            nc.vector.quantize_mx(
+                out=wc[m][:, c0:c0 + 512].bitcast(FP8X4),
+                scales=ws[m][:, c0:c0 + 512],
+                in_=grps[u][:].rearrange("p c t -> p (c t)"),
+            )
+
+        w_copy(0, 0)
+        w_copy(1, 1)
+        w_copy(2, 0)
+        w_quant(0)
+        w_copy(3, 1)
+        w_quant(1)
+        pe_xT(0)
+        s_xcopy(0)
+        pe_xT(1)
+        w_quant(2)
+        w_copy(4, 0)
+        w_quant(3)
+        v_q(0)
+        w_copy(5, 1)
+        pe_mean(0, 0)
+        for k in range(LEAD):
+            pe_main(0, k)
+        w_copy(6, 0)
+        w_quant(4)
+        w_copy(7, 1)
+        w_quant(5)
+        s_xcopy(1)
+        w_quant(6)
+        s_nm(0, 0)
+        for k in range(LEAD):
+            s_sq(0, k)
+        w_quant(7)
+        v_q(1)
+        pe_mean(0, 1)
+        s_nm(0, 1)
+        nc.gpsimd.tensor_tensor(out=bsum[:], in0=b1[:], in1=b2[:], op=ALU.add)
+
+        for p in range(NT + 5):
+            a, b, c, d, e = p, p - 1, p - 2, p - 3, p - 4
+            if ok(b):
+                g_r(b)
+            if ok(d):
+                g_rc(d)
+            if ok(c):
+                g_fa(c)
+                g_ig(c)
+            if ok(e):
+                g_ht(e)
+            if ok(a + 2):
+                if (a + 2) % GRP == 0:
+                    for which in range(3):
+                        load_group((a + 2) // GRP, which)
+                pe_xT(a + 2)
+            if ok(a):
+                for k in range(8):
+                    if k >= LEAD:
+                        pe_main(a, k)
+                        s_sq(a, k)
+                    v_s(a, k)
+                v_red(a)
+            if ok(a + 1):
+                pe_mean(a + 1, 0)
+                pe_mean(a + 1, 1)
+            if ok(a + 2):
+                s_xcopy(a + 2)
+            if ok(c):
+                s_act(c, 3)
+                v_c(c)
+                s_cstat(c)
+            if ok(d):
+                v_lnc(d)
+                s_tanh(d)
+            if ok(a + 2):
+                v_q(a + 2)
+            for idx, blk in enumerate((1, 0, 2, 3)):
+                if ok(b):
+                    v_uw(b, blk)
+                    if blk != 3:
+                        s_act(b, blk)
+                if ok(a + 1):
+                    if idx == 1:
+                        s_nm(a + 1, 0)
+                        s_nm(a + 1, 1)
+                        pe_main(a + 1, 0)
+                        s_sq(a + 1, 0)
+                    if idx == 2:
+                        pe_main(a + 1, 1)
+                        s_sq(a + 1, 1)
+                        pe_main(a + 1, 2)
+                        s_sq(a + 1, 2)

@@ -21,7 +21,41 @@ NT = B // P
 GRP = 4
 EPS = 1e-5
 FLOPS = 2 * 2 * B * K * G
-LEAD = 3
+GATE = {"i": 0, "f": 1, "g": 2, "o": 3}
+ENGINES = ("PE", "S", "V", "G", "SP")
+ACC_BUFS = 3
+TP_BUFS = 4
+S_BUFS = 3
+
+ORDER = {
+    "PE": (
+        ("main", 0, 1), ("main", 0, 2), ("fwd", -2, "o"), ("mean", 0, 1),
+        ("main", 0, 3), ("main", 0, 4), ("bq", -2, None), ("fwd", -1, "f"),
+        ("bo", -3, None), ("xt", 2, None), ("main", 0, 5), ("main", 0, 6),
+        ("mean", 1, 0), ("main", 0, 7), ("main", 1, 0), ("fwd", -1, "i"),
+        ("fwd", -1, "g"), ("bf", -1, None),
+    ),
+    "S": (
+        ("sq", 0, 1), ("act", -2, "o"), ("sq", 0, 2), ("sq", 0, 3),
+        ("nm", 0, 1), ("sq", 0, 4), ("tanh", -3, None), ("act", -1, "f"),
+        ("sq", 0, 5), ("sq", 0, 6), ("cstat", -2, None), ("sq", 0, 7),
+        ("nm", 1, 0), ("sq", 1, 0), ("act", -1, "i"), ("act", -1, "g"),
+    ),
+    "V": (
+        ("apply", 0, 1), ("LN", -3, None), ("apply", 0, 2), ("red", 0, 0),
+        ("apply", 0, 3), ("xq", 1, None), ("c", -2, None), ("nmc", -2, None),
+        ("apply", 0, 4), ("apply", 0, 5), ("h", -3, None), ("apply", 0, 6),
+        ("red", 0, 1), ("apply", 0, 7), ("xcopy", 2, None), ("apply", 1, 0),
+        ("p", -1, None), ("q", -1, None),
+    ),
+    "G": (
+        ("r", 0, 0), ("rs", 0, 0), ("rc", -2, None), ("r", 0, 1),
+        ("rs", 0, 1),
+    ),
+    "SP": (
+        ("ld", 6, None), ("stc", -2, None), ("sth", -3, None),
+    ),
+}
 
 
 def tile_layernormlstmcell_kernel(
@@ -38,42 +72,85 @@ def tile_layernormlstmcell_kernel(
         const = ctx.enter_context(tc.tile_pool(name="const", bufs=1))
         io = ctx.enter_context(tc.tile_pool(name="io", bufs=2))
         xp = ctx.enter_context(tc.tile_pool(name="xp", bufs=4))
-        prep = ctx.enter_context(tc.tile_pool(name="prep", bufs=1))
+        prep = ctx.enter_context(tc.tile_pool(name="prep", bufs=4))
         work = ctx.enter_context(tc.tile_pool(name="work", bufs=2))
         small = ctx.enter_context(tc.tile_pool(name="small", bufs=4))
-        ps_xt = ctx.enter_context(tc.psum_pool(name="ps_xt", bufs=1))
-        ps_mean = ctx.enter_context(tc.psum_pool(name="ps_mean", bufs=2))
-        ps_acc = ctx.enter_context(tc.psum_pool(name="ps_acc", bufs=5))
+        ps_acc = ctx.enter_context(tc.psum_pool(name="ps_acc", bufs=ACC_BUFS))
+        ps_tp = ctx.enter_context(tc.psum_pool(name="ps_tp", bufs=TP_BUFS))
+        ps_mean = ctx.enter_context(tc.psum_pool(name="ps_mean", bufs=1))
         ctx.enter_context(tc.manual_schedule())
 
         ident = const.tile([P, P], F32, name="ident")
         make_identity(nc, ident[:])
-        neghalf = const.tile([P, 2], F32, name="neghalf")
+        neghalf = const.tile([P, 1], F32, name="neghalf")
         nc.gpsimd.memset(neghalf[:], -0.5)
         junkm = const.tile([P, P], F32, name="junkm")
         junkc = const.tile([P, H], F32, name="junkc")
-
         wc = [const.tile([P, G], U32, name="wc%d" % m, align_bytes=64) for m in range(2)]
         ws = [const.tile([P, G], U8, name="ws%d" % m, align_bytes=64) for m in range(2)]
         gam = [const.tile([P, G], BF16, name="gam%d" % m) for m in range(2)]
-        bsum = const.tile([P, G], F32, name="bsum")
         gamc = const.tile([P, H], BF16, name="gamc")
         betc = const.tile([P, H], BF16, name="betc")
+        cin = const.tile([P, NT, H], BF16, name="cin")
+        bt32 = const.tile([P, P], F32, name="bt32")
+        betaT = const.tile([P, G // P], F32, name="betaT")
 
         T = {}
 
-        def ok(t):
-            return 0 <= t < NT
+        def load_group(g):
+            for nm_, view in (("xin", x_v), ("hin", h_v)):
+                til = io.tile([P, GRP, K], BF16, name=nm_)
+                nc.sync.dma_start(out=til[:], in_=view[:, g * GRP:(g + 1) * GRP, :])
+                T[(nm_, g)] = til
 
-        def load_group(g, which):
-            names = ("xin", "hin", "cin")
-            views = (x_v, h_v, c_v)
-            til = io.tile([P, GRP, K], BF16, name=names[which])
-            nc.sync.dma_start(out=til[:], in_=views[which][:, g * GRP:(g + 1) * GRP, :])
-            T[(names[which], g)] = til
+        load_group(0)
+        raws = []
+        for W in (W_ih, W_hh):
+            for hf in range(2):
+                raw = prep.tile([P, 4, 1024], BF16, name="raw")
+                nc.sync.dma_start(out=raw[:], in_=W[:, hf * 1024:(hf + 1) * 1024].rearrange("(p j) c -> p j c", j=4))
+                raws.append(raw)
+        nc.sync.dma_start(out=cin[:], in_=c_v)
+        load_group(1)
+        ba = prep.tile([16, P], BF16, name="ba", bufs=1)
+        bb = prep.tile([16, P], BF16, name="bb", bufs=1)
+        nc.scalar.dma_start(out=ba[:], in_=beta_ih.rearrange("(r c) -> r c", c=P))
+        nc.scalar.dma_start(out=bb[:], in_=beta_hh.rearrange("(r c) -> r c", c=P))
+        nc.scalar.dma_start(out=gam[0][:], in_=gamma_ih.partition_broadcast(P))
+        nc.scalar.dma_start(out=gam[1][:], in_=gamma_hh.partition_broadcast(P))
+        nc.scalar.dma_start(out=gamc[:], in_=gamma_c.partition_broadcast(P))
+        nc.scalar.dma_start(out=betc[:], in_=beta_c.partition_broadcast(P))
 
-        def pe_xT(t):
-            xt = ps_xt.tile([P, 4, P], F32, name="xt")
+        nc.vector.memset(bt32[:], 0.0)
+        nc.vector.tensor_tensor(out=bt32[0:16, :], in0=ba[:], in1=bb[:], op=ALU.add)
+        tpb = ps_tp.tile([P, 4, P], F32, name="tp")
+        nc.tensor.transpose(tpb[:, 0, :], bt32[:], ident[:])
+        nc.vector.tensor_copy(out=betaT[:], in_=tpb[:, 0, 0:G // P])
+
+        def e_wcopy(eng, u):
+            grp = prep.tile([P, 512, 4], BF16, name="grp", align_bytes=64)
+            dst = grp[:].rearrange("p (c i) t -> p c t i", i=4)
+            src = raws[u // 2][:, :, (u % 2) * 512:(u % 2 + 1) * 512].rearrange("p t (c i) -> p c t i", i=4)
+            if eng == "V":
+                nc.vector.tensor_copy(out=dst, in_=src)
+            else:
+                nc.scalar.copy(out=dst, in_=src)
+            T[("grp", u)] = grp
+
+        def e_wq(eng, u):
+            m = u // 4
+            c0 = (u % 4) * 512
+            nc.vector.quantize_mx(
+                out=wc[m][:, c0:c0 + 512].bitcast(FP8X4),
+                scales=ws[m][:, c0:c0 + 512],
+                in_=T[("grp", u)][:].rearrange("p c t -> p (c t)"),
+            )
+
+        def e_ld(eng, t):
+            load_group(t // GRP)
+
+        def e_xt(eng, t):
+            xt = ps_tp.tile([P, 4, P], F32, name="tp")
             for o, nm_ in enumerate(("xin", "hin")):
                 src = T[(nm_, t // GRP)]
                 words = src[:, t % GRP, :].bitcast(F32).rearrange("p (w u) -> p u w", u=2)
@@ -81,12 +158,16 @@ def tile_layernormlstmcell_kernel(
                     nc.tensor.transpose(xt[:, 2 * o + u, :], words[:, u, :], ident[:])
             T[("xt", t)] = xt
 
-        def s_xcopy(t):
+        def e_xcopy(eng, t):
             gx = xp.tile([P, 2, P, 2], F32, name="gx", bufs=2, align_bytes=64)
-            nc.scalar.copy(out=gx[:], in_=T[("xt", t)][:].rearrange("p (o u) r -> p o r u", u=2))
+            src = T[("xt", t)][:].rearrange("p (o u) r -> p o r u", u=2)
+            if eng == "V":
+                nc.vector.tensor_copy(out=gx[:], in_=src)
+            else:
+                nc.scalar.copy(out=gx[:], in_=src)
             T[("gx", t)] = gx
 
-        def v_q(t):
+        def e_xq(eng, t):
             xc = xp.tile([P, 2 * P], U32, name="xc", align_bytes=64)
             xs = xp.tile([P, 2 * P], U8, name="xs", align_bytes=64)
             nc.vector.quantize_mx(
@@ -108,124 +189,143 @@ def tile_layernormlstmcell_kernel(
                 stop=stop,
             )
 
-        def pe_mean(t, m):
-            if m == 0:
-                T[("mean", t)] = ps_mean.tile([P, 2, P], F32, name="mean_ps")
+        def e_mean(eng, t, m):
+            mp = ps_mean.tile([P, P], F32, name="mean_ps")
             for j in range(G // P):
-                mx(T[("mean", t)][:, m, :], t, m, slice(j * P, (j + 1) * P), j == 0, j == G // P - 1)
+                mx(mp[:], t, m, slice(j * P, (j + 1) * P), j == 0, j == G // P - 1)
+            T[("mean", t, m)] = mp
 
-        def s_nm(t, m):
-            if m == 0:
-                T[("nm", t)] = small.tile([P, 2], F32, name="nm")
+        def e_nm(eng, t, m):
+            nm = small.tile([P, 1], F32, name="nm")
             nc.scalar.activation(
-                out=junkm[:], in_=T[("mean", t)][:, m, :], func=ACT.Identity, scale=-1.0 / G,
-                accum_out=T[("nm", t)][:, m:m + 1],
+                out=junkm[:], in_=T[("mean", t, m)][:], func=ACT.Identity, scale=-1.0 / G, accum_out=nm[:]
             )
+            T[("nm", t, m)] = nm
 
-        def pe_main(t, k):
+        def e_main(eng, t, mk):
+            m, k = mk // 4, mk % 4
             acc = ps_acc.tile([P, 512], F32, name="acc")
-            mx(acc[:], t, k // 4, slice((k % 4) * 512, (k % 4 + 1) * 512), True, True)
-            T[("acc", t, k)] = acc
+            mx(acc[:], t, m, slice(k * 512, (k + 1) * 512), True, True)
+            T[("acc", t, mk)] = acc
 
-        def s_sq(t, k):
-            m = k // 4
-            cols = slice((k % 4) * 512, (k % 4 + 1) * 512)
+        def e_sq(eng, t, mk):
+            m, k = mk // 4, mk % 4
             if k == 0:
-                T[("ssq", t)] = small.tile([P, 8], F32, name="ssq")
-            if k % 4 == 0:
-                T[("s", t, m)] = work.tile([P, G], F32, name="s%d" % m, bufs=3)
+                T[("ssq", t, m)] = small.tile([P, 4], F32, name="ssq")
+                T[("s", t, m)] = work.tile([P, G], F32, name="s%d" % m, bufs=S_BUFS)
             nc.scalar.activation(
-                out=T[("s", t, m)][:, cols], in_=T[("acc", t, k)][:], func=ACT.Square,
-                bias=T[("nm", t)][:, m:m + 1], scale=1.0, accum_out=T[("ssq", t)][:, k:k + 1],
+                out=T[("s", t, m)][:, k * 512:(k + 1) * 512], in_=T[("acc", t, mk)][:], func=ACT.Square,
+                bias=T[("nm", t, m)][:], scale=1.0, accum_out=T[("ssq", t, m)][:, k:k + 1],
             )
 
-        def v_s(t, k):
-            m = k // 4
-            cols = slice((k % 4) * 512, (k % 4 + 1) * 512)
+        def e_apply(eng, t, mk):
+            m, k = mk // 4, mk % 4
+            cols = slice(k * 512, (k + 1) * 512)
             nc.vector.scalar_tensor_tensor(
-                out=T[("s", t, m)][:, cols], in0=T[("acc", t, k)][:], scalar=T[("nm", t)][:, m:m + 1],
+                out=T[("s", t, m)][:, cols], in0=T[("acc", t, mk)][:], scalar=T[("nm", t, m)][:],
                 in1=gam[m][:, cols], op0=ALU.add, op1=ALU.mult,
             )
 
-        def v_red(t):
-            ssum = small.tile([P, 2], F32, name="ssum")
-            nc.vector.tensor_reduce(
-                out=ssum[:], in_=T[("ssq", t)][:].rearrange("p (m j) -> p m j", m=2), axis=AX.X, op=ALU.add
-            )
-            T[("ssum", t)] = ssum
+        def e_red(eng, t, m):
+            ssum = small.tile([P, 1], F32, name="ssum")
+            nc.vector.tensor_reduce(out=ssum[:], in_=T[("ssq", t, m)][:], axis=AX.X, op=ALU.add)
+            T[("ssum", t, m)] = ssum
 
-        def g_r(t):
-            var = small.tile([P, 2], F32, name="var")
-            nc.gpsimd.tensor_scalar(
-                out=var[:], in0=T[("ssum", t)][:], scalar1=1.0 / G, scalar2=EPS, op0=ALU.mult, op1=ALU.add
-            )
-            r = small.tile([P, 2], F32, name="r")
+        def rstd(sumsq, count, nm_):
+            var = small.tile([P, 1], F32, name="var" + nm_)
+            nc.gpsimd.tensor_scalar(out=var[:], in0=sumsq[:], scalar1=1.0 / count, scalar2=EPS, op0=ALU.mult, op1=ALU.add)
+            r = small.tile([P, 1], F32, name="r" + nm_)
             nc.gpsimd.tensor_tensor(out=r[:], in0=var[:], in1=neghalf[:], op=ALU.pow)
-            T[("r", t)] = r
+            return r
 
-        def v_uw(t, blk):
-            cols = slice(blk * 512, (blk + 1) * 512)
-            s0 = T[("s", t, 0)]
-            s1 = T[("s", t, 1)]
-            r = T[("r", t)]
-            nc.vector.scalar_tensor_tensor(
-                out=s0[:, cols], in0=s0[:, cols], scalar=r[:, 0:1], in1=bsum[:, cols], op0=ALU.mult, op1=ALU.add
-            )
-            nc.vector.scalar_tensor_tensor(
-                out=s1[:, cols], in0=s1[:, cols], scalar=r[:, 1:2], in1=s0[:, cols], op0=ALU.mult, op1=ALU.add
-            )
+        def e_r(eng, t, m):
+            T[("r", t, m)] = rstd(T[("ssum", t, m)], G, "g")
 
-        def s_act(t, blk):
-            cols = slice(blk * 512, (blk + 1) * 512)
-            gt = work.tile([P, H], F32, name="gate%d" % blk, bufs=(5 if blk == 3 else 2))
-            nc.scalar.activation(
-                out=gt[:], in_=T[("s", t, 1)][:, cols], func=(ACT.Tanh if blk == 2 else ACT.Sigmoid)
-            )
-            T[("gate", t, blk)] = gt
+        def e_rs(eng, t, m):
+            s = T[("s", t, m)]
+            r = T[("r", t, m)]
+            if eng == "G":
+                nc.gpsimd.tensor_scalar(out=s[:], in0=s[:], scalar1=r[:], scalar2=0.0, op0=ALU.mult, op1=ALU.add)
+            elif eng == "V":
+                nc.vector.tensor_scalar(out=s[:], in0=s[:], scalar1=r[:], scalar2=None, op0=ALU.mult)
+            else:
+                nc.scalar.activation(out=s[:], in_=s[:], func=ACT.Copy, scale=r[:])
 
-        def g_fa(t):
-            fa = work.tile([P, H], F32, name="fa")
-            nc.gpsimd.tensor_tensor(
-                out=fa[:], in0=T[("gate", t, 1)][:], in1=T[("cin", t // GRP)][:, t % GRP, :], op=ALU.mult
-            )
-            T[("fa", t)] = fa
+        def e_fwd(eng, t, j):
+            zt = ps_tp.tile([P, 4, P], F32, name="tp")
+            for q in range(4):
+                cols = slice((GATE[j] * 4 + q) * P, (GATE[j] * 4 + q + 1) * P)
+                for m in range(2):
+                    nc.tensor.matmul(
+                        out=zt[:, q, :], lhsT=T[("s", t, m)][:, cols], rhs=ident[:], is_transpose=True,
+                        start=(m == 0), stop=(m == 1),
+                    )
+            T[("zt", t, j)] = zt
 
-        def g_ig(t):
-            ig = work.tile([P, H], F32, name="ig")
-            nc.gpsimd.tensor_tensor(out=ig[:], in0=T[("gate", t, 0)][:], in1=T[("gate", t, 2)][:], op=ALU.mult)
-            T[("ig", t)] = ig
+        def e_act(eng, t, j):
+            gt = work.tile([P, 4, P], F32, name="gate_" + j, bufs=(3 if j == "o" else 2))
+            for q in range(4):
+                gb = GATE[j] * 4 + q
+                nc.scalar.activation(
+                    out=gt[:, q, :], in_=T[("zt", t, j)][:, q, :], func=(ACT.Tanh if j == "g" else ACT.Sigmoid),
+                    bias=betaT[:, gb:gb + 1], scale=1.0,
+                )
+            T[("gate", t, j)] = gt
 
-        def v_c(t):
+        def back(src):
+            bk = ps_tp.tile([P, 4, P], F32, name="tp")
+            for q in range(4):
+                nc.tensor.transpose(bk[:, q, :], src[:, q, :], ident[:])
+            return bk
+
+        def e_bf(eng, t):
+            T[("bf", t)] = back(T[("gate", t, "f")])
+
+        def e_bq(eng, t):
+            T[("bq", t)] = back(T[("qT", t)])
+
+        def e_bo(eng, t):
+            T[("bo", t)] = back(T[("gate", t, "o")])
+
+        def flat(til):
+            return til[:].rearrange("p q r -> p (q r)")
+
+        def e_q(eng, t):
+            qT = work.tile([P, 4, P], F32, name="qT")
+            nc.vector.tensor_tensor(out=flat(qT), in0=flat(T[("gate", t, "i")]), in1=flat(T[("gate", t, "g")]), op=ALU.mult)
+            T[("qT", t)] = qT
+
+        def e_p(eng, t):
+            pt = work.tile([P, H], F32, name="pt")
+            nc.vector.tensor_tensor(out=pt[:], in0=flat(T[("bf", t)]), in1=cin[:, t, :], op=ALU.mult)
+            T[("pt", t)] = pt
+
+        def e_c(eng, t):
             ct = work.tile([P, H], F32, name="ct", bufs=3)
             csum = small.tile([P, 1], F32, name="csum")
             nc.vector.scalar_tensor_tensor(
-                out=ct[:], in0=T[("fa", t)][:], scalar=1.0, in1=T[("ig", t)][:], op0=ALU.mult, op1=ALU.add,
+                out=ct[:], in0=flat(T[("bq", t)]), scalar=1.0, in1=T[("pt", t)][:], op0=ALU.mult, op1=ALU.add,
                 accum_out=csum[:],
             )
-            nc.sync.dma_start(out=co_v[:, t, :], in_=ct[:])
             T[("ct", t)] = ct
             T[("csum", t)] = csum
 
-        def s_cstat(t):
+        def e_nmc(eng, t):
             nmc = small.tile([P, 1], F32, name="nmc")
-            nc.scalar.mul(out=nmc[:], in_=T[("csum", t)][:], mul=-1.0 / H)
+            nc.vector.tensor_scalar(out=nmc[:], in0=T[("csum", t)][:], scalar1=-1.0 / H, scalar2=None, op0=ALU.mult)
+            T[("nmc", t)] = nmc
+
+        def e_cstat(eng, t):
             ssqc = small.tile([P, 1], F32, name="ssqc")
             nc.scalar.activation(
-                out=junkc[:], in_=T[("ct", t)][:], func=ACT.Square, bias=nmc[:], scale=1.0, accum_out=ssqc[:]
+                out=junkc[:], in_=T[("ct", t)][:], func=ACT.Square, bias=T[("nmc", t)][:], scale=1.0, accum_out=ssqc[:]
             )
-            T[("nmc", t)] = nmc
             T[("ssqc", t)] = ssqc
 
-        def g_rc(t):
-            varc = small.tile([P, 1], F32, name="varc")
-            nc.gpsimd.tensor_scalar(
-                out=varc[:], in0=T[("ssqc", t)][:], scalar1=1.0 / H, scalar2=EPS, op0=ALU.mult, op1=ALU.add
-            )
-            rc = small.tile([P, 1], F32, name="rc")
-            nc.gpsimd.tensor_tensor(out=rc[:], in0=varc[:], in1=neghalf[:, 0:1], op=ALU.pow)
-            T[("rc", t)] = rc
+        def e_rc(eng, t):
+            T[("rc", t)] = rstd(T[("ssqc", t)], H, "c")
 
-        def v_lnc(t):
+        def e_LN(eng, t):
             sc = work.tile([P, H], F32, name="sc")
             nc.vector.scalar_tensor_tensor(
                 out=sc[:], in0=T[("ct", t)][:], scalar=T[("nmc", t)][:], in1=gamc[:], op0=ALU.add, op1=ALU.mult
@@ -235,140 +335,131 @@ def tile_layernormlstmcell_kernel(
             )
             T[("sc", t)] = sc
 
-        def s_tanh(t):
+        def e_tanh(eng, t):
             th = work.tile([P, H], F32, name="th")
             nc.scalar.activation(out=th[:], in_=T[("sc", t)][:], func=ACT.Tanh)
             T[("th", t)] = th
 
-        def g_ht(t):
-            ht = work.tile([P, H], F32, name="ht")
-            nc.gpsimd.tensor_tensor(out=ht[:], in0=T[("gate", t, 3)][:], in1=T[("th", t)][:], op=ALU.mult)
-            nc.sync.dma_start(out=ho_v[:, t, :], in_=ht[:])
+        def e_h(eng, t):
+            ht = work.tile([P, H], F32, name="ht", bufs=3)
+            nc.vector.tensor_tensor(out=ht[:], in0=flat(T[("bo", t)]), in1=T[("th", t)][:], op=ALU.mult)
+            T[("ht", t)] = ht
 
-        raws = []
-        for m, W in enumerate((W_ih, W_hh)):
-            for hf in range(2):
-                raw = prep.tile([P, 4, 1024], BF16, name="raw", bufs=4)
-                nc.sync.dma_start(
-                    out=raw[:], in_=W[:, hf * 1024:(hf + 1) * 1024].rearrange("(p j) c -> p j c", j=4)
-                )
-                raws.append(raw)
-            if m == 0:
-                load_group(0, 0)
-                load_group(0, 1)
-        load_group(0, 2)
-        nc.scalar.dma_start(out=gam[0][:], in_=gamma_ih.partition_broadcast(P))
-        nc.scalar.dma_start(out=gam[1][:], in_=gamma_hh.partition_broadcast(P))
-        b1 = prep.tile([P, G], BF16, name="b1")
-        b2 = prep.tile([P, G], BF16, name="b2")
-        nc.scalar.dma_start(out=b1[:], in_=beta_ih.partition_broadcast(P))
-        nc.scalar.dma_start(out=b2[:], in_=beta_hh.partition_broadcast(P))
-        nc.scalar.dma_start(out=gamc[:], in_=gamma_c.partition_broadcast(P))
-        nc.scalar.dma_start(out=betc[:], in_=beta_c.partition_broadcast(P))
+        def e_stc(eng, t):
+            nc.sync.dma_start(out=co_v[:, t, :], in_=T[("ct", t)][:])
 
-        grps = {}
+        def e_sth(eng, t):
+            nc.sync.dma_start(out=ho_v[:, t, :], in_=T[("ht", t)][:])
 
-        def w_copy(u, eng):
-            grp = prep.tile([P, 512, 4], BF16, name="grp", bufs=4, align_bytes=64)
-            dst = grp[:].rearrange("p (c i) t -> p c t i", i=4)
-            src = raws[u // 2][:, :, (u % 2) * 512:(u % 2 + 1) * 512].rearrange("p t (c i) -> p c t i", i=4)
-            if eng == 0:
-                nc.vector.tensor_copy(out=dst, in_=src)
-            else:
-                nc.scalar.copy(out=dst, in_=src)
-            grps[u] = grp
+        tp_drains = ["pre"]
 
-        def w_quant(u):
-            m = u // 4
-            c0 = (u % 4) * 512
-            nc.vector.quantize_mx(
-                out=wc[m][:, c0:c0 + 512].bitcast(FP8X4),
-                scales=ws[m][:, c0:c0 + 512],
-                in_=grps[u][:].rearrange("p c t -> p (c t)"),
-            )
+        def tp_slot(drain):
+            tp_drains.append(drain)
+            n = len(tp_drains) - 1
+            return tp_drains[n - TP_BUFS] if n >= TP_BUFS else "pre"
 
-        w_copy(0, 0)
-        w_copy(1, 1)
-        w_copy(2, 0)
-        w_quant(0)
-        w_copy(3, 1)
-        w_quant(1)
-        pe_xT(0)
-        s_xcopy(0)
-        pe_xT(1)
-        w_quant(2)
-        w_copy(4, 0)
-        w_quant(3)
-        v_q(0)
-        w_copy(5, 1)
-        pe_mean(0, 0)
-        for k in range(LEAD):
-            pe_main(0, k)
-        w_copy(6, 0)
-        w_quant(4)
-        w_copy(7, 1)
-        w_quant(5)
-        s_xcopy(1)
-        w_quant(6)
-        s_nm(0, 0)
-        for k in range(LEAD):
-            s_sq(0, k)
-        w_quant(7)
-        v_q(1)
-        pe_mean(0, 1)
-        s_nm(0, 1)
-        nc.gpsimd.tensor_tensor(out=bsum[:], in0=b1[:], in1=b2[:], op=ALU.add)
+        def unit(t, mk):
+            return 2 * t + mk // 4, mk % 4
 
-        for p in range(NT + 5):
-            a, b, c, d, e = p, p - 1, p - 2, p - 3, p - 4
-            if ok(b):
-                g_r(b)
-            if ok(d):
-                g_rc(d)
-            if ok(c):
-                g_fa(c)
-                g_ig(c)
-            if ok(e):
-                g_ht(e)
-            if ok(a + 2):
-                if (a + 2) % GRP == 0:
-                    for which in range(3):
-                        load_group((a + 2) // GRP, which)
-                pe_xT(a + 2)
-            if ok(a):
-                for k in range(8):
-                    if k >= LEAD:
-                        pe_main(a, k)
-                        s_sq(a, k)
-                    v_s(a, k)
-                v_red(a)
-            if ok(a + 1):
-                pe_mean(a + 1, 0)
-                pe_mean(a + 1, 1)
-            if ok(a + 2):
-                s_xcopy(a + 2)
-            if ok(c):
-                s_act(c, 3)
-                v_c(c)
-                s_cstat(c)
-            if ok(d):
-                v_lnc(d)
-                s_tanh(d)
-            if ok(a + 2):
-                v_q(a + 2)
-            for idx, blk in enumerate((1, 0, 2, 3)):
-                if ok(b):
-                    v_uw(b, blk)
-                    if blk != 3:
-                        s_act(b, blk)
-                if ok(a + 1):
-                    if idx == 1:
-                        s_nm(a + 1, 0)
-                        s_nm(a + 1, 1)
-                        pe_main(a + 1, 0)
-                        s_sq(a + 1, 0)
-                    if idx == 2:
-                        pe_main(a + 1, 1)
-                        s_sq(a + 1, 1)
-                        pe_main(a + 1, 2)
-                        s_sq(a + 1, 2)
+        def d_main(t, mk):
+            u, k = unit(t, mk)
+            n = 4 * u + k - ACC_BUFS
+            return "main%d_%d" % (u, k), ["xq%d" % t, "wq%d" % mk, "apply%d_%d" % (n // 4, n % 4)]
+
+        def d_sq(t, mk):
+            u, k = unit(t, mk)
+            deps = ["main%d_%d" % (u, k), "nm%d" % u]
+            if k == 0:
+                deps.extend(["fwd%d_%s" % (t - S_BUFS, j) for j in GATE])
+                deps.append("red%d" % (u - 4))
+            return "sq%d_%d" % (u, k), deps
+
+        def d_apply(t, mk):
+            u, k = unit(t, mk)
+            return "apply%d_%d" % (u, k), ["sq%d_%d" % (u, k)]
+
+        RING = {"f": ("bf", 2), "i": ("q", 2), "g": ("q", 2), "o": ("bo", 3)}
+        STEPS = {
+            "wcopy": (e_wcopy, lambda t, a: ("wcopy%d" % t, ["wq%d" % (t - 4)])),
+            "wq": (e_wq, lambda t, a: ("wq%d" % t, ["wcopy%d" % t])),
+            "ld": (e_ld, lambda t, a: ("ld%d" % (t // GRP), ["xt%d" % (t - GRP - 1)])),
+            "xt": (e_xt, lambda t, a: ("xt%d" % t, ["ld%d" % (t // GRP), tp_slot("xcopy%d" % t)])),
+            "xcopy": (e_xcopy, lambda t, a: ("xcopy%d" % t, ["xt%d" % t, "xq%d" % (t - 2)])),
+            "xq": (e_xq, lambda t, a: ("xq%d" % t, ["xcopy%d" % t, "main%d_3" % (2 * (t - 4) + 1)])),
+            "mean": (e_mean, lambda t, a: ("mean%d" % (2 * t + a), ["xq%d" % t, "wq%d" % (4 * a + 3), "nm%d" % (2 * t + a - 1)])),
+            "nm": (e_nm, lambda t, a: ("nm%d" % (2 * t + a), ["mean%d" % (2 * t + a), "apply%d_3" % (2 * t + a - 4)])),
+            "main": (e_main, d_main),
+            "sq": (e_sq, d_sq),
+            "apply": (e_apply, d_apply),
+            "red": (e_red, lambda t, a: ("red%d" % (2 * t + a), ["sq%d_3" % (2 * t + a), "r%d" % (2 * t + a - 4)])),
+            "r": (e_r, lambda t, a: ("r%d" % (2 * t + a), ["red%d" % (2 * t + a), "rs%d" % (2 * t + a - 4)])),
+            "rs": (e_rs, lambda t, a: ("rs%d" % (2 * t + a), ["r%d" % (2 * t + a), "apply%d_3" % (2 * t + a)])),
+            "fwd": (e_fwd, lambda t, a: ("fwd%d_%s" % (t, a), ["rs%d" % (2 * t), "rs%d" % (2 * t + 1), tp_slot("act%d_%s" % (t, a))])),
+            "act": (e_act, lambda t, a: ("act%d_%s" % (t, a), ["fwd%d_%s" % (t, a), "%s%d" % (RING[a][0], t - RING[a][1])])),
+            "bf": (e_bf, lambda t, a: ("bf%d" % t, ["act%d_f" % t, tp_slot("p%d" % t)])),
+            "bq": (e_bq, lambda t, a: ("bq%d" % t, ["q%d" % t, tp_slot("c%d" % t)])),
+            "bo": (e_bo, lambda t, a: ("bo%d" % t, ["act%d_o" % t, tp_slot("h%d" % t)])),
+            "q": (e_q, lambda t, a: ("q%d" % t, ["act%d_i" % t, "act%d_g" % t, "bq%d" % (t - 2)])),
+            "p": (e_p, lambda t, a: ("p%d" % t, ["bf%d" % t, "c%d" % (t - 2)])),
+            "c": (e_c, lambda t, a: ("c%d" % t, ["bq%d" % t, "p%d" % t, "LN%d" % (t - 3), "cstat%d" % (t - 3), "stc%d" % (t - 3)])),
+            "nmc": (e_nmc, lambda t, a: ("nmc%d" % t, ["c%d" % t, "LN%d" % (t - 4)])),
+            "cstat": (e_cstat, lambda t, a: ("cstat%d" % t, ["nmc%d" % t, "rc%d" % (t - 4)])),
+            "rc": (e_rc, lambda t, a: ("rc%d" % t, ["cstat%d" % t, "LN%d" % (t - 4)])),
+            "LN": (e_LN, lambda t, a: ("LN%d" % t, ["rc%d" % t, "tanh%d" % (t - 2)])),
+            "tanh": (e_tanh, lambda t, a: ("tanh%d" % t, ["LN%d" % t, "h%d" % (t - 2)])),
+            "h": (e_h, lambda t, a: ("h%d" % t, ["bo%d" % t, "tanh%d" % t, "sth%d" % (t - 3)])),
+            "stc": (e_stc, lambda t, a: ("stc%d" % t, ["c%d" % t])),
+            "sth": (e_sth, lambda t, a: ("sth%d" % t, ["h%d" % t])),
+        }
+        HEAD = {
+            "PE": (("xt", 0, None), ("xt", 1, None)),
+            "S": (("wcopy", 1, None), ("wcopy", 3, None), ("wcopy", 5, None), ("wcopy", 7, None)),
+            "V": (
+                ("xcopy", 0, None), ("xcopy", 1, None), ("xq", 0, None), ("wcopy", 0, None), ("xq", 1, None),
+                ("wcopy", 2, None), ("wq", 0, None), ("wq", 1, None), ("wq", 2, None), ("wcopy", 4, None),
+                ("wq", 3, None), ("wcopy", 6, None), ("wq", 4, None), ("wq", 5, None), ("wq", 6, None), ("wq", 7, None),
+            ),
+            "G": (),
+            "SP": (),
+        }
+
+        queues = {}
+        for eng in ENGINES:
+            todo = list(HEAD[eng])
+            for a in range(-3, NT + 8):
+                for op, off, arg in ORDER[eng]:
+                    t = a + off
+                    if t < 0 or t >= NT:
+                        continue
+                    if op in ("xt", "xcopy", "xq") and t < 2:
+                        continue
+                    if op == "ld" and (t % GRP != 0 or t < 2 * GRP):
+                        continue
+                    todo.append((op, t, arg))
+            queues[eng] = []
+            for op, t, arg in todo:
+                name, deps = STEPS[op][1](t, arg)
+                queues[eng].append((name, deps, op, t, arg))
+
+        names = set()
+        for eng in ENGINES:
+            for item in queues[eng]:
+                names.add(item[0])
+        done = set()
+        at = {eng: 0 for eng in ENGINES}
+        left = len(names)
+        while left > 0:
+            before = left
+            for eng in ENGINES:
+                while at[eng] < len(queues[eng]):
+                    name, deps, op, t, arg = queues[eng][at[eng]]
+                    if any(d in names and d not in done for d in deps):
+                        break
+                    if arg is None:
+                        STEPS[op][0](eng, t)
+                    else:
+                        STEPS[op][0](eng, t, arg)
+                    done.add(name)
+                    at[eng] += 1
+                    left -= 1
+            assert left < before, "the per-engine orders wait for each other"

@@ -29,31 +29,31 @@ S_BUFS = 3
 
 ORDER = {
     "PE": (
-        ("main", 0, 1), ("main", 0, 2), ("fwd", -2, "o"), ("mean", 0, 1),
-        ("main", 0, 3), ("main", 0, 4), ("bq", -2, None), ("fwd", -1, "f"),
-        ("bo", -3, None), ("xt", 2, None), ("main", 0, 5), ("main", 0, 6),
-        ("mean", 1, 0), ("main", 0, 7), ("main", 1, 0), ("fwd", -1, "i"),
-        ("fwd", -1, "g"), ("bf", -1, None),
+        ("fwd", -2, "g"), ("main", 0, 3), ("mean", 0, 1), ("main", 0, 4),
+        ("main", 0, 5), ("cpt", -2, None), ("fwd", -2, "o"), ("xt", 2, None),
+        ("main", 0, 6), ("main", 0, 7), ("mean", 1, 0), ("main", 1, 0),
+        ("bo", -4, None), ("cb", -2, None), ("main", 1, 1), ("main", 1, 2),
+        ("fwd", -1, "f"), ("fwd", -1, "i"),
     ),
     "S": (
-        ("sq", 0, 1), ("act", -2, "o"), ("sq", 0, 2), ("sq", 0, 3),
-        ("nm", 0, 1), ("sq", 0, 4), ("tanh", -3, None), ("act", -1, "f"),
-        ("sq", 0, 5), ("sq", 0, 6), ("cstat", -2, None), ("sq", 0, 7),
-        ("nm", 1, 0), ("sq", 1, 0), ("act", -1, "i"), ("act", -1, "g"),
+        ("act", -2, "i"), ("act", -2, "g"), ("sq", 0, 3), ("nm", 0, 1),
+        ("sq", 0, 4), ("sq", 0, 5), ("tanh", -4, None), ("sq", 0, 6),
+        ("cstat", -3, None), ("sq", 0, 7), ("xcopy", 2, None), ("act", -2, "o"),
+        ("nm", 1, 0), ("sq", 1, 0), ("sq", 1, 1), ("sq", 1, 2),
+        ("act", -1, "f"), ("ccopy", -2, None),
     ),
     "V": (
-        ("apply", 0, 1), ("LN", -3, None), ("apply", 0, 2), ("red", 0, 0),
-        ("apply", 0, 3), ("xq", 1, None), ("c", -2, None), ("nmc", -2, None),
-        ("apply", 0, 4), ("apply", 0, 5), ("h", -3, None), ("apply", 0, 6),
-        ("red", 0, 1), ("apply", 0, 7), ("xcopy", 2, None), ("apply", 1, 0),
-        ("p", -1, None), ("q", -1, None),
+        ("apply", 0, 3), ("xq", 1, None), ("nmc", -3, None), ("apply", 0, 4),
+        ("p", -2, None), ("apply", 0, 5), ("rs", -1, 1), ("apply", 0, 6),
+        ("apply", 0, 7), ("red", 0, 0), ("h", -4, None), ("red", 0, 1),
+        ("apply", 1, 0), ("apply", 1, 1), ("LN", -3, None), ("apply", 1, 2),
+        ("rs", 0, 0), ("q", -1, None),
     ),
     "G": (
-        ("r", 0, 0), ("rs", 0, 0), ("rc", -2, None), ("r", 0, 1),
-        ("rs", 0, 1),
+        ("rc", -3, None), ("r", 0, 0), ("r", 0, 1),
     ),
     "SP": (
-        ("ld", 6, None), ("stc", -2, None), ("sth", -3, None),
+        ("ld", 6, None), ("stc", -2, None), ("sth", -4, None),
     ),
 }
 
@@ -84,7 +84,10 @@ def tile_layernormlstmcell_kernel(
         make_identity(nc, ident[:])
         neghalf = const.tile([P, 1], F32, name="neghalf")
         nc.gpsimd.memset(neghalf[:], -0.5)
+        identb = const.tile([P, P], BF16, name="identb")
+        nc.vector.tensor_copy(out=identb[:], in_=ident[:])
         junkm = const.tile([P, P], F32, name="junkm")
+        junkv = const.tile([P, P], F32, name="junkv")
         junkc = const.tile([P, H], F32, name="junkc")
         wc = [const.tile([P, G], U32, name="wc%d" % m, align_bytes=64) for m in range(2)]
         ws = [const.tile([P, G], U8, name="ws%d" % m, align_bytes=64) for m in range(2)]
@@ -197,9 +200,15 @@ def tile_layernormlstmcell_kernel(
 
         def e_nm(eng, t, m):
             nm = small.tile([P, 1], F32, name="nm")
-            nc.scalar.activation(
-                out=junkm[:], in_=T[("mean", t, m)][:], func=ACT.Identity, scale=-1.0 / G, accum_out=nm[:]
-            )
+            if eng == "V":
+                nc.vector.tensor_scalar(
+                    out=junkv[:], in0=T[("mean", t, m)][:], scalar1=-1.0 / G, scalar2=0.0, op0=ALU.mult, op1=ALU.add,
+                    accum_out=nm[:],
+                )
+            else:
+                nc.scalar.activation(
+                    out=junkm[:], in_=T[("mean", t, m)][:], func=ACT.Identity, scale=-1.0 / G, accum_out=nm[:]
+                )
             T[("nm", t, m)] = nm
 
         def e_main(eng, t, mk):
@@ -272,23 +281,21 @@ def tile_layernormlstmcell_kernel(
                 )
             T[("gate", t, j)] = gt
 
-        def back(src):
-            bk = ps_tp.tile([P, 4, P], F32, name="tp")
-            for q in range(4):
-                nc.tensor.transpose(bk[:, q, :], src[:, q, :], ident[:])
-            return bk
-
-        def e_bf(eng, t):
-            T[("bf", t)] = back(T[("gate", t, "f")])
-
-        def e_bq(eng, t):
-            T[("bq", t)] = back(T[("qT", t)])
-
-        def e_bo(eng, t):
-            T[("bo", t)] = back(T[("gate", t, "o")])
-
         def flat(til):
             return til[:].rearrange("p q r -> p (q r)")
+
+        def e_bo(eng, t):
+            bk = ps_tp.tile([P, 4, P], F32, name="tp")
+            for q in range(4):
+                nc.tensor.transpose(bk[:, q, :], T[("gate", t, "o")][:, q, :], ident[:])
+            T[("bo", t)] = bk
+
+        def e_cpt(eng, t):
+            cp = ps_tp.tile([P, 4, P], F32, name="tp")
+            view = flat(cp).bitcast(BF16)
+            for q in range(4):
+                nc.tensor.transpose(view[:, q * P:(q + 1) * P], cin[:, t, q * P:(q + 1) * P], identb[:])
+            T[("cpt", t)] = view[:, 0:H]
 
         def e_q(eng, t):
             qT = work.tile([P, 4, P], F32, name="qT")
@@ -296,17 +303,24 @@ def tile_layernormlstmcell_kernel(
             T[("qT", t)] = qT
 
         def e_p(eng, t):
-            pt = work.tile([P, H], F32, name="pt")
-            nc.vector.tensor_tensor(out=pt[:], in0=flat(T[("bf", t)]), in1=cin[:, t, :], op=ALU.mult)
-            T[("pt", t)] = pt
+            pT = work.tile([P, 4, P], F32, name="pT")
+            nc.vector.tensor_tensor(out=flat(pT), in0=flat(T[("gate", t, "f")]), in1=T[("cpt", t)], op=ALU.mult)
+            T[("pT", t)] = pT
 
-        def e_c(eng, t):
+        def e_cb(eng, t):
+            cb = ps_tp.tile([P, 4, P], F32, name="tp")
+            for q in range(4):
+                for n, key in enumerate(("pT", "qT")):
+                    nc.tensor.matmul(
+                        out=cb[:, q, :], lhsT=T[(key, t)][:, q, :], rhs=ident[:], is_transpose=True,
+                        start=(n == 0), stop=(n == 1),
+                    )
+            T[("cb", t)] = cb
+
+        def e_ccopy(eng, t):
             ct = work.tile([P, H], F32, name="ct", bufs=3)
             csum = small.tile([P, 1], F32, name="csum")
-            nc.vector.scalar_tensor_tensor(
-                out=ct[:], in0=flat(T[("bq", t)]), scalar=1.0, in1=T[("pt", t)][:], op0=ALU.mult, op1=ALU.add,
-                accum_out=csum[:],
-            )
+            nc.scalar.activation(out=ct[:], in_=flat(T[("cb", t)]), func=ACT.Identity, accum_out=csum[:])
             T[("ct", t)] = ct
             T[("csum", t)] = csum
 
@@ -378,7 +392,7 @@ def tile_layernormlstmcell_kernel(
             u, k = unit(t, mk)
             return "apply%d_%d" % (u, k), ["sq%d_%d" % (u, k)]
 
-        RING = {"f": ("bf", 2), "i": ("q", 2), "g": ("q", 2), "o": ("bo", 3)}
+        RING = {"f": ("p", 2), "i": ("q", 2), "g": ("q", 2), "o": ("bo", 3)}
         STEPS = {
             "wcopy": (e_wcopy, lambda t, a: ("wcopy%d" % t, ["wq%d" % (t - 4)])),
             "wq": (e_wq, lambda t, a: ("wq%d" % t, ["wcopy%d" % t])),
@@ -396,19 +410,19 @@ def tile_layernormlstmcell_kernel(
             "rs": (e_rs, lambda t, a: ("rs%d" % (2 * t + a), ["r%d" % (2 * t + a), "apply%d_3" % (2 * t + a)])),
             "fwd": (e_fwd, lambda t, a: ("fwd%d_%s" % (t, a), ["rs%d" % (2 * t), "rs%d" % (2 * t + 1), tp_slot("act%d_%s" % (t, a))])),
             "act": (e_act, lambda t, a: ("act%d_%s" % (t, a), ["fwd%d_%s" % (t, a), "%s%d" % (RING[a][0], t - RING[a][1])])),
-            "bf": (e_bf, lambda t, a: ("bf%d" % t, ["act%d_f" % t, tp_slot("p%d" % t)])),
-            "bq": (e_bq, lambda t, a: ("bq%d" % t, ["q%d" % t, tp_slot("c%d" % t)])),
+            "cpt": (e_cpt, lambda t, a: ("cpt%d" % t, [tp_slot("p%d" % t)])),
+            "cb": (e_cb, lambda t, a: ("cb%d" % t, ["p%d" % t, "q%d" % t, tp_slot("ccopy%d" % t)])),
             "bo": (e_bo, lambda t, a: ("bo%d" % t, ["act%d_o" % t, tp_slot("h%d" % t)])),
-            "q": (e_q, lambda t, a: ("q%d" % t, ["act%d_i" % t, "act%d_g" % t, "bq%d" % (t - 2)])),
-            "p": (e_p, lambda t, a: ("p%d" % t, ["bf%d" % t, "c%d" % (t - 2)])),
-            "c": (e_c, lambda t, a: ("c%d" % t, ["bq%d" % t, "p%d" % t, "LN%d" % (t - 3), "cstat%d" % (t - 3), "stc%d" % (t - 3)])),
-            "nmc": (e_nmc, lambda t, a: ("nmc%d" % t, ["c%d" % t, "LN%d" % (t - 4)])),
+            "q": (e_q, lambda t, a: ("q%d" % t, ["act%d_i" % t, "act%d_g" % t, "cb%d" % (t - 2)])),
+            "p": (e_p, lambda t, a: ("p%d" % t, ["act%d_f" % t, "cpt%d" % t, "cb%d" % (t - 2)])),
+            "ccopy": (e_ccopy, lambda t, a: ("ccopy%d" % t, ["cb%d" % t, "LN%d" % (t - 3), "cstat%d" % (t - 3), "stc%d" % (t - 3)])),
+            "nmc": (e_nmc, lambda t, a: ("nmc%d" % t, ["ccopy%d" % t, "LN%d" % (t - 4)])),
             "cstat": (e_cstat, lambda t, a: ("cstat%d" % t, ["nmc%d" % t, "rc%d" % (t - 4)])),
             "rc": (e_rc, lambda t, a: ("rc%d" % t, ["cstat%d" % t, "LN%d" % (t - 4)])),
             "LN": (e_LN, lambda t, a: ("LN%d" % t, ["rc%d" % t, "tanh%d" % (t - 2)])),
             "tanh": (e_tanh, lambda t, a: ("tanh%d" % t, ["LN%d" % t, "h%d" % (t - 2)])),
             "h": (e_h, lambda t, a: ("h%d" % t, ["bo%d" % t, "tanh%d" % t, "sth%d" % (t - 3)])),
-            "stc": (e_stc, lambda t, a: ("stc%d" % t, ["c%d" % t])),
+            "stc": (e_stc, lambda t, a: ("stc%d" % t, ["ccopy%d" % t])),
             "sth": (e_sth, lambda t, a: ("sth%d" % t, ["h%d" % t])),
         }
         HEAD = {
@@ -426,7 +440,7 @@ def tile_layernormlstmcell_kernel(
         queues = {}
         for eng in ENGINES:
             todo = list(HEAD[eng])
-            for a in range(-3, NT + 8):
+            for a in range(-3, NT + 9):
                 for op, off, arg in ORDER[eng]:
                     t = a + off
                     if t < 0 or t >= NT:

@@ -21,39 +21,39 @@ NT = B // P
 GRP = 4
 EPS = 1e-5
 FLOPS = 2 * 2 * B * K * G
-GATE = {"i": 0, "f": 1, "g": 2, "o": 3}
+GATE = {"i": 0, "f": 1, "g": 2}
+TCOLS = 3 * H
 ENGINES = ("PE", "S", "V", "G", "SP")
-ACC_BUFS = 3
-TP_BUFS = 4
+ACC_BUFS = 4
+TP_BUFS = 3
 S_BUFS = 3
 
 ORDER = {
     "PE": (
-        ("fwd", -2, "g"), ("main", 0, 3), ("mean", 0, 1), ("main", 0, 4),
-        ("main", 0, 5), ("cpt", -2, None), ("fwd", -2, "o"), ("xt", 2, None),
-        ("main", 0, 6), ("main", 0, 7), ("mean", 1, 0), ("main", 1, 0),
-        ("bo", -4, None), ("cb", -2, None), ("main", 1, 1), ("main", 1, 2),
-        ("fwd", -1, "f"), ("fwd", -1, "i"),
+        ("main", 0, 5), ("mean", 1, 0), ("main", 0, 6), ("fwd", -2, "f"),
+        ("fwd", -2, "i"), ("main", 0, 7), ("main", 1, 0), ("main", 1, 1),
+        ("xt", 2, None), ("cb", -3, None), ("main", 1, 2), ("mean", 1, 1),
+        ("main", 1, 3), ("main", 1, 4), ("cpt", -2, None), ("fwd", -1, "g"),
     ),
     "S": (
-        ("act", -2, "i"), ("act", -2, "g"), ("sq", 0, 3), ("nm", 0, 1),
-        ("sq", 0, 4), ("sq", 0, 5), ("tanh", -4, None), ("sq", 0, 6),
-        ("cstat", -3, None), ("sq", 0, 7), ("xcopy", 2, None), ("act", -2, "o"),
-        ("nm", 1, 0), ("sq", 1, 0), ("sq", 1, 1), ("sq", 1, 2),
-        ("act", -1, "f"), ("ccopy", -2, None),
+        ("act", -2, "i"), ("nm", 1, 0), ("sq", 0, 7), ("sq", 1, 0),
+        ("sq", 1, 1), ("xcopy", 2, None), ("sq", 1, 2), ("nm", 1, 1),
+        ("tanh", -6, None), ("sq", 1, 3), ("ccopy", -3, None), ("nmc", -4, None),
+        ("sq", 1, 4), ("cstat", -4, None), ("sq", 1, 5), ("act", -1, "g"),
+        ("sq", 1, 6), ("acto", -3, None), ("act", -1, "f"),
     ),
     "V": (
-        ("apply", 0, 3), ("xq", 1, None), ("nmc", -3, None), ("apply", 0, 4),
-        ("p", -2, None), ("apply", 0, 5), ("rs", -1, 1), ("apply", 0, 6),
-        ("apply", 0, 7), ("red", 0, 0), ("h", -4, None), ("red", 0, 1),
-        ("apply", 1, 0), ("apply", 1, 1), ("LN", -3, None), ("apply", 1, 2),
-        ("rs", 0, 0), ("q", -1, None),
+        ("apply", 0, 7), ("apply", 1, 0), ("red", 0, 0), ("apply", 1, 1),
+        ("xq", 2, None), ("LN", -5, None), ("apply", 1, 2), ("q", -2, None),
+        ("p", -2, None), ("apply", 1, 3), ("h", -6, None), ("apply", 1, 4),
+        ("red", 0, 1), ("apply", 1, 5), ("rs", 0, 0), ("apply", 1, 6),
+        ("uo", -1, None), ("rs", 0, 1),
     ),
     "G": (
-        ("rc", -3, None), ("r", 0, 0), ("r", 0, 1),
+        ("rc", -4, None), ("r", 0, 1), ("r", 1, 0),
     ),
     "SP": (
-        ("ld", 6, None), ("stc", -2, None), ("sth", -4, None),
+        ("ld", 6, None), ("stc", -3, None), ("sth", -6, None),
     ),
 }
 
@@ -97,6 +97,7 @@ def tile_layernormlstmcell_kernel(
         cin = const.tile([P, NT, H], BF16, name="cin")
         bt32 = const.tile([P, P], F32, name="bt32")
         betaT = const.tile([P, G // P], F32, name="betaT")
+        bso = const.tile([P, H], F32, name="bso")
 
         T = {}
 
@@ -111,7 +112,11 @@ def tile_layernormlstmcell_kernel(
         for W in (W_ih, W_hh):
             for hf in range(2):
                 raw = prep.tile([P, 4, 1024], BF16, name="raw")
-                nc.sync.dma_start(out=raw[:], in_=W[:, hf * 1024:(hf + 1) * 1024].rearrange("(p j) c -> p j c", j=4))
+                for u in range(2):
+                    nc.sync.dma_start(
+                        out=raw[:, 2 * u:2 * u + 2, :],
+                        in_=W[256 * u:256 * (u + 1), hf * 1024:(hf + 1) * 1024].rearrange("(p e) c -> p e c", e=2),
+                    )
                 raws.append(raw)
         nc.sync.dma_start(out=cin[:], in_=c_v)
         load_group(1)
@@ -121,8 +126,12 @@ def tile_layernormlstmcell_kernel(
         nc.scalar.dma_start(out=bb[:], in_=beta_hh.rearrange("(r c) -> r c", c=P))
         nc.scalar.dma_start(out=gam[0][:], in_=gamma_ih.partition_broadcast(P))
         nc.scalar.dma_start(out=gam[1][:], in_=gamma_hh.partition_broadcast(P))
-        nc.scalar.dma_start(out=gamc[:], in_=gamma_c.partition_broadcast(P))
-        nc.scalar.dma_start(out=betc[:], in_=beta_c.partition_broadcast(P))
+        bo1 = prep.tile([P, H], BF16, name="bo1", bufs=1)
+        bo2 = prep.tile([P, H], BF16, name="bo2", bufs=1)
+        nc.sync.dma_start(out=bo1[:], in_=beta_ih[TCOLS:G].partition_broadcast(P))
+        nc.sync.dma_start(out=bo2[:], in_=beta_hh[TCOLS:G].partition_broadcast(P))
+        nc.sync.dma_start(out=gamc[:], in_=gamma_c.partition_broadcast(P))
+        nc.sync.dma_start(out=betc[:], in_=beta_c.partition_broadcast(P))
 
         nc.vector.memset(bt32[:], 0.0)
         nc.vector.tensor_tensor(out=bt32[0:16, :], in0=ba[:], in1=bb[:], op=ALU.add)
@@ -156,9 +165,9 @@ def tile_layernormlstmcell_kernel(
             xt = ps_tp.tile([P, 4, P], F32, name="tp")
             for o, nm_ in enumerate(("xin", "hin")):
                 src = T[(nm_, t // GRP)]
-                words = src[:, t % GRP, :].bitcast(F32).rearrange("p (w u) -> p u w", u=2)
+                words = src[:, t % GRP, :].bitcast(F32)
                 for u in range(2):
-                    nc.tensor.transpose(xt[:, 2 * o + u, :], words[:, u, :], ident[:])
+                    nc.tensor.transpose(xt[:, 2 * o + u, :], words[:, u * P:(u + 1) * P], ident[:])
             T[("xt", t)] = xt
 
         def e_xcopy(eng, t):
@@ -243,7 +252,7 @@ def tile_layernormlstmcell_kernel(
         def rstd(sumsq, count, nm_):
             var = small.tile([P, 1], F32, name="var" + nm_)
             nc.gpsimd.tensor_scalar(out=var[:], in0=sumsq[:], scalar1=1.0 / count, scalar2=EPS, op0=ALU.mult, op1=ALU.add)
-            r = small.tile([P, 1], F32, name="r" + nm_)
+            r = small.tile([P, 1], F32, name="r" + nm_, bufs=6)
             nc.gpsimd.tensor_tensor(out=r[:], in0=var[:], in1=neghalf[:], op=ALU.pow)
             return r
 
@@ -251,14 +260,29 @@ def tile_layernormlstmcell_kernel(
             T[("r", t, m)] = rstd(T[("ssum", t, m)], G, "g")
 
         def e_rs(eng, t, m):
-            s = T[("s", t, m)]
+            s = T[("s", t, m)][:, 0:TCOLS]
             r = T[("r", t, m)]
-            if eng == "G":
-                nc.gpsimd.tensor_scalar(out=s[:], in0=s[:], scalar1=r[:], scalar2=0.0, op0=ALU.mult, op1=ALU.add)
-            elif eng == "V":
-                nc.vector.tensor_scalar(out=s[:], in0=s[:], scalar1=r[:], scalar2=None, op0=ALU.mult)
+            if eng == "V":
+                nc.vector.tensor_scalar(out=s, in0=s, scalar1=r[:], scalar2=None, op0=ALU.mult)
             else:
-                nc.scalar.activation(out=s[:], in_=s[:], func=ACT.Copy, scale=r[:])
+                nc.scalar.activation(out=s, in_=s, func=ACT.Copy, scale=r[:])
+
+        def e_uo(eng, t):
+            if t == 0:
+                nc.vector.tensor_tensor(out=bso[:], in0=bo1[:], in1=bo2[:], op=ALU.add)
+            uo = work.tile([P, H], F32, name="uo")
+            nc.vector.scalar_tensor_tensor(
+                out=uo[:], in0=T[("s", t, 0)][:, TCOLS:G], scalar=T[("r", t, 0)][:], in1=bso[:], op0=ALU.mult, op1=ALU.add
+            )
+            nc.vector.scalar_tensor_tensor(
+                out=uo[:], in0=T[("s", t, 1)][:, TCOLS:G], scalar=T[("r", t, 1)][:], in1=uo[:], op0=ALU.mult, op1=ALU.add
+            )
+            T[("uo", t)] = uo
+
+        def e_acto(eng, t):
+            og = work.tile([P, H], F32, name="og", bufs=3)
+            nc.scalar.activation(out=og[:], in_=T[("uo", t)][:], func=ACT.Sigmoid)
+            T[("og", t)] = og
 
         def e_fwd(eng, t, j):
             zt = ps_tp.tile([P, 4, P], F32, name="tp")
@@ -272,7 +296,7 @@ def tile_layernormlstmcell_kernel(
             T[("zt", t, j)] = zt
 
         def e_act(eng, t, j):
-            gt = work.tile([P, 4, P], F32, name="gate_" + j, bufs=(3 if j == "o" else 2))
+            gt = work.tile([P, 4, P], F32, name="gate_" + j)
             for q in range(4):
                 gb = GATE[j] * 4 + q
                 nc.scalar.activation(
@@ -283,12 +307,6 @@ def tile_layernormlstmcell_kernel(
 
         def flat(til):
             return til[:].rearrange("p q r -> p (q r)")
-
-        def e_bo(eng, t):
-            bk = ps_tp.tile([P, 4, P], F32, name="tp")
-            for q in range(4):
-                nc.tensor.transpose(bk[:, q, :], T[("gate", t, "o")][:, q, :], ident[:])
-            T[("bo", t)] = bk
 
         def e_cpt(eng, t):
             cp = ps_tp.tile([P, 4, P], F32, name="tp")
@@ -326,7 +344,10 @@ def tile_layernormlstmcell_kernel(
 
         def e_nmc(eng, t):
             nmc = small.tile([P, 1], F32, name="nmc")
-            nc.vector.tensor_scalar(out=nmc[:], in0=T[("csum", t)][:], scalar1=-1.0 / H, scalar2=None, op0=ALU.mult)
+            if eng == "V":
+                nc.vector.tensor_scalar(out=nmc[:], in0=T[("csum", t)][:], scalar1=-1.0 / H, scalar2=None, op0=ALU.mult)
+            else:
+                nc.scalar.mul(out=nmc[:], in_=T[("csum", t)][:], mul=-1.0 / H)
             T[("nmc", t)] = nmc
 
         def e_cstat(eng, t):
@@ -356,7 +377,7 @@ def tile_layernormlstmcell_kernel(
 
         def e_h(eng, t):
             ht = work.tile([P, H], F32, name="ht", bufs=3)
-            nc.vector.tensor_tensor(out=ht[:], in0=flat(T[("bo", t)]), in1=T[("th", t)][:], op=ALU.mult)
+            nc.vector.tensor_tensor(out=ht[:], in0=T[("og", t)][:], in1=T[("th", t)][:], op=ALU.mult)
             T[("ht", t)] = ht
 
         def e_stc(eng, t):
@@ -385,6 +406,7 @@ def tile_layernormlstmcell_kernel(
             deps = ["main%d_%d" % (u, k), "nm%d" % u]
             if k == 0:
                 deps.extend(["fwd%d_%s" % (t - S_BUFS, j) for j in GATE])
+                deps.append("uo%d" % (t - S_BUFS))
                 deps.append("red%d" % (u - 4))
             return "sq%d_%d" % (u, k), deps
 
@@ -392,7 +414,7 @@ def tile_layernormlstmcell_kernel(
             u, k = unit(t, mk)
             return "apply%d_%d" % (u, k), ["sq%d_%d" % (u, k)]
 
-        RING = {"f": ("p", 2), "i": ("q", 2), "g": ("q", 2), "o": ("bo", 3)}
+        RING = {"f": ("p", 2), "i": ("q", 2), "g": ("q", 2)}
         STEPS = {
             "wcopy": (e_wcopy, lambda t, a: ("wcopy%d" % t, ["wq%d" % (t - 4)])),
             "wq": (e_wq, lambda t, a: ("wq%d" % t, ["wcopy%d" % t])),
@@ -406,13 +428,14 @@ def tile_layernormlstmcell_kernel(
             "sq": (e_sq, d_sq),
             "apply": (e_apply, d_apply),
             "red": (e_red, lambda t, a: ("red%d" % (2 * t + a), ["sq%d_3" % (2 * t + a), "r%d" % (2 * t + a - 4)])),
-            "r": (e_r, lambda t, a: ("r%d" % (2 * t + a), ["red%d" % (2 * t + a), "rs%d" % (2 * t + a - 4)])),
-            "rs": (e_rs, lambda t, a: ("rs%d" % (2 * t + a), ["r%d" % (2 * t + a), "apply%d_3" % (2 * t + a)])),
+            "r": (e_r, lambda t, a: ("r%d" % (2 * t + a), ["red%d" % (2 * t + a), "rs%d" % (2 * t + a - 4), "uo%d" % (t - 3)])),
+            "rs": (e_rs, lambda t, a: ("rs%d" % (2 * t + a), ["r%d" % (2 * t + a), "apply%d_2" % (2 * t + a)])),
+            "uo": (e_uo, lambda t, a: ("uo%d" % t, ["r%d" % (2 * t), "r%d" % (2 * t + 1), "apply%d_3" % (2 * t), "apply%d_3" % (2 * t + 1), "acto%d" % (t - 2)])),
+            "acto": (e_acto, lambda t, a: ("acto%d" % t, ["uo%d" % t, "h%d" % (t - 3)])),
             "fwd": (e_fwd, lambda t, a: ("fwd%d_%s" % (t, a), ["rs%d" % (2 * t), "rs%d" % (2 * t + 1), tp_slot("act%d_%s" % (t, a))])),
             "act": (e_act, lambda t, a: ("act%d_%s" % (t, a), ["fwd%d_%s" % (t, a), "%s%d" % (RING[a][0], t - RING[a][1])])),
             "cpt": (e_cpt, lambda t, a: ("cpt%d" % t, [tp_slot("p%d" % t)])),
             "cb": (e_cb, lambda t, a: ("cb%d" % t, ["p%d" % t, "q%d" % t, tp_slot("ccopy%d" % t)])),
-            "bo": (e_bo, lambda t, a: ("bo%d" % t, ["act%d_o" % t, tp_slot("h%d" % t)])),
             "q": (e_q, lambda t, a: ("q%d" % t, ["act%d_i" % t, "act%d_g" % t, "cb%d" % (t - 2)])),
             "p": (e_p, lambda t, a: ("p%d" % t, ["act%d_f" % t, "cpt%d" % t, "cb%d" % (t - 2)])),
             "ccopy": (e_ccopy, lambda t, a: ("ccopy%d" % t, ["cb%d" % t, "LN%d" % (t - 3), "cstat%d" % (t - 3), "stc%d" % (t - 3)])),
@@ -421,7 +444,7 @@ def tile_layernormlstmcell_kernel(
             "rc": (e_rc, lambda t, a: ("rc%d" % t, ["cstat%d" % t, "LN%d" % (t - 4)])),
             "LN": (e_LN, lambda t, a: ("LN%d" % t, ["rc%d" % t, "tanh%d" % (t - 2)])),
             "tanh": (e_tanh, lambda t, a: ("tanh%d" % t, ["LN%d" % t, "h%d" % (t - 2)])),
-            "h": (e_h, lambda t, a: ("h%d" % t, ["bo%d" % t, "tanh%d" % t, "sth%d" % (t - 3)])),
+            "h": (e_h, lambda t, a: ("h%d" % t, ["acto%d" % t, "tanh%d" % t, "sth%d" % (t - 3)])),
             "stc": (e_stc, lambda t, a: ("stc%d" % t, ["ccopy%d" % t])),
             "sth": (e_sth, lambda t, a: ("sth%d" % t, ["h%d" % t])),
         }

@@ -30,24 +30,24 @@ S_BUFS = 3
 
 ORDER = {
     "PE": (
-        ("main", 0, 5), ("mean", 1, 0), ("main", 0, 6), ("fwd", -2, "f"),
-        ("fwd", -2, "i"), ("main", 0, 7), ("main", 1, 0), ("main", 1, 1),
-        ("xt", 2, None), ("cb", -3, None), ("main", 1, 2), ("mean", 1, 1),
-        ("main", 1, 3), ("main", 1, 4), ("cpt", -2, None), ("fwd", -1, "g"),
+        ("main", 0, 5), ("main", 0, 6), ("fwd", -2, "f"), ("mean", 1, 0),
+        ("main", 0, 7), ("main", 1, 0), ("fwd", -2, "i"), ("xt", 2, None),
+        ("main", 1, 1), ("main", 1, 2), ("mean", 1, 1), ("cpt", -2, None),
+        ("cb", -3, None), ("fwd", -1, "g"), ("main", 1, 3), ("main", 1, 4),
     ),
     "S": (
-        ("act", -2, "i"), ("nm", 1, 0), ("sq", 0, 7), ("sq", 1, 0),
-        ("sq", 1, 1), ("xcopy", 2, None), ("sq", 1, 2), ("nm", 1, 1),
-        ("tanh", -6, None), ("sq", 1, 3), ("ccopy", -3, None), ("nmc", -4, None),
-        ("sq", 1, 4), ("cstat", -4, None), ("sq", 1, 5), ("act", -1, "g"),
-        ("sq", 1, 6), ("acto", -3, None), ("act", -1, "f"),
+        ("nm", 1, 0), ("sq", 0, 7), ("sq", 1, 0), ("act", -2, "i"),
+        ("xcopy", 2, None), ("sq", 1, 1), ("sq", 1, 2), ("cstat", -4, None),
+        ("nm", 1, 1), ("ccopy", -3, None), ("sq", 1, 3), ("sq", 1, 4),
+        ("sq", 1, 5), ("acto", -3, None), ("sq", 1, 6), ("act", -1, "g"),
+        ("act", -1, "f"), ("tanh", -5, None),
     ),
     "V": (
-        ("apply", 0, 7), ("apply", 1, 0), ("red", 0, 0), ("apply", 1, 1),
-        ("xq", 2, None), ("LN", -5, None), ("apply", 1, 2), ("q", -2, None),
-        ("p", -2, None), ("apply", 1, 3), ("h", -6, None), ("apply", 1, 4),
-        ("red", 0, 1), ("apply", 1, 5), ("rs", 0, 0), ("apply", 1, 6),
-        ("uo", -1, None), ("rs", 0, 1),
+        ("apply", 0, 6), ("rs", -1, 1), ("LN", -5, None), ("apply", 0, 7),
+        ("h", -6, None), ("apply", 1, 0), ("red", 0, 0), ("xq", 2, None),
+        ("apply", 1, 1), ("apply", 1, 2), ("p", -2, None), ("q", -2, None),
+        ("rs", 0, 0), ("apply", 1, 3), ("red", 0, 1), ("apply", 1, 4),
+        ("apply", 1, 5), ("uo", -1, None), ("nmc", -3, None),
     ),
     "G": (
         ("rc", -4, None), ("r", 0, 1), ("r", 1, 0),
@@ -95,9 +95,7 @@ def tile_layernormlstmcell_kernel(
         gamc = const.tile([P, H], BF16, name="gamc")
         betc = const.tile([P, H], BF16, name="betc")
         cin = const.tile([P, NT, H], BF16, name="cin")
-        bt32 = const.tile([P, P], F32, name="bt32")
-        betaT = const.tile([P, G // P], F32, name="betaT")
-        bso = const.tile([P, H], F32, name="bso")
+        bsum = const.tile([P, G], F32, name="bsum")
 
         T = {}
 
@@ -107,9 +105,13 @@ def tile_layernormlstmcell_kernel(
                 nc.sync.dma_start(out=til[:], in_=view[:, g * GRP:(g + 1) * GRP, :])
                 T[(nm_, g)] = til
 
-        load_group(0)
+        first = {}
+        for nm_, view in (("xin", x_v), ("hin", h_v)):
+            first[nm_] = io.tile([P, GRP, K], BF16, name=nm_)
+            nc.sync.dma_start(out=first[nm_][:, 0:2, :], in_=view[:, 0:2, :])
+            T[(nm_, 0)] = first[nm_]
         raws = []
-        for W in (W_ih, W_hh):
+        for m, W in enumerate((W_ih, W_hh)):
             for hf in range(2):
                 raw = prep.tile([P, 4, 1024], BF16, name="raw")
                 for u in range(2):
@@ -118,26 +120,16 @@ def tile_layernormlstmcell_kernel(
                         in_=W[256 * u:256 * (u + 1), hf * 1024:(hf + 1) * 1024].rearrange("(p e) c -> p e c", e=2),
                     )
                 raws.append(raw)
+            nc.sync.dma_start(out=gam[m][:], in_=(gamma_ih, gamma_hh)[m].partition_broadcast(P))
+        for nm_, view in (("xin", x_v), ("hin", h_v)):
+            nc.sync.dma_start(out=first[nm_][:, 2:GRP, :], in_=view[:, 2:GRP, :])
         nc.sync.dma_start(out=cin[:], in_=c_v)
         load_group(1)
-        ba = prep.tile([16, P], BF16, name="ba", bufs=1)
-        bb = prep.tile([16, P], BF16, name="bb", bufs=1)
-        nc.scalar.dma_start(out=ba[:], in_=beta_ih.rearrange("(r c) -> r c", c=P))
-        nc.scalar.dma_start(out=bb[:], in_=beta_hh.rearrange("(r c) -> r c", c=P))
-        nc.scalar.dma_start(out=gam[0][:], in_=gamma_ih.partition_broadcast(P))
-        nc.scalar.dma_start(out=gam[1][:], in_=gamma_hh.partition_broadcast(P))
-        bo1 = prep.tile([P, H], BF16, name="bo1", bufs=1)
-        bo2 = prep.tile([P, H], BF16, name="bo2", bufs=1)
-        nc.sync.dma_start(out=bo1[:], in_=beta_ih[TCOLS:G].partition_broadcast(P))
-        nc.sync.dma_start(out=bo2[:], in_=beta_hh[TCOLS:G].partition_broadcast(P))
         nc.sync.dma_start(out=gamc[:], in_=gamma_c.partition_broadcast(P))
         nc.sync.dma_start(out=betc[:], in_=beta_c.partition_broadcast(P))
 
-        nc.vector.memset(bt32[:], 0.0)
-        nc.vector.tensor_tensor(out=bt32[0:16, :], in0=ba[:], in1=bb[:], op=ALU.add)
-        tpb = ps_tp.tile([P, 4, P], F32, name="tp")
-        nc.tensor.transpose(tpb[:, 0, :], bt32[:], ident[:])
-        nc.vector.tensor_copy(out=betaT[:], in_=tpb[:, 0, 0:G // P])
+        def flat(til):
+            return til[:].rearrange("p q r -> p (q r)")
 
         def e_wcopy(eng, u):
             grp = prep.tile([P, 512, 4], BF16, name="grp", align_bytes=64)
@@ -160,6 +152,18 @@ def tile_layernormlstmcell_kernel(
 
         def e_ld(eng, t):
             load_group(t // GRP)
+
+        def e_ldb(eng, t):
+            for n, vec in enumerate((beta_ih, beta_hh)):
+                stage = prep.tile([P, 512, 4], BF16, name="grp", align_bytes=64)
+                nc.sync.dma_start(out=stage[:].rearrange("p c t -> p (c t)"), in_=vec.partition_broadcast(P))
+                T[("bstage", n)] = stage
+
+        def e_bsum(eng, t):
+            nc.vector.tensor_tensor(
+                out=bsum[:], in0=T[("bstage", 0)][:].rearrange("p c t -> p (c t)"),
+                in1=T[("bstage", 1)][:].rearrange("p c t -> p (c t)"), op=ALU.add,
+            )
 
         def e_xt(eng, t):
             xt = ps_tp.tile([P, 4, P], F32, name="tp")
@@ -268,11 +272,9 @@ def tile_layernormlstmcell_kernel(
                 nc.scalar.activation(out=s, in_=s, func=ACT.Copy, scale=r[:])
 
         def e_uo(eng, t):
-            if t == 0:
-                nc.vector.tensor_tensor(out=bso[:], in0=bo1[:], in1=bo2[:], op=ALU.add)
             uo = work.tile([P, H], F32, name="uo")
             nc.vector.scalar_tensor_tensor(
-                out=uo[:], in0=T[("s", t, 0)][:, TCOLS:G], scalar=T[("r", t, 0)][:], in1=bso[:], op0=ALU.mult, op1=ALU.add
+                out=uo[:], in0=T[("s", t, 0)][:, TCOLS:G], scalar=T[("r", t, 0)][:], in1=bsum[:, TCOLS:G], op0=ALU.mult, op1=ALU.add
             )
             nc.vector.scalar_tensor_tensor(
                 out=uo[:], in0=T[("s", t, 1)][:, TCOLS:G], scalar=T[("r", t, 1)][:], in1=uo[:], op0=ALU.mult, op1=ALU.add
@@ -288,25 +290,17 @@ def tile_layernormlstmcell_kernel(
             zt = ps_tp.tile([P, 4, P], F32, name="tp")
             for q in range(4):
                 cols = slice((GATE[j] * 4 + q) * P, (GATE[j] * 4 + q + 1) * P)
-                for m in range(2):
+                for n, term in enumerate((T[("s", t, 0)], T[("s", t, 1)], bsum)):
                     nc.tensor.matmul(
-                        out=zt[:, q, :], lhsT=T[("s", t, m)][:, cols], rhs=ident[:], is_transpose=True,
-                        start=(m == 0), stop=(m == 1),
+                        out=zt[:, q, :], lhsT=term[:, cols], rhs=ident[:], is_transpose=True,
+                        start=(n == 0), stop=(n == 2),
                     )
             T[("zt", t, j)] = zt
 
         def e_act(eng, t, j):
             gt = work.tile([P, 4, P], F32, name="gate_" + j)
-            for q in range(4):
-                gb = GATE[j] * 4 + q
-                nc.scalar.activation(
-                    out=gt[:, q, :], in_=T[("zt", t, j)][:, q, :], func=(ACT.Tanh if j == "g" else ACT.Sigmoid),
-                    bias=betaT[:, gb:gb + 1], scale=1.0,
-                )
+            nc.scalar.activation(out=flat(gt), in_=flat(T[("zt", t, j)]), func=(ACT.Tanh if j == "g" else ACT.Sigmoid))
             T[("gate", t, j)] = gt
-
-        def flat(til):
-            return til[:].rearrange("p q r -> p (q r)")
 
         def e_cpt(eng, t):
             cp = ps_tp.tile([P, 4, P], F32, name="tp")
@@ -386,12 +380,12 @@ def tile_layernormlstmcell_kernel(
         def e_sth(eng, t):
             nc.sync.dma_start(out=ho_v[:, t, :], in_=T[("ht", t)][:])
 
-        tp_drains = ["pre"]
+        tp_drains = []
 
         def tp_slot(drain):
             tp_drains.append(drain)
             n = len(tp_drains) - 1
-            return tp_drains[n - TP_BUFS] if n >= TP_BUFS else "pre"
+            return tp_drains[n - TP_BUFS] if n >= TP_BUFS else "none"
 
         def unit(t, mk):
             return 2 * t + mk // 4, mk % 4
@@ -418,6 +412,8 @@ def tile_layernormlstmcell_kernel(
         STEPS = {
             "wcopy": (e_wcopy, lambda t, a: ("wcopy%d" % t, ["wq%d" % (t - 4)])),
             "wq": (e_wq, lambda t, a: ("wq%d" % t, ["wcopy%d" % t])),
+            "ldb": (e_ldb, lambda t, a: ("ldb", ["wq5"])),
+            "bsum": (e_bsum, lambda t, a: ("bsum", ["ldb"])),
             "ld": (e_ld, lambda t, a: ("ld%d" % (t // GRP), ["xt%d" % (t - GRP - 1)])),
             "xt": (e_xt, lambda t, a: ("xt%d" % t, ["ld%d" % (t // GRP), tp_slot("xcopy%d" % t)])),
             "xcopy": (e_xcopy, lambda t, a: ("xcopy%d" % t, ["xt%d" % t, "xq%d" % (t - 2)])),
@@ -430,9 +426,9 @@ def tile_layernormlstmcell_kernel(
             "red": (e_red, lambda t, a: ("red%d" % (2 * t + a), ["sq%d_3" % (2 * t + a), "r%d" % (2 * t + a - 4)])),
             "r": (e_r, lambda t, a: ("r%d" % (2 * t + a), ["red%d" % (2 * t + a), "rs%d" % (2 * t + a - 4), "uo%d" % (t - 3)])),
             "rs": (e_rs, lambda t, a: ("rs%d" % (2 * t + a), ["r%d" % (2 * t + a), "apply%d_2" % (2 * t + a)])),
-            "uo": (e_uo, lambda t, a: ("uo%d" % t, ["r%d" % (2 * t), "r%d" % (2 * t + 1), "apply%d_3" % (2 * t), "apply%d_3" % (2 * t + 1), "acto%d" % (t - 2)])),
+            "uo": (e_uo, lambda t, a: ("uo%d" % t, ["bsum", "r%d" % (2 * t), "r%d" % (2 * t + 1), "apply%d_3" % (2 * t), "apply%d_3" % (2 * t + 1), "acto%d" % (t - 2)])),
             "acto": (e_acto, lambda t, a: ("acto%d" % t, ["uo%d" % t, "h%d" % (t - 3)])),
-            "fwd": (e_fwd, lambda t, a: ("fwd%d_%s" % (t, a), ["rs%d" % (2 * t), "rs%d" % (2 * t + 1), tp_slot("act%d_%s" % (t, a))])),
+            "fwd": (e_fwd, lambda t, a: ("fwd%d_%s" % (t, a), ["bsum", "rs%d" % (2 * t), "rs%d" % (2 * t + 1), tp_slot("act%d_%s" % (t, a))])),
             "act": (e_act, lambda t, a: ("act%d_%s" % (t, a), ["fwd%d_%s" % (t, a), "%s%d" % (RING[a][0], t - RING[a][1])])),
             "cpt": (e_cpt, lambda t, a: ("cpt%d" % t, [tp_slot("p%d" % t)])),
             "cb": (e_cb, lambda t, a: ("cb%d" % t, ["p%d" % t, "q%d" % t, tp_slot("ccopy%d" % t)])),
@@ -457,7 +453,7 @@ def tile_layernormlstmcell_kernel(
                 ("wq", 3, None), ("wcopy", 6, None), ("wq", 4, None), ("wq", 5, None), ("wq", 6, None), ("wq", 7, None),
             ),
             "G": (),
-            "SP": (),
+            "SP": (("ldb", 0, None),),
         }
 
         queues = {}
@@ -472,6 +468,8 @@ def tile_layernormlstmcell_kernel(
                         continue
                     if op == "ld" and (t % GRP != 0 or t < 2 * GRP):
                         continue
+                    if op == "rs" and t == 0 and arg == 0:
+                        todo.append(("bsum", 0, None))
                     todo.append((op, t, arg))
             queues[eng] = []
             for op, t, arg in todo:

@@ -30,24 +30,24 @@ S_BUFS = 3
 
 ORDER = {
     "PE": (
-        ("main", 0, 5), ("main", 0, 6), ("fwd", -2, "f"), ("mean", 1, 0),
-        ("main", 0, 7), ("main", 1, 0), ("fwd", -2, "i"), ("xt", 2, None),
-        ("main", 1, 1), ("main", 1, 2), ("mean", 1, 1), ("cpt", -2, None),
-        ("cb", -3, None), ("fwd", -1, "g"), ("main", 1, 3), ("main", 1, 4),
+        ("fwd", -2, "g"), ("main", 0, 6), ("main", 0, 7), ("mean", 1, 0),
+        ("fwd", -2, "f"), ("fwd", -2, "i"), ("main", 1, 0), ("main", 1, 1),
+        ("main", 1, 2), ("xt", 2, None), ("main", 1, 3), ("mean", 1, 1),
+        ("main", 1, 4), ("cb", -3, None), ("cpt", -2, None), ("main", 1, 5),
     ),
     "S": (
-        ("nm", 1, 0), ("sq", 0, 7), ("sq", 1, 0), ("act", -2, "i"),
-        ("xcopy", 2, None), ("sq", 1, 1), ("sq", 1, 2), ("cstat", -4, None),
-        ("nm", 1, 1), ("ccopy", -3, None), ("sq", 1, 3), ("sq", 1, 4),
-        ("sq", 1, 5), ("acto", -3, None), ("sq", 1, 6), ("act", -1, "g"),
-        ("act", -1, "f"), ("tanh", -5, None),
+        ("nm", 1, 0), ("sq", 1, 0), ("sq", 1, 1), ("act", -2, "i"),
+        ("sq", 1, 2), ("sq", 1, 3), ("xcopy", 2, None), ("nm", 1, 1),
+        ("tanh", -6, None), ("nmc", -4, None), ("red", 0, 0), ("sq", 1, 4),
+        ("sq", 1, 5), ("cstat", -4, None), ("ccopy", -3, None), ("acto", -3, None),
+        ("sq", 1, 6), ("sq", 1, 7), ("act", -1, "g"), ("red", 0, 1),
+        ("act", -1, "f"),
     ),
     "V": (
-        ("apply", 0, 6), ("rs", -1, 1), ("LN", -5, None), ("apply", 0, 7),
-        ("h", -6, None), ("apply", 1, 0), ("red", 0, 0), ("xq", 2, None),
-        ("apply", 1, 1), ("apply", 1, 2), ("p", -2, None), ("q", -2, None),
-        ("rs", 0, 0), ("apply", 1, 3), ("red", 0, 1), ("apply", 1, 4),
-        ("apply", 1, 5), ("uo", -1, None), ("nmc", -3, None),
+        ("apply", 1, 0), ("apply", 1, 1), ("rs", -1, 1), ("apply", 1, 2),
+        ("apply", 1, 3), ("LN", -5, None), ("xq", 2, None), ("h", -6, None),
+        ("p", -2, None), ("q", -2, None), ("apply", 1, 4), ("apply", 1, 5),
+        ("uo", -1, None), ("apply", 1, 6), ("apply", 1, 7), ("rs", 0, 0),
     ),
     "G": (
         ("rc", -4, None), ("r", 0, 1), ("r", 1, 0),
@@ -95,7 +95,9 @@ def tile_layernormlstmcell_kernel(
         gamc = const.tile([P, H], BF16, name="gamc")
         betc = const.tile([P, H], BF16, name="betc")
         cin = const.tile([P, NT, H], BF16, name="cin")
-        bsum = const.tile([P, G], F32, name="bsum")
+        bt32 = const.tile([P, P], F32, name="bt32")
+        betaT = const.tile([P, G // P], F32, name="betaT")
+        bso = const.tile([P, H], F32, name="bso")
 
         T = {}
 
@@ -110,6 +112,10 @@ def tile_layernormlstmcell_kernel(
             first[nm_] = io.tile([P, GRP, K], BF16, name=nm_)
             nc.sync.dma_start(out=first[nm_][:, 0:2, :], in_=view[:, 0:2, :])
             T[(nm_, 0)] = first[nm_]
+        ba = prep.tile([16, P], BF16, name="ba", bufs=1)
+        bb = prep.tile([16, P], BF16, name="bb", bufs=1)
+        nc.scalar.dma_start(out=ba[:], in_=beta_ih.rearrange("(r c) -> r c", c=P))
+        nc.scalar.dma_start(out=bb[:], in_=beta_hh.rearrange("(r c) -> r c", c=P))
         raws = []
         for m, W in enumerate((W_ih, W_hh)):
             for hf in range(2):
@@ -125,11 +131,18 @@ def tile_layernormlstmcell_kernel(
             nc.sync.dma_start(out=first[nm_][:, 2:GRP, :], in_=view[:, 2:GRP, :])
         nc.sync.dma_start(out=cin[:], in_=c_v)
         load_group(1)
+        bo1 = prep.tile([P, H], BF16, name="bo1", bufs=1)
+        bo2 = prep.tile([P, H], BF16, name="bo2", bufs=1)
+        nc.sync.dma_start(out=bo1[:], in_=beta_ih[TCOLS:G].partition_broadcast(P))
+        nc.sync.dma_start(out=bo2[:], in_=beta_hh[TCOLS:G].partition_broadcast(P))
         nc.sync.dma_start(out=gamc[:], in_=gamma_c.partition_broadcast(P))
         nc.sync.dma_start(out=betc[:], in_=beta_c.partition_broadcast(P))
 
-        def flat(til):
-            return til[:].rearrange("p q r -> p (q r)")
+        nc.vector.memset(bt32[:], 0.0)
+        nc.vector.tensor_tensor(out=bt32[0:16, :], in0=ba[:], in1=bb[:], op=ALU.add)
+        tpb = ps_tp.tile([P, 4, P], F32, name="tp")
+        nc.tensor.transpose(tpb[:, 0, :], bt32[:], ident[:])
+        nc.vector.tensor_copy(out=betaT[:], in_=tpb[:, 0, 0:G // P])
 
         def e_wcopy(eng, u):
             grp = prep.tile([P, 512, 4], BF16, name="grp", align_bytes=64)
@@ -152,18 +165,6 @@ def tile_layernormlstmcell_kernel(
 
         def e_ld(eng, t):
             load_group(t // GRP)
-
-        def e_ldb(eng, t):
-            for n, vec in enumerate((beta_ih, beta_hh)):
-                stage = prep.tile([P, 512, 4], BF16, name="grp", align_bytes=64)
-                nc.sync.dma_start(out=stage[:].rearrange("p c t -> p (c t)"), in_=vec.partition_broadcast(P))
-                T[("bstage", n)] = stage
-
-        def e_bsum(eng, t):
-            nc.vector.tensor_tensor(
-                out=bsum[:], in0=T[("bstage", 0)][:].rearrange("p c t -> p (c t)"),
-                in1=T[("bstage", 1)][:].rearrange("p c t -> p (c t)"), op=ALU.add,
-            )
 
         def e_xt(eng, t):
             xt = ps_tp.tile([P, 4, P], F32, name="tp")
@@ -250,7 +251,10 @@ def tile_layernormlstmcell_kernel(
 
         def e_red(eng, t, m):
             ssum = small.tile([P, 1], F32, name="ssum")
-            nc.vector.tensor_reduce(out=ssum[:], in_=T[("ssq", t, m)][:], axis=AX.X, op=ALU.add)
+            if eng == "V":
+                nc.vector.tensor_reduce(out=ssum[:], in_=T[("ssq", t, m)][:], axis=AX.X, op=ALU.add)
+            else:
+                nc.scalar.activation(out=junkm[:, 0:4], in_=T[("ssq", t, m)][:], func=ACT.Identity, accum_out=ssum[:])
             T[("ssum", t, m)] = ssum
 
         def rstd(sumsq, count, nm_):
@@ -272,9 +276,11 @@ def tile_layernormlstmcell_kernel(
                 nc.scalar.activation(out=s, in_=s, func=ACT.Copy, scale=r[:])
 
         def e_uo(eng, t):
+            if t == 0:
+                nc.vector.tensor_tensor(out=bso[:], in0=bo1[:], in1=bo2[:], op=ALU.add)
             uo = work.tile([P, H], F32, name="uo")
             nc.vector.scalar_tensor_tensor(
-                out=uo[:], in0=T[("s", t, 0)][:, TCOLS:G], scalar=T[("r", t, 0)][:], in1=bsum[:, TCOLS:G], op0=ALU.mult, op1=ALU.add
+                out=uo[:], in0=T[("s", t, 0)][:, TCOLS:G], scalar=T[("r", t, 0)][:], in1=bso[:], op0=ALU.mult, op1=ALU.add
             )
             nc.vector.scalar_tensor_tensor(
                 out=uo[:], in0=T[("s", t, 1)][:, TCOLS:G], scalar=T[("r", t, 1)][:], in1=uo[:], op0=ALU.mult, op1=ALU.add
@@ -290,17 +296,25 @@ def tile_layernormlstmcell_kernel(
             zt = ps_tp.tile([P, 4, P], F32, name="tp")
             for q in range(4):
                 cols = slice((GATE[j] * 4 + q) * P, (GATE[j] * 4 + q + 1) * P)
-                for n, term in enumerate((T[("s", t, 0)], T[("s", t, 1)], bsum)):
+                for m in range(2):
                     nc.tensor.matmul(
-                        out=zt[:, q, :], lhsT=term[:, cols], rhs=ident[:], is_transpose=True,
-                        start=(n == 0), stop=(n == 2),
+                        out=zt[:, q, :], lhsT=T[("s", t, m)][:, cols], rhs=ident[:], is_transpose=True,
+                        start=(m == 0), stop=(m == 1),
                     )
             T[("zt", t, j)] = zt
 
         def e_act(eng, t, j):
             gt = work.tile([P, 4, P], F32, name="gate_" + j)
-            nc.scalar.activation(out=flat(gt), in_=flat(T[("zt", t, j)]), func=(ACT.Tanh if j == "g" else ACT.Sigmoid))
+            for q in range(4):
+                gb = GATE[j] * 4 + q
+                nc.scalar.activation(
+                    out=gt[:, q, :], in_=T[("zt", t, j)][:, q, :], func=(ACT.Tanh if j == "g" else ACT.Sigmoid),
+                    bias=betaT[:, gb:gb + 1], scale=1.0,
+                )
             T[("gate", t, j)] = gt
+
+        def flat(til):
+            return til[:].rearrange("p q r -> p (q r)")
 
         def e_cpt(eng, t):
             cp = ps_tp.tile([P, 4, P], F32, name="tp")
@@ -380,12 +394,12 @@ def tile_layernormlstmcell_kernel(
         def e_sth(eng, t):
             nc.sync.dma_start(out=ho_v[:, t, :], in_=T[("ht", t)][:])
 
-        tp_drains = []
+        tp_drains = ["pre"]
 
         def tp_slot(drain):
             tp_drains.append(drain)
             n = len(tp_drains) - 1
-            return tp_drains[n - TP_BUFS] if n >= TP_BUFS else "none"
+            return tp_drains[n - TP_BUFS] if n >= TP_BUFS else "pre"
 
         def unit(t, mk):
             return 2 * t + mk // 4, mk % 4
@@ -412,8 +426,6 @@ def tile_layernormlstmcell_kernel(
         STEPS = {
             "wcopy": (e_wcopy, lambda t, a: ("wcopy%d" % t, ["wq%d" % (t - 4)])),
             "wq": (e_wq, lambda t, a: ("wq%d" % t, ["wcopy%d" % t])),
-            "ldb": (e_ldb, lambda t, a: ("ldb", ["wq5"])),
-            "bsum": (e_bsum, lambda t, a: ("bsum", ["ldb"])),
             "ld": (e_ld, lambda t, a: ("ld%d" % (t // GRP), ["xt%d" % (t - GRP - 1)])),
             "xt": (e_xt, lambda t, a: ("xt%d" % t, ["ld%d" % (t // GRP), tp_slot("xcopy%d" % t)])),
             "xcopy": (e_xcopy, lambda t, a: ("xcopy%d" % t, ["xt%d" % t, "xq%d" % (t - 2)])),
@@ -426,9 +438,9 @@ def tile_layernormlstmcell_kernel(
             "red": (e_red, lambda t, a: ("red%d" % (2 * t + a), ["sq%d_3" % (2 * t + a), "r%d" % (2 * t + a - 4)])),
             "r": (e_r, lambda t, a: ("r%d" % (2 * t + a), ["red%d" % (2 * t + a), "rs%d" % (2 * t + a - 4), "uo%d" % (t - 3)])),
             "rs": (e_rs, lambda t, a: ("rs%d" % (2 * t + a), ["r%d" % (2 * t + a), "apply%d_2" % (2 * t + a)])),
-            "uo": (e_uo, lambda t, a: ("uo%d" % t, ["bsum", "r%d" % (2 * t), "r%d" % (2 * t + 1), "apply%d_3" % (2 * t), "apply%d_3" % (2 * t + 1), "acto%d" % (t - 2)])),
+            "uo": (e_uo, lambda t, a: ("uo%d" % t, ["r%d" % (2 * t), "r%d" % (2 * t + 1), "apply%d_3" % (2 * t), "apply%d_3" % (2 * t + 1), "acto%d" % (t - 2)])),
             "acto": (e_acto, lambda t, a: ("acto%d" % t, ["uo%d" % t, "h%d" % (t - 3)])),
-            "fwd": (e_fwd, lambda t, a: ("fwd%d_%s" % (t, a), ["bsum", "rs%d" % (2 * t), "rs%d" % (2 * t + 1), tp_slot("act%d_%s" % (t, a))])),
+            "fwd": (e_fwd, lambda t, a: ("fwd%d_%s" % (t, a), ["rs%d" % (2 * t), "rs%d" % (2 * t + 1), tp_slot("act%d_%s" % (t, a))])),
             "act": (e_act, lambda t, a: ("act%d_%s" % (t, a), ["fwd%d_%s" % (t, a), "%s%d" % (RING[a][0], t - RING[a][1])])),
             "cpt": (e_cpt, lambda t, a: ("cpt%d" % t, [tp_slot("p%d" % t)])),
             "cb": (e_cb, lambda t, a: ("cb%d" % t, ["p%d" % t, "q%d" % t, tp_slot("ccopy%d" % t)])),
@@ -446,14 +458,17 @@ def tile_layernormlstmcell_kernel(
         }
         HEAD = {
             "PE": (("xt", 0, None), ("xt", 1, None)),
-            "S": (("wcopy", 1, None), ("wcopy", 3, None), ("wcopy", 5, None), ("wcopy", 7, None)),
+            "S": (
+                ("xcopy", 0, None), ("xcopy", 1, None), ("wcopy", 1, None), ("wcopy", 3, None), ("wcopy", 5, None),
+                ("wcopy", 7, None),
+            ),
             "V": (
-                ("xcopy", 0, None), ("xcopy", 1, None), ("xq", 0, None), ("wcopy", 0, None), ("xq", 1, None),
+                ("xq", 0, None), ("wcopy", 0, None), ("xq", 1, None),
                 ("wcopy", 2, None), ("wq", 0, None), ("wq", 1, None), ("wq", 2, None), ("wcopy", 4, None),
                 ("wq", 3, None), ("wcopy", 6, None), ("wq", 4, None), ("wq", 5, None), ("wq", 6, None), ("wq", 7, None),
             ),
             "G": (),
-            "SP": (("ldb", 0, None),),
+            "SP": (),
         }
 
         queues = {}
@@ -468,8 +483,6 @@ def tile_layernormlstmcell_kernel(
                         continue
                     if op == "ld" and (t % GRP != 0 or t < 2 * GRP):
                         continue
-                    if op == "rs" and t == 0 and arg == 0:
-                        todo.append(("bsum", 0, None))
                     todo.append((op, t, arg))
             queues[eng] = []
             for op, t, arg in todo:

@@ -10,504 +10,433 @@ U8 = mybir.dt.uint8
 FP8X4 = mybir.dt.float8_e4m3fn_x4
 ALU = mybir.AluOpType
 ACT = mybir.ActivationFunctionType
-AX = mybir.AxisListType
 
 P = 128
 B = 2048
 K = 512
+HALF_K = K // 2
 H = 512
-G = 2048
+G = 4 * H
+BANK = 512
 NT = B // P
+UNITS = 2 * NT
 GRP = 4
+AHEAD = 2
+DRAIN = 8
+CHUNK = 512
+W_CHUNKS = 2 * G // CHUNK
+TCOLS = 3 * H
+FIRST_COLUMN = {"i": 0, "f": H, "g": 2 * H}
 EPS = 1e-5
 FLOPS = 2 * 2 * B * K * G
-GATE = {"i": 0, "f": 1, "g": 2}
-TCOLS = 3 * H
-ENGINES = ("PE", "S", "V", "G", "SP")
-ACC_BUFS = 4
-TP_BUFS = 3
-S_BUFS = 3
-
-ORDER = {
-    "PE": (
-        ("fwd", -2, "g"), ("main", 0, 6), ("main", 0, 7), ("mean", 1, 0),
-        ("fwd", -2, "f"), ("fwd", -2, "i"), ("main", 1, 0), ("main", 1, 1),
-        ("main", 1, 2), ("xt", 2, None), ("main", 1, 3), ("mean", 1, 1),
-        ("main", 1, 4), ("cb", -3, None), ("cpt", -2, None), ("main", 1, 5),
-    ),
-    "S": (
-        ("nm", 1, 0), ("sq", 1, 0), ("sq", 1, 1), ("act", -2, "i"),
-        ("sq", 1, 2), ("sq", 1, 3), ("xcopy", 2, None), ("nm", 1, 1),
-        ("tanh", -6, None), ("nmc", -4, None), ("red", 0, 0), ("sq", 1, 4),
-        ("sq", 1, 5), ("cstat", -4, None), ("ccopy", -3, None), ("acto", -3, None),
-        ("sq", 1, 6), ("sq", 1, 7), ("act", -1, "g"), ("red", 0, 1),
-        ("act", -1, "f"),
-    ),
-    "V": (
-        ("apply", 1, 0), ("apply", 1, 1), ("rs", -1, 1), ("apply", 1, 2),
-        ("apply", 1, 3), ("LN", -5, None), ("xq", 2, None), ("h", -6, None),
-        ("p", -2, None), ("q", -2, None), ("apply", 1, 4), ("apply", 1, 5),
-        ("uo", -1, None), ("apply", 1, 6), ("apply", 1, 7), ("rs", 0, 0),
-    ),
-    "G": (
-        ("rc", -4, None), ("r", 0, 1), ("r", 1, 0),
-    ),
-    "SP": (
-        ("ld", 6, None), ("stc", -3, None), ("sth", -6, None),
-    ),
-}
 
 
 def tile_layernormlstmcell_kernel(
     tc, x, h_prev, c_prev, W_ih, W_hh, gamma_ih, beta_ih, gamma_hh, beta_hh, gamma_c, beta_c, out_0, out_1
 ):
     nc = tc.nc
-    x_v = x.rearrange("(p t) k -> p t k", t=NT)
-    h_v = h_prev.rearrange("(p t) k -> p t k", t=NT)
-    c_v = c_prev.rearrange("(p t) k -> p t k", t=NT)
-    ho_v = out_0.rearrange("(p t) k -> p t k", t=NT)
-    co_v = out_1.rearrange("(p t) k -> p t k", t=NT)
+    x_rows = x.rearrange("(p t) k -> p t k", t=NT)
+    h_rows = h_prev.rearrange("(p t) k -> p t k", t=NT)
+    c_rows_in = c_prev.rearrange("(p t) k -> p t k", t=NT)
+    h_rows_out = out_0.rearrange("(p t) k -> p t k", t=NT)
+    c_rows_out = out_1.rearrange("(p t) k -> p t k", t=NT)
 
     with ExitStack() as ctx:
         const = ctx.enter_context(tc.tile_pool(name="const", bufs=1))
-        io = ctx.enter_context(tc.tile_pool(name="io", bufs=2))
-        xp = ctx.enter_context(tc.tile_pool(name="xp", bufs=4))
-        prep = ctx.enter_context(tc.tile_pool(name="prep", bufs=4))
+        rows_in = ctx.enter_context(tc.tile_pool(name="rows_in", bufs=2))
+        xq = ctx.enter_context(tc.tile_pool(name="xq", bufs=4))
+        wprep = ctx.enter_context(tc.tile_pool(name="wprep", bufs=4))
         work = ctx.enter_context(tc.tile_pool(name="work", bufs=2))
         small = ctx.enter_context(tc.tile_pool(name="small", bufs=4))
-        ps_acc = ctx.enter_context(tc.psum_pool(name="ps_acc", bufs=ACC_BUFS))
-        ps_tp = ctx.enter_context(tc.psum_pool(name="ps_tp", bufs=TP_BUFS))
-        ps_mean = ctx.enter_context(tc.psum_pool(name="ps_mean", bufs=1))
+        ps_prod = ctx.enter_context(tc.psum_pool(name="ps_prod", bufs=4))
+        ps_tr = ctx.enter_context(tc.psum_pool(name="ps_tr", bufs=3))
+        ps_sum = ctx.enter_context(tc.psum_pool(name="ps_sum", bufs=1))
         ctx.enter_context(tc.manual_schedule())
 
         ident = const.tile([P, P], F32, name="ident")
         make_identity(nc, ident[:])
-        neghalf = const.tile([P, 1], F32, name="neghalf")
-        nc.gpsimd.memset(neghalf[:], -0.5)
-        identb = const.tile([P, P], BF16, name="identb")
-        nc.vector.tensor_copy(out=identb[:], in_=ident[:])
-        junkm = const.tile([P, P], F32, name="junkm")
-        junkv = const.tile([P, P], F32, name="junkv")
-        junkc = const.tile([P, H], F32, name="junkc")
-        wc = [const.tile([P, G], U32, name="wc%d" % m, align_bytes=64) for m in range(2)]
-        ws = [const.tile([P, G], U8, name="ws%d" % m, align_bytes=64) for m in range(2)]
-        gam = [const.tile([P, G], BF16, name="gam%d" % m) for m in range(2)]
-        gamc = const.tile([P, H], BF16, name="gamc")
-        betc = const.tile([P, H], BF16, name="betc")
-        cin = const.tile([P, NT, H], BF16, name="cin")
-        bt32 = const.tile([P, P], F32, name="bt32")
-        betaT = const.tile([P, G // P], F32, name="betaT")
-        bso = const.tile([P, H], F32, name="bso")
+        ident_bf = const.tile([P, P], BF16, name="ident_bf")
+        nc.vector.tensor_copy(out=ident_bf[:], in_=ident[:])
+        minus_half = const.tile([P, 1], F32, name="minus_half")
+        nc.gpsimd.memset(minus_half[:], -0.5)
+        unread_narrow = const.tile([P, P], F32, name="unread_narrow")
+        unread_wide = const.tile([P, H], F32, name="unread_wide")
+        w_words = [const.tile([P, G], U32, name="w_words%d" % m, align_bytes=64) for m in range(2)]
+        w_scales = [const.tile([P, G], U8, name="w_scales%d" % m, align_bytes=64) for m in range(2)]
+        gamma = [const.tile([P, G], BF16, name="gamma%d" % m) for m in range(2)]
+        gamma_c_all = const.tile([P, H], BF16, name="gamma_c_all")
+        beta_c_all = const.tile([P, H], BF16, name="beta_c_all")
+        c_prev_all = const.tile([P, NT, H], BF16, name="c_prev_all")
+        beta_rows = const.tile([P, P], F32, name="beta_rows")
+        beta_col = const.tile([P, G // P], F32, name="beta_col")
+        beta_o = const.tile([P, H], F32, name="beta_o")
 
-        T = {}
+        live = {}
 
-        def load_group(g):
-            for nm_, view in (("xin", x_v), ("hin", h_v)):
-                til = io.tile([P, GRP, K], BF16, name=nm_)
-                nc.sync.dma_start(out=til[:], in_=view[:, g * GRP:(g + 1) * GRP, :])
-                T[(nm_, g)] = til
+        def flat(four_blocks):
+            return four_blocks[:].rearrange("p q r -> p (q r)")
 
-        first = {}
-        for nm_, view in (("xin", x_v), ("hin", h_v)):
-            first[nm_] = io.tile([P, GRP, K], BF16, name=nm_)
-            nc.sync.dma_start(out=first[nm_][:, 0:2, :], in_=view[:, 0:2, :])
-            T[(nm_, 0)] = first[nm_]
-        ba = prep.tile([16, P], BF16, name="ba", bufs=1)
-        bb = prep.tile([16, P], BF16, name="bb", bufs=1)
-        nc.scalar.dma_start(out=ba[:], in_=beta_ih.rearrange("(r c) -> r c", c=P))
-        nc.scalar.dma_start(out=bb[:], in_=beta_hh.rearrange("(r c) -> r c", c=P))
-        raws = []
+        def load_rows(group, first, last):
+            for what, view in (("x", x_rows), ("h", h_rows)):
+                if first == 0:
+                    live[(what, group)] = rows_in.tile([P, GRP, K], BF16, name=what + "_rows")
+                nc.sync.dma_start(
+                    out=live[(what, group)][:, first:last, :], in_=view[:, group * GRP + first:group * GRP + last, :]
+                )
+
+        load_rows(0, 0, AHEAD)
+        beta_a = wprep.tile([G // P, P], BF16, name="beta_a", bufs=1)
+        beta_b = wprep.tile([G // P, P], BF16, name="beta_b", bufs=1)
+        nc.scalar.dma_start(out=beta_a[:], in_=beta_ih.rearrange("(r c) -> r c", c=P))
+        nc.scalar.dma_start(out=beta_b[:], in_=beta_hh.rearrange("(r c) -> r c", c=P))
+        w_raw = []
         for m, W in enumerate((W_ih, W_hh)):
-            for hf in range(2):
-                raw = prep.tile([P, 4, 1024], BF16, name="raw")
+            for half in range(2):
+                raw = wprep.tile([P, 4, G // 2], BF16, name="raw")
                 for u in range(2):
                     nc.sync.dma_start(
                         out=raw[:, 2 * u:2 * u + 2, :],
-                        in_=W[256 * u:256 * (u + 1), hf * 1024:(hf + 1) * 1024].rearrange("(p e) c -> p e c", e=2),
+                        in_=W[HALF_K * u:HALF_K * (u + 1), half * (G // 2):(half + 1) * (G // 2)].rearrange(
+                            "(p e) c -> p e c", e=2
+                        ),
                     )
-                raws.append(raw)
-            nc.sync.dma_start(out=gam[m][:], in_=(gamma_ih, gamma_hh)[m].partition_broadcast(P))
-        for nm_, view in (("xin", x_v), ("hin", h_v)):
-            nc.sync.dma_start(out=first[nm_][:, 2:GRP, :], in_=view[:, 2:GRP, :])
-        nc.sync.dma_start(out=cin[:], in_=c_v)
-        load_group(1)
-        bo1 = prep.tile([P, H], BF16, name="bo1", bufs=1)
-        bo2 = prep.tile([P, H], BF16, name="bo2", bufs=1)
-        nc.sync.dma_start(out=bo1[:], in_=beta_ih[TCOLS:G].partition_broadcast(P))
-        nc.sync.dma_start(out=bo2[:], in_=beta_hh[TCOLS:G].partition_broadcast(P))
-        nc.sync.dma_start(out=gamc[:], in_=gamma_c.partition_broadcast(P))
-        nc.sync.dma_start(out=betc[:], in_=beta_c.partition_broadcast(P))
+                w_raw.append(raw)
+            nc.sync.dma_start(out=gamma[m][:], in_=(gamma_ih, gamma_hh)[m].partition_broadcast(P))
+        load_rows(0, AHEAD, GRP)
+        beta_o_a = wprep.tile([P, H], BF16, name="beta_o_a", bufs=1)
+        beta_o_b = wprep.tile([P, H], BF16, name="beta_o_b", bufs=1)
+        nc.sync.dma_start(out=beta_o_a[:], in_=beta_ih[TCOLS:G].partition_broadcast(P))
+        nc.sync.dma_start(out=beta_o_b[:], in_=beta_hh[TCOLS:G].partition_broadcast(P))
+        nc.sync.dma_start(out=c_prev_all[:], in_=c_rows_in)
+        load_rows(1, 0, GRP)
+        nc.sync.dma_start(out=gamma_c_all[:], in_=gamma_c.partition_broadcast(P))
+        nc.sync.dma_start(out=beta_c_all[:], in_=beta_c.partition_broadcast(P))
 
-        nc.vector.memset(bt32[:], 0.0)
-        nc.vector.tensor_tensor(out=bt32[0:16, :], in0=ba[:], in1=bb[:], op=ALU.add)
-        tpb = ps_tp.tile([P, 4, P], F32, name="tp")
-        nc.tensor.transpose(tpb[:, 0, :], bt32[:], ident[:])
-        nc.vector.tensor_copy(out=betaT[:], in_=tpb[:, 0, 0:G // P])
+        nc.vector.memset(beta_rows[:], 0.0)
+        nc.vector.tensor_tensor(out=beta_rows[0:G // P, :], in0=beta_a[:], in1=beta_b[:], op=ALU.add)
+        beta_t = ps_tr.tile([P, 4, P], F32, name="tr")
+        nc.tensor.transpose(beta_t[:, 0, :], beta_rows[:], ident[:])
+        nc.vector.tensor_copy(out=beta_col[:], in_=beta_t[:, 0, 0:G // P])
+        nc.gpsimd.tensor_tensor(out=beta_o[:], in0=beta_o_a[:], in1=beta_o_b[:], op=ALU.add)
 
-        def e_wcopy(eng, u):
-            grp = prep.tile([P, 512, 4], BF16, name="grp", align_bytes=64)
-            dst = grp[:].rearrange("p (c i) t -> p c t i", i=4)
-            src = raws[u // 2][:, :, (u % 2) * 512:(u % 2 + 1) * 512].rearrange("p t (c i) -> p c t i", i=4)
-            if eng == "V":
+        def regroup_weights(chunk):
+            grouped = wprep.tile([P, CHUNK, 4], BF16, name="grouped", align_bytes=64)
+            dst = grouped[:].rearrange("p (c i) j -> p c j i", i=4)
+            src = w_raw[chunk // 2][:, :, (chunk % 2) * CHUNK:(chunk % 2 + 1) * CHUNK].rearrange(
+                "p j (c i) -> p c j i", i=4
+            )
+            if chunk % 2 == 0:
                 nc.vector.tensor_copy(out=dst, in_=src)
             else:
                 nc.scalar.copy(out=dst, in_=src)
-            T[("grp", u)] = grp
+            live[("grouped", chunk)] = grouped
 
-        def e_wq(eng, u):
-            m = u // 4
-            c0 = (u % 4) * 512
+        def quantise_weights(chunk):
+            m = chunk // 4
+            cols = slice((chunk % 4) * CHUNK, (chunk % 4 + 1) * CHUNK)
             nc.vector.quantize_mx(
-                out=wc[m][:, c0:c0 + 512].bitcast(FP8X4),
-                scales=ws[m][:, c0:c0 + 512],
-                in_=T[("grp", u)][:].rearrange("p c t -> p (c t)"),
+                out=w_words[m][:, cols].bitcast(FP8X4),
+                scales=w_scales[m][:, cols],
+                in_=live[("grouped", chunk)][:].rearrange("p c j -> p (c j)"),
             )
 
-        def e_ld(eng, t):
-            load_group(t // GRP)
-
-        def e_xt(eng, t):
-            xt = ps_tp.tile([P, 4, P], F32, name="tp")
-            for o, nm_ in enumerate(("xin", "hin")):
-                src = T[(nm_, t // GRP)]
-                words = src[:, t % GRP, :].bitcast(F32)
+        def transpose_x(t):
+            if not 0 <= t < NT:
+                return
+            pairs_t = ps_tr.tile([P, 4, P], F32, name="tr")
+            for operand, what in enumerate(("x", "h")):
+                pairs = live[(what, t // GRP)][:, t % GRP, :].bitcast(F32)
                 for u in range(2):
-                    nc.tensor.transpose(xt[:, 2 * o + u, :], words[:, u * P:(u + 1) * P], ident[:])
-            T[("xt", t)] = xt
+                    nc.tensor.transpose(pairs_t[:, 2 * operand + u, :], pairs[:, u * P:(u + 1) * P], ident[:])
+            live[("pairs_t", t)] = pairs_t
 
-        def e_xcopy(eng, t):
-            gx = xp.tile([P, 2, P, 2], F32, name="gx", bufs=2, align_bytes=64)
-            src = T[("xt", t)][:].rearrange("p (o u) r -> p o r u", u=2)
-            if eng == "V":
-                nc.vector.tensor_copy(out=gx[:], in_=src)
-            else:
-                nc.scalar.copy(out=gx[:], in_=src)
-            T[("gx", t)] = gx
+        def copy_x(t):
+            if not 0 <= t < NT:
+                return
+            grouped = xq.tile([P, 2, P, 2], F32, name="x_grouped", bufs=2, align_bytes=64)
+            nc.scalar.copy(out=grouped[:], in_=live[("pairs_t", t)][:].rearrange("p (o u) r -> p o r u", u=2))
+            live[("x_grouped", t)] = grouped
 
-        def e_xq(eng, t):
-            xc = xp.tile([P, 2 * P], U32, name="xc", align_bytes=64)
-            xs = xp.tile([P, 2 * P], U8, name="xs", align_bytes=64)
+        def quantise_x(t):
+            if not 0 <= t < NT:
+                return
+            words = xq.tile([P, 2 * P], U32, name="x_words", align_bytes=64)
+            scales = xq.tile([P, 2 * P], U8, name="x_scales", align_bytes=64)
             nc.vector.quantize_mx(
-                out=xc[:].bitcast(FP8X4),
-                scales=xs[:],
-                in_=T[("gx", t)][:].rearrange("p o r u -> p (o r u)").bitcast(BF16),
+                out=words[:].bitcast(FP8X4),
+                scales=scales[:],
+                in_=live[("x_grouped", t)][:].rearrange("p o r u -> p (o r u)").bitcast(BF16),
             )
-            T[("xc", t)] = xc
-            T[("xs", t)] = xs
+            live[("x_words", t)] = words
+            live[("x_scales", t)] = scales
 
-        def mx(out, t, m, cols, start, stop):
+        def mx_pass(out, unit, cols, start, stop):
+            t, m = unit // 2, unit % 2
             nc.tensor.matmul_mx(
                 out=out,
-                lhsT=T[("xc", t)][:, m * P:(m + 1) * P].bitcast(FP8X4),
-                lhsT_scale=T[("xs", t)][:, m * P:(m + 1) * P],
-                rhs=wc[m][:, cols].bitcast(FP8X4),
-                rhs_scale=ws[m][:, cols],
+                lhsT=live[("x_words", t)][:, m * P:(m + 1) * P].bitcast(FP8X4),
+                lhsT_scale=live[("x_scales", t)][:, m * P:(m + 1) * P],
+                rhs=w_words[m][:, cols].bitcast(FP8X4),
+                rhs_scale=w_scales[m][:, cols],
                 start=start,
                 stop=stop,
             )
 
-        def e_mean(eng, t, m):
-            mp = ps_mean.tile([P, P], F32, name="mean_ps")
+        def row_sums(unit):
+            if not 0 <= unit < UNITS:
+                return
+            sums = ps_sum.tile([P, P], F32, name="sums")
             for j in range(G // P):
-                mx(mp[:], t, m, slice(j * P, (j + 1) * P), j == 0, j == G // P - 1)
-            T[("mean", t, m)] = mp
+                mx_pass(sums[:], unit, slice(j * P, (j + 1) * P), j == 0, j == G // P - 1)
+            live[("sums", unit)] = sums
 
-        def e_nm(eng, t, m):
-            nm = small.tile([P, 1], F32, name="nm")
-            if eng == "V":
-                nc.vector.tensor_scalar(
-                    out=junkv[:], in0=T[("mean", t, m)][:], scalar1=-1.0 / G, scalar2=0.0, op0=ALU.mult, op1=ALU.add,
-                    accum_out=nm[:],
-                )
-            else:
-                nc.scalar.activation(
-                    out=junkm[:], in_=T[("mean", t, m)][:], func=ACT.Identity, scale=-1.0 / G, accum_out=nm[:]
-                )
-            T[("nm", t, m)] = nm
-
-        def e_main(eng, t, mk):
-            m, k = mk // 4, mk % 4
-            acc = ps_acc.tile([P, 512], F32, name="acc")
-            mx(acc[:], t, m, slice(k * 512, (k + 1) * 512), True, True)
-            T[("acc", t, mk)] = acc
-
-        def e_sq(eng, t, mk):
-            m, k = mk // 4, mk % 4
-            if k == 0:
-                T[("ssq", t, m)] = small.tile([P, 4], F32, name="ssq")
-                T[("s", t, m)] = work.tile([P, G], F32, name="s%d" % m, bufs=S_BUFS)
+        def negative_mean(unit):
+            if not 0 <= unit < UNITS:
+                return
+            neg_mean = small.tile([P, 1], F32, name="neg_mean")
             nc.scalar.activation(
-                out=T[("s", t, m)][:, k * 512:(k + 1) * 512], in_=T[("acc", t, mk)][:], func=ACT.Square,
-                bias=T[("nm", t, m)][:], scale=1.0, accum_out=T[("ssq", t, m)][:, k:k + 1],
+                out=unread_narrow[:], in_=live[("sums", unit)][:], func=ACT.Identity, scale=-1.0 / G,
+                accum_out=neg_mean[:],
+            )
+            live[("neg_mean", unit)] = neg_mean
+
+        def product_bank(unit, k):
+            if not 0 <= unit < UNITS:
+                return
+            bank = ps_prod.tile([P, BANK], F32, name="bank")
+            mx_pass(bank[:], unit, slice(k * BANK, (k + 1) * BANK), True, True)
+            live[("bank", unit, k)] = bank
+
+        def square_sum(unit, k):
+            if k == 0:
+                live[("squares", unit)] = small.tile([P, 4], F32, name="squares")
+                live[("s", unit)] = work.tile([P, G], F32, name="s%d" % (unit % 2), bufs=3)
+            nc.scalar.activation(
+                out=live[("s", unit)][:, k * BANK:(k + 1) * BANK], in_=live[("bank", unit, k)][:], func=ACT.Square,
+                bias=live[("neg_mean", unit)][:], scale=1.0, accum_out=live[("squares", unit)][:, k:k + 1],
             )
 
-        def e_apply(eng, t, mk):
-            m, k = mk // 4, mk % 4
-            cols = slice(k * 512, (k + 1) * 512)
+        def centre_and_gain(unit, k):
+            cols = slice(k * BANK, (k + 1) * BANK)
             nc.vector.scalar_tensor_tensor(
-                out=T[("s", t, m)][:, cols], in0=T[("acc", t, mk)][:], scalar=T[("nm", t, m)][:],
-                in1=gam[m][:, cols], op0=ALU.add, op1=ALU.mult,
+                out=live[("s", unit)][:, cols], in0=live[("bank", unit, k)][:], scalar=live[("neg_mean", unit)][:],
+                in1=gamma[unit % 2][:, cols], op0=ALU.add, op1=ALU.mult,
             )
 
-        def e_red(eng, t, m):
-            ssum = small.tile([P, 1], F32, name="ssum")
-            if eng == "V":
-                nc.vector.tensor_reduce(out=ssum[:], in_=T[("ssq", t, m)][:], axis=AX.X, op=ALU.add)
-            else:
-                nc.scalar.activation(out=junkm[:, 0:4], in_=T[("ssq", t, m)][:], func=ACT.Identity, accum_out=ssum[:])
-            T[("ssum", t, m)] = ssum
-
-        def rstd(sumsq, count, nm_):
-            var = small.tile([P, 1], F32, name="var" + nm_)
-            nc.gpsimd.tensor_scalar(out=var[:], in0=sumsq[:], scalar1=1.0 / count, scalar2=EPS, op0=ALU.mult, op1=ALU.add)
-            r = small.tile([P, 1], F32, name="r" + nm_, bufs=6)
-            nc.gpsimd.tensor_tensor(out=r[:], in0=var[:], in1=neghalf[:], op=ALU.pow)
+        def inverse_std(sum_of_squares, count, name):
+            var = small.tile([P, 1], F32, name="var_" + name)
+            nc.gpsimd.tensor_scalar(
+                out=var[:], in0=sum_of_squares[:], scalar1=1.0 / count, scalar2=EPS, op0=ALU.mult, op1=ALU.add
+            )
+            r = small.tile([P, 1], F32, name="r_" + name)
+            nc.gpsimd.tensor_tensor(out=r[:], in0=var[:], in1=minus_half[:], op=ALU.pow)
             return r
 
-        def e_r(eng, t, m):
-            T[("r", t, m)] = rstd(T[("ssum", t, m)], G, "g")
-
-        def e_rs(eng, t, m):
-            s = T[("s", t, m)][:, 0:TCOLS]
-            r = T[("r", t, m)]
-            if eng == "V":
-                nc.vector.tensor_scalar(out=s, in0=s, scalar1=r[:], scalar2=None, op0=ALU.mult)
-            else:
-                nc.scalar.activation(out=s, in_=s, func=ACT.Copy, scale=r[:])
-
-        def e_uo(eng, t):
-            if t == 0:
-                nc.vector.tensor_tensor(out=bso[:], in0=bo1[:], in1=bo2[:], op=ALU.add)
-            uo = work.tile([P, H], F32, name="uo")
-            nc.vector.scalar_tensor_tensor(
-                out=uo[:], in0=T[("s", t, 0)][:, TCOLS:G], scalar=T[("r", t, 0)][:], in1=bso[:], op0=ALU.mult, op1=ALU.add
-            )
-            nc.vector.scalar_tensor_tensor(
-                out=uo[:], in0=T[("s", t, 1)][:, TCOLS:G], scalar=T[("r", t, 1)][:], in1=uo[:], op0=ALU.mult, op1=ALU.add
-            )
-            T[("uo", t)] = uo
-
-        def e_acto(eng, t):
-            og = work.tile([P, H], F32, name="og", bufs=3)
-            nc.scalar.activation(out=og[:], in_=T[("uo", t)][:], func=ACT.Sigmoid)
-            T[("og", t)] = og
-
-        def e_fwd(eng, t, j):
-            zt = ps_tp.tile([P, 4, P], F32, name="tp")
-            for q in range(4):
-                cols = slice((GATE[j] * 4 + q) * P, (GATE[j] * 4 + q + 1) * P)
-                for m in range(2):
-                    nc.tensor.matmul(
-                        out=zt[:, q, :], lhsT=T[("s", t, m)][:, cols], rhs=ident[:], is_transpose=True,
-                        start=(m == 0), stop=(m == 1),
-                    )
-            T[("zt", t, j)] = zt
-
-        def e_act(eng, t, j):
-            gt = work.tile([P, 4, P], F32, name="gate_" + j)
-            for q in range(4):
-                gb = GATE[j] * 4 + q
-                nc.scalar.activation(
-                    out=gt[:, q, :], in_=T[("zt", t, j)][:, q, :], func=(ACT.Tanh if j == "g" else ACT.Sigmoid),
-                    bias=betaT[:, gb:gb + 1], scale=1.0,
-                )
-            T[("gate", t, j)] = gt
-
-        def flat(til):
-            return til[:].rearrange("p q r -> p (q r)")
-
-        def e_cpt(eng, t):
-            cp = ps_tp.tile([P, 4, P], F32, name="tp")
-            view = flat(cp).bitcast(BF16)
-            for q in range(4):
-                nc.tensor.transpose(view[:, q * P:(q + 1) * P], cin[:, t, q * P:(q + 1) * P], identb[:])
-            T[("cpt", t)] = view[:, 0:H]
-
-        def e_q(eng, t):
-            qT = work.tile([P, 4, P], F32, name="qT")
-            nc.vector.tensor_tensor(out=flat(qT), in0=flat(T[("gate", t, "i")]), in1=flat(T[("gate", t, "g")]), op=ALU.mult)
-            T[("qT", t)] = qT
-
-        def e_p(eng, t):
-            pT = work.tile([P, 4, P], F32, name="pT")
-            nc.vector.tensor_tensor(out=flat(pT), in0=flat(T[("gate", t, "f")]), in1=T[("cpt", t)], op=ALU.mult)
-            T[("pT", t)] = pT
-
-        def e_cb(eng, t):
-            cb = ps_tp.tile([P, 4, P], F32, name="tp")
-            for q in range(4):
-                for n, key in enumerate(("pT", "qT")):
-                    nc.tensor.matmul(
-                        out=cb[:, q, :], lhsT=T[(key, t)][:, q, :], rhs=ident[:], is_transpose=True,
-                        start=(n == 0), stop=(n == 1),
-                    )
-            T[("cb", t)] = cb
-
-        def e_ccopy(eng, t):
-            ct = work.tile([P, H], F32, name="ct", bufs=3)
-            csum = small.tile([P, 1], F32, name="csum")
-            nc.scalar.activation(out=ct[:], in_=flat(T[("cb", t)]), func=ACT.Identity, accum_out=csum[:])
-            T[("ct", t)] = ct
-            T[("csum", t)] = csum
-
-        def e_nmc(eng, t):
-            nmc = small.tile([P, 1], F32, name="nmc")
-            if eng == "V":
-                nc.vector.tensor_scalar(out=nmc[:], in0=T[("csum", t)][:], scalar1=-1.0 / H, scalar2=None, op0=ALU.mult)
-            else:
-                nc.scalar.mul(out=nmc[:], in_=T[("csum", t)][:], mul=-1.0 / H)
-            T[("nmc", t)] = nmc
-
-        def e_cstat(eng, t):
-            ssqc = small.tile([P, 1], F32, name="ssqc")
+        def unit_inverse_std(unit):
+            total = small.tile([P, 1], F32, name="total")
             nc.scalar.activation(
-                out=junkc[:], in_=T[("ct", t)][:], func=ACT.Square, bias=T[("nmc", t)][:], scale=1.0, accum_out=ssqc[:]
+                out=unread_narrow[:, 0:4], in_=live[("squares", unit)][:], func=ACT.Identity, accum_out=total[:]
             )
-            T[("ssqc", t)] = ssqc
+            live[("r", unit)] = inverse_std(total, G, "gates")
 
-        def e_rc(eng, t):
-            T[("rc", t)] = rstd(T[("ssqc", t)], H, "c")
+        def scale_rows(t, m):
+            if not 0 <= t < NT:
+                return
+            s = live[("s", 2 * t + m)][:, 0:TCOLS]
+            nc.vector.tensor_scalar(out=s, in0=s, scalar1=live[("r", 2 * t + m)][:], scalar2=None, op0=ALU.mult)
 
-        def e_LN(eng, t):
-            sc = work.tile([P, H], F32, name="sc")
+        def o_gate_sum(t):
+            if not 0 <= t < NT:
+                return
+            o_sum = work.tile([P, H], F32, name="o_sum")
             nc.vector.scalar_tensor_tensor(
-                out=sc[:], in0=T[("ct", t)][:], scalar=T[("nmc", t)][:], in1=gamc[:], op0=ALU.add, op1=ALU.mult
+                out=o_sum[:], in0=live[("s", 2 * t)][:, TCOLS:G], scalar=live[("r", 2 * t)][:], in1=beta_o[:],
+                op0=ALU.mult, op1=ALU.add,
             )
             nc.vector.scalar_tensor_tensor(
-                out=sc[:], in0=sc[:], scalar=T[("rc", t)][:], in1=betc[:], op0=ALU.mult, op1=ALU.add
+                out=o_sum[:], in0=live[("s", 2 * t + 1)][:, TCOLS:G], scalar=live[("r", 2 * t + 1)][:], in1=o_sum[:],
+                op0=ALU.mult, op1=ALU.add,
             )
-            T[("sc", t)] = sc
+            live[("o_sum", t)] = o_sum
 
-        def e_tanh(eng, t):
-            th = work.tile([P, H], F32, name="th")
-            nc.scalar.activation(out=th[:], in_=T[("sc", t)][:], func=ACT.Tanh)
-            T[("th", t)] = th
+        def o_gate(t):
+            if not 0 <= t < NT:
+                return
+            o = work.tile([P, H], F32, name="o", bufs=3)
+            nc.scalar.activation(out=o[:], in_=live[("o_sum", t)][:], func=ACT.Sigmoid)
+            live[("o", t)] = o
 
-        def e_h(eng, t):
-            ht = work.tile([P, H], F32, name="ht", bufs=3)
-            nc.vector.tensor_tensor(out=ht[:], in0=T[("og", t)][:], in1=T[("th", t)][:], op=ALU.mult)
-            T[("ht", t)] = ht
+        def add_transposed(terms):
+            summed = ps_tr.tile([P, 4, P], F32, name="tr")
+            for q in range(4):
+                for second, term in enumerate(terms):
+                    nc.tensor.matmul(
+                        out=summed[:, q, :], lhsT=term[:, q * P:(q + 1) * P], rhs=ident[:], is_transpose=True,
+                        start=(second == 0), stop=(second == 1),
+                    )
+            return summed
 
-        def e_stc(eng, t):
-            nc.sync.dma_start(out=co_v[:, t, :], in_=T[("ct", t)][:])
+        def gate_sum_t(t, gate):
+            if not 0 <= t < NT:
+                return
+            cols = slice(FIRST_COLUMN[gate], FIRST_COLUMN[gate] + H)
+            live[("gate_sum_t", t, gate)] = add_transposed([live[("s", 2 * t + m)][:, cols] for m in range(2)])
 
-        def e_sth(eng, t):
-            nc.sync.dma_start(out=ho_v[:, t, :], in_=T[("ht", t)][:])
+        def gate_t(t, gate):
+            if not 0 <= t < NT:
+                return
+            values = work.tile([P, 4, P], F32, name="gate_" + gate)
+            for q in range(4):
+                block = FIRST_COLUMN[gate] // P + q
+                nc.scalar.activation(
+                    out=values[:, q, :], in_=live[("gate_sum_t", t, gate)][:, q, :],
+                    func=(ACT.Tanh if gate == "g" else ACT.Sigmoid), bias=beta_col[:, block:block + 1], scale=1.0,
+                )
+            live[("gate_t", t, gate)] = values
 
-        tp_drains = ["pre"]
+        def c_prev_t(t):
+            if not 0 <= t < NT:
+                return
+            half_used = ps_tr.tile([P, 4, P], F32, name="tr")
+            as_bf16 = flat(half_used).bitcast(BF16)
+            for q in range(4):
+                nc.tensor.transpose(as_bf16[:, q * P:(q + 1) * P], c_prev_all[:, t, q * P:(q + 1) * P], ident_bf[:])
+            live[("c_prev_t", t)] = as_bf16[:, 0:H]
 
-        def tp_slot(drain):
-            tp_drains.append(drain)
-            n = len(tp_drains) - 1
-            return tp_drains[n - TP_BUFS] if n >= TP_BUFS else "pre"
+        def forget_t(t):
+            if not 0 <= t < NT:
+                return
+            kept = work.tile([P, 4, P], F32, name="kept")
+            nc.vector.tensor_tensor(
+                out=flat(kept), in0=flat(live[("gate_t", t, "f")]), in1=live[("c_prev_t", t)], op=ALU.mult
+            )
+            live[("kept", t)] = kept
 
-        def unit(t, mk):
-            return 2 * t + mk // 4, mk % 4
+        def input_t(t):
+            if not 0 <= t < NT:
+                return
+            new = work.tile([P, 4, P], F32, name="new")
+            nc.vector.tensor_tensor(
+                out=flat(new), in0=flat(live[("gate_t", t, "i")]), in1=flat(live[("gate_t", t, "g")]), op=ALU.mult
+            )
+            live[("new", t)] = new
 
-        def d_main(t, mk):
-            u, k = unit(t, mk)
-            n = 4 * u + k - ACC_BUFS
-            return "main%d_%d" % (u, k), ["xq%d" % t, "wq%d" % mk, "apply%d_%d" % (n // 4, n % 4)]
+        def c_rows(t):
+            if not 0 <= t < NT:
+                return
+            live[("c_psum", t)] = add_transposed([flat(live[("kept", t)]), flat(live[("new", t)])])
 
-        def d_sq(t, mk):
-            u, k = unit(t, mk)
-            deps = ["main%d_%d" % (u, k), "nm%d" % u]
-            if k == 0:
-                deps.extend(["fwd%d_%s" % (t - S_BUFS, j) for j in GATE])
-                deps.append("uo%d" % (t - S_BUFS))
-                deps.append("red%d" % (u - 4))
-            return "sq%d_%d" % (u, k), deps
+        def c_out(t):
+            if not 0 <= t < NT:
+                return
+            c = work.tile([P, H], F32, name="c", bufs=3)
+            c_sum = small.tile([P, 1], F32, name="c_sum")
+            nc.scalar.activation(out=c[:], in_=flat(live[("c_psum", t)]), func=ACT.Identity, accum_out=c_sum[:])
+            nc.sync.dma_start(out=c_rows_out[:, t, :], in_=c[:])
+            c_neg_mean = small.tile([P, 1], F32, name="c_neg_mean")
+            nc.scalar.mul(out=c_neg_mean[:], in_=c_sum[:], mul=-1.0 / H)
+            live[("c", t)] = c
+            live[("c_neg_mean", t)] = c_neg_mean
 
-        def d_apply(t, mk):
-            u, k = unit(t, mk)
-            return "apply%d_%d" % (u, k), ["sq%d_%d" % (u, k)]
+        def c_inverse_std(t):
+            if not 0 <= t < NT:
+                return
+            c_squares = small.tile([P, 1], F32, name="c_squares")
+            nc.scalar.activation(
+                out=unread_wide[:], in_=live[("c", t)][:], func=ACT.Square, bias=live[("c_neg_mean", t)][:], scale=1.0,
+                accum_out=c_squares[:],
+            )
+            live[("c_r", t)] = inverse_std(c_squares, H, "c")
 
-        RING = {"f": ("p", 2), "i": ("q", 2), "g": ("q", 2)}
-        STEPS = {
-            "wcopy": (e_wcopy, lambda t, a: ("wcopy%d" % t, ["wq%d" % (t - 4)])),
-            "wq": (e_wq, lambda t, a: ("wq%d" % t, ["wcopy%d" % t])),
-            "ld": (e_ld, lambda t, a: ("ld%d" % (t // GRP), ["xt%d" % (t - GRP - 1)])),
-            "xt": (e_xt, lambda t, a: ("xt%d" % t, ["ld%d" % (t // GRP), tp_slot("xcopy%d" % t)])),
-            "xcopy": (e_xcopy, lambda t, a: ("xcopy%d" % t, ["xt%d" % t, "xq%d" % (t - 2)])),
-            "xq": (e_xq, lambda t, a: ("xq%d" % t, ["xcopy%d" % t, "main%d_3" % (2 * (t - 4) + 1)])),
-            "mean": (e_mean, lambda t, a: ("mean%d" % (2 * t + a), ["xq%d" % t, "wq%d" % (4 * a + 3), "nm%d" % (2 * t + a - 1)])),
-            "nm": (e_nm, lambda t, a: ("nm%d" % (2 * t + a), ["mean%d" % (2 * t + a), "apply%d_3" % (2 * t + a - 4)])),
-            "main": (e_main, d_main),
-            "sq": (e_sq, d_sq),
-            "apply": (e_apply, d_apply),
-            "red": (e_red, lambda t, a: ("red%d" % (2 * t + a), ["sq%d_3" % (2 * t + a), "r%d" % (2 * t + a - 4)])),
-            "r": (e_r, lambda t, a: ("r%d" % (2 * t + a), ["red%d" % (2 * t + a), "rs%d" % (2 * t + a - 4), "uo%d" % (t - 3)])),
-            "rs": (e_rs, lambda t, a: ("rs%d" % (2 * t + a), ["r%d" % (2 * t + a), "apply%d_2" % (2 * t + a)])),
-            "uo": (e_uo, lambda t, a: ("uo%d" % t, ["r%d" % (2 * t), "r%d" % (2 * t + 1), "apply%d_3" % (2 * t), "apply%d_3" % (2 * t + 1), "acto%d" % (t - 2)])),
-            "acto": (e_acto, lambda t, a: ("acto%d" % t, ["uo%d" % t, "h%d" % (t - 3)])),
-            "fwd": (e_fwd, lambda t, a: ("fwd%d_%s" % (t, a), ["rs%d" % (2 * t), "rs%d" % (2 * t + 1), tp_slot("act%d_%s" % (t, a))])),
-            "act": (e_act, lambda t, a: ("act%d_%s" % (t, a), ["fwd%d_%s" % (t, a), "%s%d" % (RING[a][0], t - RING[a][1])])),
-            "cpt": (e_cpt, lambda t, a: ("cpt%d" % t, [tp_slot("p%d" % t)])),
-            "cb": (e_cb, lambda t, a: ("cb%d" % t, ["p%d" % t, "q%d" % t, tp_slot("ccopy%d" % t)])),
-            "q": (e_q, lambda t, a: ("q%d" % t, ["act%d_i" % t, "act%d_g" % t, "cb%d" % (t - 2)])),
-            "p": (e_p, lambda t, a: ("p%d" % t, ["act%d_f" % t, "cpt%d" % t, "cb%d" % (t - 2)])),
-            "ccopy": (e_ccopy, lambda t, a: ("ccopy%d" % t, ["cb%d" % t, "LN%d" % (t - 3), "cstat%d" % (t - 3), "stc%d" % (t - 3)])),
-            "nmc": (e_nmc, lambda t, a: ("nmc%d" % t, ["ccopy%d" % t, "LN%d" % (t - 4)])),
-            "cstat": (e_cstat, lambda t, a: ("cstat%d" % t, ["nmc%d" % t, "rc%d" % (t - 4)])),
-            "rc": (e_rc, lambda t, a: ("rc%d" % t, ["cstat%d" % t, "LN%d" % (t - 4)])),
-            "LN": (e_LN, lambda t, a: ("LN%d" % t, ["rc%d" % t, "tanh%d" % (t - 2)])),
-            "tanh": (e_tanh, lambda t, a: ("tanh%d" % t, ["LN%d" % t, "h%d" % (t - 2)])),
-            "h": (e_h, lambda t, a: ("h%d" % t, ["acto%d" % t, "tanh%d" % t, "sth%d" % (t - 3)])),
-            "stc": (e_stc, lambda t, a: ("stc%d" % t, ["ccopy%d" % t])),
-            "sth": (e_sth, lambda t, a: ("sth%d" % t, ["h%d" % t])),
-        }
-        HEAD = {
-            "PE": (("xt", 0, None), ("xt", 1, None)),
-            "S": (
-                ("xcopy", 0, None), ("xcopy", 1, None), ("wcopy", 1, None), ("wcopy", 3, None), ("wcopy", 5, None),
-                ("wcopy", 7, None),
-            ),
-            "V": (
-                ("xq", 0, None), ("wcopy", 0, None), ("xq", 1, None),
-                ("wcopy", 2, None), ("wq", 0, None), ("wq", 1, None), ("wq", 2, None), ("wcopy", 4, None),
-                ("wq", 3, None), ("wcopy", 6, None), ("wq", 4, None), ("wq", 5, None), ("wq", 6, None), ("wq", 7, None),
-            ),
-            "G": (),
-            "SP": (),
-        }
+        def c_norm(t):
+            if not 0 <= t < NT:
+                return
+            normed = work.tile([P, H], F32, name="normed")
+            nc.vector.scalar_tensor_tensor(
+                out=normed[:], in0=live[("c", t)][:], scalar=live[("c_neg_mean", t)][:], in1=gamma_c_all[:],
+                op0=ALU.add, op1=ALU.mult,
+            )
+            nc.vector.scalar_tensor_tensor(
+                out=normed[:], in0=normed[:], scalar=live[("c_r", t)][:], in1=beta_c_all[:], op0=ALU.mult, op1=ALU.add
+            )
+            live[("normed", t)] = normed
 
-        queues = {}
-        for eng in ENGINES:
-            todo = list(HEAD[eng])
-            for a in range(-3, NT + 9):
-                for op, off, arg in ORDER[eng]:
-                    t = a + off
-                    if t < 0 or t >= NT:
-                        continue
-                    if op in ("xt", "xcopy", "xq") and t < 2:
-                        continue
-                    if op == "ld" and (t % GRP != 0 or t < 2 * GRP):
-                        continue
-                    todo.append((op, t, arg))
-            queues[eng] = []
-            for op, t, arg in todo:
-                name, deps = STEPS[op][1](t, arg)
-                queues[eng].append((name, deps, op, t, arg))
+        def c_tanh(t):
+            if not 0 <= t < NT:
+                return
+            squashed = work.tile([P, H], F32, name="squashed")
+            nc.scalar.activation(out=squashed[:], in_=live[("normed", t)][:], func=ACT.Tanh)
+            live[("squashed", t)] = squashed
 
-        names = set()
-        for eng in ENGINES:
-            for item in queues[eng]:
-                names.add(item[0])
-        done = set()
-        at = {eng: 0 for eng in ENGINES}
-        left = len(names)
-        while left > 0:
-            before = left
-            for eng in ENGINES:
-                while at[eng] < len(queues[eng]):
-                    name, deps, op, t, arg = queues[eng][at[eng]]
-                    if any(d in names and d not in done for d in deps):
-                        break
-                    if arg is None:
-                        STEPS[op][0](eng, t)
-                    else:
-                        STEPS[op][0](eng, t, arg)
-                    done.add(name)
-                    at[eng] += 1
-                    left -= 1
-            assert left < before, "the per-engine orders wait for each other"
+        def h_out(t):
+            if not 0 <= t < NT:
+                return
+            h = work.tile([P, H], F32, name="h", bufs=3)
+            nc.vector.tensor_tensor(out=h[:], in0=live[("o", t)][:], in1=live[("squashed", t)][:], op=ALU.mult)
+            nc.sync.dma_start(out=h_rows_out[:, t, :], in_=h[:])
+
+        for t in range(AHEAD):
+            transpose_x(t)
+            copy_x(t)
+        for t in range(AHEAD):
+            quantise_x(t)
+        for chunk in range(W_CHUNKS):
+            regroup_weights(chunk)
+            if chunk >= 2:
+                quantise_weights(chunk - 2)
+        quantise_weights(W_CHUNKS - 2)
+        quantise_weights(W_CHUNKS - 1)
+        product_bank(0, 0)
+        row_sums(0)
+        product_bank(0, 1)
+        product_bank(0, 2)
+        negative_mean(0)
+
+        for unit in range(UNITS + DRAIN):
+            t, m = unit // 2, unit % 2
+            busy = unit < UNITS
+            if m == 0:
+                if t % GRP == 0 and 0 < t < NT - GRP:
+                    load_rows(t // GRP + 1, 0, GRP)
+                c_prev_t(t - 2)
+                transpose_x(t + AHEAD)
+                c_rows(t - 3)
+            else:
+                for gate in ("f", "i", "g"):
+                    gate_sum_t(t - 1, gate)
+            product_bank(unit, 3)
+            for k in range(4):
+                if busy:
+                    square_sum(unit, k)
+                    centre_and_gain(unit, k)
+                if (m, k) == (0, 0):
+                    o_gate(t - 2)
+                    forget_t(t - 2)
+                elif (m, k) == (0, 1):
+                    copy_x(t + AHEAD)
+                    scale_rows(t - 1, 1)
+                elif (m, k) == (0, 2):
+                    c_out(t - 3)
+                    o_gate_sum(t - 1)
+                elif (m, k) == (0, 3):
+                    c_inverse_std(t - 3)
+                    input_t(t - 2)
+                elif (m, k) == (1, 0):
+                    c_tanh(t - 4)
+                    scale_rows(t, 0)
+                elif (m, k) == (1, 1):
+                    gate_t(t - 1, "f")
+                    c_norm(t - 3)
+                elif (m, k) == (1, 2):
+                    gate_t(t - 1, "i")
+                    h_out(t - 4)
+                else:
+                    gate_t(t - 1, "g")
+                    quantise_x(t + AHEAD)
+                if k < 3:
+                    product_bank(unit + 1, k)
+                if k == 0:
+                    row_sums(unit + 1)
+            negative_mean(unit + 1)
+            if busy:
+                unit_inverse_std(unit)

from contextlib import ExitStack

import concourse.mybir as mybir
from concourse.masks import make_identity

F32 = mybir.dt.float32
BF16 = mybir.dt.bfloat16
U32 = mybir.dt.uint32
U8 = mybir.dt.uint8
FP8X4 = mybir.dt.float8_e4m3fn_x4
ALU = mybir.AluOpType
ACT = mybir.ActivationFunctionType

P = 128
B = 2048
K = 512
HALF_K = K // 2
H = 512
G = 4 * H
BANK = 512
NT = B // P
UNITS = 2 * NT
GRP = 4
AHEAD = 2
DRAIN = 8
CHUNK = 512
W_CHUNKS = 2 * G // CHUNK
TCOLS = 3 * H
FIRST_COLUMN = {"i": 0, "f": H, "g": 2 * H}
EPS = 1e-5
FLOPS = 2 * 2 * B * K * G


def tile_layernormlstmcell_kernel(
    tc, x, h_prev, c_prev, W_ih, W_hh, gamma_ih, beta_ih, gamma_hh, beta_hh, gamma_c, beta_c, out_0, out_1
):
    nc = tc.nc
    x_rows = x.rearrange("(p t) k -> p t k", t=NT)
    h_rows = h_prev.rearrange("(p t) k -> p t k", t=NT)
    c_rows_in = c_prev.rearrange("(p t) k -> p t k", t=NT)
    h_rows_out = out_0.rearrange("(p t) k -> p t k", t=NT)
    c_rows_out = out_1.rearrange("(p t) k -> p t k", t=NT)

    with ExitStack() as ctx:
        const = ctx.enter_context(tc.tile_pool(name="const", bufs=1))
        rows_in = ctx.enter_context(tc.tile_pool(name="rows_in", bufs=2))
        xq = ctx.enter_context(tc.tile_pool(name="xq", bufs=4))
        wprep = ctx.enter_context(tc.tile_pool(name="wprep", bufs=4))
        work = ctx.enter_context(tc.tile_pool(name="work", bufs=2))
        small = ctx.enter_context(tc.tile_pool(name="small", bufs=4))
        ps_prod = ctx.enter_context(tc.psum_pool(name="ps_prod", bufs=4))
        ps_tr = ctx.enter_context(tc.psum_pool(name="ps_tr", bufs=3))
        ps_sum = ctx.enter_context(tc.psum_pool(name="ps_sum", bufs=1))
        ctx.enter_context(tc.manual_schedule())

        ident = const.tile([P, P], F32, name="ident")
        make_identity(nc, ident[:])
        ident_bf = const.tile([P, P], BF16, name="ident_bf")
        nc.vector.tensor_copy(out=ident_bf[:], in_=ident[:])
        minus_half = const.tile([P, 1], F32, name="minus_half")
        nc.gpsimd.memset(minus_half[:], -0.5)
        unread_narrow = const.tile([P, P], F32, name="unread_narrow")
        unread_wide = const.tile([P, H], F32, name="unread_wide")
        w_words = [const.tile([P, G], U32, name="w_words%d" % m, align_bytes=64) for m in range(2)]
        w_scales = [const.tile([P, G], U8, name="w_scales%d" % m, align_bytes=64) for m in range(2)]
        gamma = [const.tile([P, G], BF16, name="gamma%d" % m) for m in range(2)]
        gamma_c_all = const.tile([P, H], BF16, name="gamma_c_all")
        beta_c_all = const.tile([P, H], BF16, name="beta_c_all")
        c_prev_all = const.tile([P, NT, H], BF16, name="c_prev_all")
        beta_rows = const.tile([P, P], F32, name="beta_rows")
        beta_col = const.tile([P, G // P], F32, name="beta_col")
        beta_o = const.tile([P, H], F32, name="beta_o")

        live = {}

        def flat(four_blocks):
            return four_blocks[:].rearrange("p q r -> p (q r)")

        def load_rows(group, first, last):
            for what, view in (("x", x_rows), ("h", h_rows)):
                if first == 0:
                    live[(what, group)] = rows_in.tile([P, GRP, K], BF16, name=what + "_rows")
                nc.sync.dma_start(
                    out=live[(what, group)][:, first:last, :], in_=view[:, group * GRP + first:group * GRP + last, :]
                )

        load_rows(0, 0, AHEAD)
        beta_a = wprep.tile([G // P, P], BF16, name="beta_a", bufs=1)
        beta_b = wprep.tile([G // P, P], BF16, name="beta_b", bufs=1)
        nc.scalar.dma_start(out=beta_a[:], in_=beta_ih.rearrange("(r c) -> r c", c=P))
        nc.scalar.dma_start(out=beta_b[:], in_=beta_hh.rearrange("(r c) -> r c", c=P))
        w_raw = []
        for m, W in enumerate((W_ih, W_hh)):
            for half in range(2):
                raw = wprep.tile([P, 4, G // 2], BF16, name="raw")
                for u in range(2):
                    nc.sync.dma_start(
                        out=raw[:, 2 * u:2 * u + 2, :],
                        in_=W[HALF_K * u:HALF_K * (u + 1), half * (G // 2):(half + 1) * (G // 2)].rearrange(
                            "(p e) c -> p e c", e=2
                        ),
                    )
                w_raw.append(raw)
            nc.sync.dma_start(out=gamma[m][:], in_=(gamma_ih, gamma_hh)[m].partition_broadcast(P))
        load_rows(0, AHEAD, GRP)
        beta_o_a = wprep.tile([P, H], BF16, name="beta_o_a", bufs=1)
        beta_o_b = wprep.tile([P, H], BF16, name="beta_o_b", bufs=1)
        nc.sync.dma_start(out=beta_o_a[:], in_=beta_ih[TCOLS:G].partition_broadcast(P))
        nc.sync.dma_start(out=beta_o_b[:], in_=beta_hh[TCOLS:G].partition_broadcast(P))
        nc.sync.dma_start(out=c_prev_all[:], in_=c_rows_in)
        load_rows(1, 0, GRP)
        nc.sync.dma_start(out=gamma_c_all[:], in_=gamma_c.partition_broadcast(P))
        nc.sync.dma_start(out=beta_c_all[:], in_=beta_c.partition_broadcast(P))

        nc.vector.memset(beta_rows[:], 0.0)
        nc.vector.tensor_tensor(out=beta_rows[0:G // P, :], in0=beta_a[:], in1=beta_b[:], op=ALU.add)
        beta_t = ps_tr.tile([P, 4, P], F32, name="tr")
        nc.tensor.transpose(beta_t[:, 0, :], beta_rows[:], ident[:])
        nc.vector.tensor_copy(out=beta_col[:], in_=beta_t[:, 0, 0:G // P])
        nc.gpsimd.tensor_tensor(out=beta_o[:], in0=beta_o_a[:], in1=beta_o_b[:], op=ALU.add)

        def regroup_weights(chunk):
            grouped = wprep.tile([P, CHUNK, 4], BF16, name="grouped", align_bytes=64)
            dst = grouped[:].rearrange("p (c i) j -> p c j i", i=4)
            src = w_raw[chunk // 2][:, :, (chunk % 2) * CHUNK:(chunk % 2 + 1) * CHUNK].rearrange(
                "p j (c i) -> p c j i", i=4
            )
            if chunk % 2 == 0:
                nc.vector.tensor_copy(out=dst, in_=src)
            else:
                nc.scalar.copy(out=dst, in_=src)
            live[("grouped", chunk)] = grouped

        def quantise_weights(chunk):
            m = chunk // 4
            cols = slice((chunk % 4) * CHUNK, (chunk % 4 + 1) * CHUNK)
            nc.vector.quantize_mx(
                out=w_words[m][:, cols].bitcast(FP8X4),
                scales=w_scales[m][:, cols],
                in_=live[("grouped", chunk)][:].rearrange("p c j -> p (c j)"),
            )

        def transpose_x(t):
            if not 0 <= t < NT:
                return
            pairs_t = ps_tr.tile([P, 4, P], F32, name="tr")
            for operand, what in enumerate(("x", "h")):
                pairs = live[(what, t // GRP)][:, t % GRP, :].bitcast(F32)
                for u in range(2):
                    nc.tensor.transpose(pairs_t[:, 2 * operand + u, :], pairs[:, u * P:(u + 1) * P], ident[:])
            live[("pairs_t", t)] = pairs_t

        def copy_x(t):
            if not 0 <= t < NT:
                return
            grouped = xq.tile([P, 2, P, 2], F32, name="x_grouped", bufs=2, align_bytes=64)
            nc.scalar.copy(out=grouped[:], in_=live[("pairs_t", t)][:].rearrange("p (o u) r -> p o r u", u=2))
            live[("x_grouped", t)] = grouped

        def quantise_x(t):
            if not 0 <= t < NT:
                return
            words = xq.tile([P, 2 * P], U32, name="x_words", align_bytes=64)
            scales = xq.tile([P, 2 * P], U8, name="x_scales", align_bytes=64)
            nc.vector.quantize_mx(
                out=words[:].bitcast(FP8X4),
                scales=scales[:],
                in_=live[("x_grouped", t)][:].rearrange("p o r u -> p (o r u)").bitcast(BF16),
            )
            live[("x_words", t)] = words
            live[("x_scales", t)] = scales

        def mx_pass(out, unit, cols, start, stop):
            t, m = unit // 2, unit % 2
            nc.tensor.matmul_mx(
                out=out,
                lhsT=live[("x_words", t)][:, m * P:(m + 1) * P].bitcast(FP8X4),
                lhsT_scale=live[("x_scales", t)][:, m * P:(m + 1) * P],
                rhs=w_words[m][:, cols].bitcast(FP8X4),
                rhs_scale=w_scales[m][:, cols],
                start=start,
                stop=stop,
            )

        def row_sums(unit):
            if not 0 <= unit < UNITS:
                return
            sums = ps_sum.tile([P, P], F32, name="sums")
            for j in range(G // P):
                mx_pass(sums[:], unit, slice(j * P, (j + 1) * P), j == 0, j == G // P - 1)
            live[("sums", unit)] = sums

        def negative_mean(unit):
            if not 0 <= unit < UNITS:
                return
            neg_mean = small.tile([P, 1], F32, name="neg_mean")
            nc.scalar.activation(
                out=unread_narrow[:], in_=live[("sums", unit)][:], func=ACT.Identity, scale=-1.0 / G,
                accum_out=neg_mean[:],
            )
            live[("neg_mean", unit)] = neg_mean

        def product_bank(unit, k):
            if not 0 <= unit < UNITS:
                return
            bank = ps_prod.tile([P, BANK], F32, name="bank")
            mx_pass(bank[:], unit, slice(k * BANK, (k + 1) * BANK), True, True)
            live[("bank", unit, k)] = bank

        def square_sum(unit, k):
            if k == 0:
                live[("squares", unit)] = small.tile([P, 4], F32, name="squares")
                live[("s", unit)] = work.tile([P, G], F32, name="s%d" % (unit % 2), bufs=3)
            nc.scalar.activation(
                out=live[("s", unit)][:, k * BANK:(k + 1) * BANK], in_=live[("bank", unit, k)][:], func=ACT.Square,
                bias=live[("neg_mean", unit)][:], scale=1.0, accum_out=live[("squares", unit)][:, k:k + 1],
            )

        def centre_and_gain(unit, k):
            cols = slice(k * BANK, (k + 1) * BANK)
            nc.vector.scalar_tensor_tensor(
                out=live[("s", unit)][:, cols], in0=live[("bank", unit, k)][:], scalar=live[("neg_mean", unit)][:],
                in1=gamma[unit % 2][:, cols], op0=ALU.add, op1=ALU.mult,
            )

        def inverse_std(sum_of_squares, count, name):
            var = small.tile([P, 1], F32, name="var_" + name)
            nc.gpsimd.tensor_scalar(
                out=var[:], in0=sum_of_squares[:], scalar1=1.0 / count, scalar2=EPS, op0=ALU.mult, op1=ALU.add
            )
            r = small.tile([P, 1], F32, name="r_" + name)
            nc.gpsimd.tensor_tensor(out=r[:], in0=var[:], in1=minus_half[:], op=ALU.pow)
            return r

        def unit_inverse_std(unit):
            total = small.tile([P, 1], F32, name="total")
            nc.scalar.activation(
                out=unread_narrow[:, 0:4], in_=live[("squares", unit)][:], func=ACT.Identity, accum_out=total[:]
            )
            live[("r", unit)] = inverse_std(total, G, "gates")

        def scale_rows(t, m):
            if not 0 <= t < NT:
                return
            s = live[("s", 2 * t + m)][:, 0:TCOLS]
            nc.vector.tensor_scalar(out=s, in0=s, scalar1=live[("r", 2 * t + m)][:], scalar2=None, op0=ALU.mult)

        def o_gate_sum(t):
            if not 0 <= t < NT:
                return
            o_sum = work.tile([P, H], F32, name="o_sum")
            nc.vector.scalar_tensor_tensor(
                out=o_sum[:], in0=live[("s", 2 * t)][:, TCOLS:G], scalar=live[("r", 2 * t)][:], in1=beta_o[:],
                op0=ALU.mult, op1=ALU.add,
            )
            nc.vector.scalar_tensor_tensor(
                out=o_sum[:], in0=live[("s", 2 * t + 1)][:, TCOLS:G], scalar=live[("r", 2 * t + 1)][:], in1=o_sum[:],
                op0=ALU.mult, op1=ALU.add,
            )
            live[("o_sum", t)] = o_sum

        def o_gate(t):
            if not 0 <= t < NT:
                return
            o = work.tile([P, H], F32, name="o", bufs=3)
            nc.scalar.activation(out=o[:], in_=live[("o_sum", t)][:], func=ACT.Sigmoid)
            live[("o", t)] = o

        def add_transposed(terms):
            summed = ps_tr.tile([P, 4, P], F32, name="tr")
            for q in range(4):
                for second, term in enumerate(terms):
                    nc.tensor.matmul(
                        out=summed[:, q, :], lhsT=term[:, q * P:(q + 1) * P], rhs=ident[:], is_transpose=True,
                        start=(second == 0), stop=(second == 1),
                    )
            return summed

        def gate_sum_t(t, gate):
            if not 0 <= t < NT:
                return
            cols = slice(FIRST_COLUMN[gate], FIRST_COLUMN[gate] + H)
            live[("gate_sum_t", t, gate)] = add_transposed([live[("s", 2 * t + m)][:, cols] for m in range(2)])

        def gate_t(t, gate):
            if not 0 <= t < NT:
                return
            values = work.tile([P, 4, P], F32, name="gate_" + gate)
            for q in range(4):
                block = FIRST_COLUMN[gate] // P + q
                nc.scalar.activation(
                    out=values[:, q, :], in_=live[("gate_sum_t", t, gate)][:, q, :],
                    func=(ACT.Tanh if gate == "g" else ACT.Sigmoid), bias=beta_col[:, block:block + 1], scale=1.0,
                )
            live[("gate_t", t, gate)] = values

        def c_prev_t(t):
            if not 0 <= t < NT:
                return
            half_used = ps_tr.tile([P, 4, P], F32, name="tr")
            as_bf16 = flat(half_used).bitcast(BF16)
            for q in range(4):
                nc.tensor.transpose(as_bf16[:, q * P:(q + 1) * P], c_prev_all[:, t, q * P:(q + 1) * P], ident_bf[:])
            live[("c_prev_t", t)] = as_bf16[:, 0:H]

        def forget_t(t):
            if not 0 <= t < NT:
                return
            kept = work.tile([P, 4, P], F32, name="kept")
            nc.vector.tensor_tensor(
                out=flat(kept), in0=flat(live[("gate_t", t, "f")]), in1=live[("c_prev_t", t)], op=ALU.mult
            )
            live[("kept", t)] = kept

        def input_t(t):
            if not 0 <= t < NT:
                return
            new = work.tile([P, 4, P], F32, name="new")
            nc.vector.tensor_tensor(
                out=flat(new), in0=flat(live[("gate_t", t, "i")]), in1=flat(live[("gate_t", t, "g")]), op=ALU.mult
            )
            live[("new", t)] = new

        def c_rows(t):
            if not 0 <= t < NT:
                return
            live[("c_psum", t)] = add_transposed([flat(live[("kept", t)]), flat(live[("new", t)])])

        def c_out(t):
            if not 0 <= t < NT:
                return
            c = work.tile([P, H], F32, name="c", bufs=3)
            c_sum = small.tile([P, 1], F32, name="c_sum")
            nc.scalar.activation(out=c[:], in_=flat(live[("c_psum", t)]), func=ACT.Identity, accum_out=c_sum[:])
            nc.sync.dma_start(out=c_rows_out[:, t, :], in_=c[:])
            c_neg_mean = small.tile([P, 1], F32, name="c_neg_mean")
            nc.scalar.mul(out=c_neg_mean[:], in_=c_sum[:], mul=-1.0 / H)
            live[("c", t)] = c
            live[("c_neg_mean", t)] = c_neg_mean

        def c_inverse_std(t):
            if not 0 <= t < NT:
                return
            c_squares = small.tile([P, 1], F32, name="c_squares")
            nc.scalar.activation(
                out=unread_wide[:], in_=live[("c", t)][:], func=ACT.Square, bias=live[("c_neg_mean", t)][:], scale=1.0,
                accum_out=c_squares[:],
            )
            live[("c_r", t)] = inverse_std(c_squares, H, "c")

        def c_norm(t):
            if not 0 <= t < NT:
                return
            normed = work.tile([P, H], F32, name="normed")
            nc.vector.scalar_tensor_tensor(
                out=normed[:], in0=live[("c", t)][:], scalar=live[("c_neg_mean", t)][:], in1=gamma_c_all[:],
                op0=ALU.add, op1=ALU.mult,
            )
            nc.vector.scalar_tensor_tensor(
                out=normed[:], in0=normed[:], scalar=live[("c_r", t)][:], in1=beta_c_all[:], op0=ALU.mult, op1=ALU.add
            )
            live[("normed", t)] = normed

        def c_tanh(t):
            if not 0 <= t < NT:
                return
            squashed = work.tile([P, H], F32, name="squashed")
            nc.scalar.activation(out=squashed[:], in_=live[("normed", t)][:], func=ACT.Tanh)
            live[("squashed", t)] = squashed

        def h_out(t):
            if not 0 <= t < NT:
                return
            h = work.tile([P, H], F32, name="h", bufs=3)
            nc.vector.tensor_tensor(out=h[:], in0=live[("o", t)][:], in1=live[("squashed", t)][:], op=ALU.mult)
            nc.sync.dma_start(out=h_rows_out[:, t, :], in_=h[:])

        for t in range(AHEAD):
            transpose_x(t)
            copy_x(t)
        for t in range(AHEAD):
            quantise_x(t)
        for chunk in range(W_CHUNKS):
            regroup_weights(chunk)
            if chunk >= 2:
                quantise_weights(chunk - 2)
        quantise_weights(W_CHUNKS - 2)
        quantise_weights(W_CHUNKS - 1)
        product_bank(0, 0)
        row_sums(0)
        product_bank(0, 1)
        product_bank(0, 2)
        negative_mean(0)

        for unit in range(UNITS + DRAIN):
            t, m = unit // 2, unit % 2
            busy = unit < UNITS
            if m == 0:
                if t % GRP == 0 and 0 < t < NT - GRP:
                    load_rows(t // GRP + 1, 0, GRP)
                c_prev_t(t - 2)
                transpose_x(t + AHEAD)
                c_rows(t - 3)
            else:
                for gate in ("f", "i", "g"):
                    gate_sum_t(t - 1, gate)
            product_bank(unit, 3)
            for k in range(4):
                if busy:
                    square_sum(unit, k)
                    centre_and_gain(unit, k)
                if (m, k) == (0, 0):
                    o_gate(t - 2)
                    forget_t(t - 2)
                elif (m, k) == (0, 1):
                    copy_x(t + AHEAD)
                    scale_rows(t - 1, 1)
                elif (m, k) == (0, 2):
                    c_out(t - 3)
                    o_gate_sum(t - 1)
                elif (m, k) == (0, 3):
                    c_inverse_std(t - 3)
                    input_t(t - 2)
                elif (m, k) == (1, 0):
                    c_tanh(t - 4)
                    scale_rows(t, 0)
                elif (m, k) == (1, 1):
                    gate_t(t - 1, "f")
                    c_norm(t - 3)
                elif (m, k) == (1, 2):
                    gate_t(t - 1, "i")
                    h_out(t - 4)
                else:
                    gate_t(t - 1, "g")
                    quantise_x(t + AHEAD)
                if k < 3:
                    product_bank(unit + 1, k)
                if k == 0:
                    row_sums(unit + 1)
            negative_mean(unit + 1)
            if busy:
                unit_inverse_std(unit)
